import numpy as np
import ml_dtypes


def mxq(x, axis, fmt="e4m3"):
    dtype, down = {"e4m3": (ml_dtypes.float8_e4m3fn, 7), "e5m2": (ml_dtypes.float8_e5m2, 14)}[fmt]
    v = np.moveaxis(np.asarray(x, np.float32).astype(ml_dtypes.bfloat16).astype(np.float64), axis, -1)
    blocks = v.reshape(v.shape[:-1] + (-1, 32))
    amax = np.abs(blocks).max(-1, keepdims=True)
    byte = np.maximum(np.where(amax > 0, np.frexp(amax)[1] - 1 + 127, 0) - down, 1)
    scale = np.exp2(byte - 127.0)
    codes = (blocks / scale).astype(np.float32).astype(dtype).astype(np.float64)
    return np.moveaxis((codes * scale).reshape(v.shape), -1, axis)


WIDE = False


def mx_kscale(k):
    if not WIDE:
        return np.ones(k)
    levels = np.array([30, -30])
    if k % 512:
        return np.exp2(np.random.permutation(np.resize(levels, k // 32))).repeat(32)
    a = np.empty((k // 512, 16))
    for p in range(k // 512):
        a[p, :8] = np.random.permutation(np.resize(levels, 8))
        for g in range(8):
            far = levels[np.abs(levels - a[p, g]) >= 10]
            a[p, g + 8] = far[np.random.randint(len(far))]
    return np.exp2(a.ravel()).repeat(32)


BF16 = ml_dtypes.bfloat16


def bf(x):
    return np.asarray(x, np.float32).astype(BF16)


def f64(x):
    return np.asarray(x).astype(np.float64)


B, I, H, AH, AI, G = 512, 1024, 1024, 128, 128, 4
EPS = 1e-5


def sigmoid(v):
    return 1.0 / (1.0 + np.exp(-v))


def ln(v, w, b):
    mu = v.mean(-1, keepdims=True)
    var = ((v - mu) ** 2).mean(-1, keepdims=True)
    return (v - mu) / np.sqrt(var + EPS) * w + b


def setup_inputs():
    n = np.random.standard_normal
    s, t = mx_kscale(I), mx_kscale(H)
    return {
        "x": bf(n((B, I)) * s),
        "hx": bf(n((B, H)) * t),
        "cx": bf(n((B, H))),
        "zw": bf(1.0 + 0.5 * n((B, 2 * G, AI))),
        "zb": bf(0.7 * n((B, 2 * G, AI))),
        "w_ih": bf(n((G * H, I)) / np.sqrt(I) / s),
        "w_hh": bf(n((G * H, H)) / np.sqrt(H) / t),
        "b_ih": bf(0.2 * n(G * H)),
        "b_hh": bf(0.2 * n(G * H)),
        "norm_alpha_w": bf(n((2 * G, H, AI)) / np.sqrt(AI)),
        "bias_beta_w": bf(0.7 * n((2 * G, H, AI)) / np.sqrt(AI)),
        "ln_i_w": bf(1.0 + 0.1 * n(G * H)),
        "ln_i_b": bf(0.2 * n(G * H)),
        "ln_h_w": bf(1.0 + 0.1 * n(G * H)),
        "ln_h_b": bf(0.2 * n(G * H)),
        "ln_c_w": bf(1.0 + 0.1 * n(H)),
        "ln_c_b": bf(0.2 * n(H)),
    }


def reference(x, hx, cx, zw, zb, w_ih, w_hh, b_ih, b_hh, norm_alpha_w, bias_beta_w, ln_i_w, ln_i_b, ln_h_w, ln_h_b, ln_c_w, ln_c_b):
    alpha = (f64(zw).transpose(1, 0, 2) @ f64(norm_alpha_w).transpose(0, 2, 1)).transpose(1, 0, 2)
    beta = (f64(zb).transpose(1, 0, 2) @ f64(bias_beta_w).transpose(0, 2, 1)).transpose(1, 0, 2)
    xh = (mxq(f64(x), 1, "e5m2") @ mxq(f64(w_ih), 1, "e5m2").T).reshape(-1, G, H)
    hh = (mxq(f64(hx), 1, "e5m2") @ mxq(f64(w_hh), 1, "e5m2").T).reshape(-1, G, H)
    in_g = (xh * alpha[:, :G] + f64(b_ih).reshape(G, H) + beta[:, :G]).reshape(-1, G * H)
    hid_g = (hh * alpha[:, G:] + f64(b_hh).reshape(G, H) + beta[:, G:]).reshape(-1, G * H)
    gates = ln(in_g, f64(ln_i_w), f64(ln_i_b)) + ln(hid_g, f64(ln_h_w), f64(ln_h_b))
    i, j, f, o = np.split(gates, G, axis=1)
    cy = ln(sigmoid(f) * f64(cx) + sigmoid(i) * np.tanh(j), f64(ln_c_w), f64(ln_c_b))
    hy = sigmoid(o) * np.tanh(cy)
    return hy, cy

@@ -1,0 +1,277 @@
+from contextlib import ExitStack
+
+import concourse.mybir as mybir
+from concourse.masks import make_identity
+
+F32 = mybir.dt.float32
+BF16 = mybir.dt.bfloat16
+U32 = mybir.dt.uint32
+U8 = mybir.dt.uint8
+FP8X4 = mybir.dt.float8_e5m2_x4
+ALU = mybir.AluOpType
+ACT = mybir.ActivationFunctionType
+AX = mybir.AxisListType
+
+P = 128
+BATCH = 512
+K = 1024
+H = 1024
+GATES = 4096
+NT = 512
+MT = BATCH // P
+PASSES = 2
+CHUNKS = GATES // NT
+EPS = 1e-5
+
+FLOPS = 2 * 2 * BATCH * GATES * K + 16 * 2 * BATCH * H * 128
+
+
+def tile_adaptivelstmcell_pb_kernel(
+    tc, x, hx, cx, zw, zb, w_ih, w_hh, b_ih, b_hh, norm_alpha_w, bias_beta_w,
+    ln_i_w, ln_i_b, ln_h_w, ln_h_b, ln_c_w, ln_c_b, out_0, out_1,
+):
+    nc = tc.nc
+    with ExitStack() as ctx:
+        keep = ctx.enter_context(tc.tile_pool(name="keep", bufs=1))
+        rawp = ctx.enter_context(tc.tile_pool(name="rawp", bufs=2))
+        grp = ctx.enter_context(tc.tile_pool(name="grp", bufs=2))
+        wq = ctx.enter_context(tc.tile_pool(name="wq", bufs=2))
+        abp = ctx.enter_context(tc.tile_pool(name="abp", bufs=2))
+        work = ctx.enter_context(tc.tile_pool(name="work", bufs=3))
+        cst = ctx.enter_context(tc.tile_pool(name="cst", bufs=2))
+        pst = ctx.enter_context(tc.psum_pool(name="pst", bufs=2))
+        psx = ctx.enter_context(tc.psum_pool(name="psx", bufs=2))
+        psa = ctx.enter_context(tc.psum_pool(name="psa", bufs=2))
+        psb = ctx.enter_context(tc.psum_pool(name="psb", bufs=2))
+
+        ident_f = keep.tile([P, P], F32, name="ident_f")
+        make_identity(nc, ident_f[:])
+        ident_b = keep.tile([P, P], BF16, name="ident_b")
+        make_identity(nc, ident_b[:])
+        ones_f = keep.tile([P, P], F32, name="ones_f")
+        nc.vector.memset(ones_f[:], 1.0)
+        neg_half = keep.tile([P, MT], F32, name="neg_half")
+        nc.vector.memset(neg_half[:], -0.5)
+
+        xcodes = [keep.tile([P, PASSES, BATCH], U32, name="xcodes%d" % q, align_bytes=64) for q in range(2)]
+        xscales = [keep.tile([P, PASSES, BATCH], U8, name="xscales%d" % q, align_bytes=64) for q in range(2)]
+        zT = [keep.tile([P, 8, BATCH], BF16, name="zT%d" % i) for i in range(2)]
+        gbuf = [[keep.tile([P, GATES], F32, name="g%d_%d" % (q, m)) for m in range(MT)] for q in range(2)]
+        sum_u = keep.tile([P, 2, MT, CHUNKS], F32, name="sum_u")
+        sum_sq = keep.tile([P, 2, MT, CHUNKS], F32, name="sum_sq")
+        csum = keep.tile([P, MT], F32, name="csum")
+        csq = keep.tile([P, MT], F32, name="csq")
+        bsum = keep.tile([P, 2], F32, name="bsum")
+
+        def copy_on(eng, out, in_):
+            if eng == 0:
+                nc.scalar.copy(out=out, in_=in_)
+            else:
+                nc.vector.tensor_copy(out=out, in_=in_)
+
+        def transpose_quantize(raw, codes, scales, engines):
+            words = raw[:].bitcast(F32)
+            for g in range(PASSES):
+                grouped = grp.tile([P, 4 * NT], BF16, name="grouped", tag="grouped", align_bytes=64)
+                gw = grouped[:].bitcast(F32).rearrange("p (c u) -> p c u", u=2)
+                for half in range(2):
+                    pt = pst.tile([P, 2, 256], F32, name="pt", tag="t")
+                    for bb in range(2):
+                        for u in range(2):
+                            nc.tensor.transpose(
+                                pt[:, u, P * bb:P * (bb + 1)],
+                                words[:, 2 * half + bb, 256 * g + u:256 * (g + 1):2],
+                                ident_f[:],
+                            )
+                    copy_on(engines[2 * g + half], gw[:, 256 * half:256 * (half + 1), :],
+                            pt[:].rearrange("p u c -> p c u"))
+                nc.vector.quantize_mx(out=codes[:, g, :].bitcast(FP8X4), scales=scales[:, g, :], in_=grouped[:])
+
+        def load_rows(src2d):
+            raw = rawp.tile([P, 4, K], BF16, name="raw", tag="raw")
+            nc.sync.dma_start(out=raw[:], in_=src2d.rearrange("(b r) k -> r b k", r=P))
+            return raw
+
+        def prep_x(q):
+            raw = load_rows((x, hx)[q])
+            transpose_quantize(raw, xcodes[q], xscales[q], (0, 1, 0, 1))
+
+        def prep_z(i):
+            raw = load_rows((zw, zb)[i].rearrange("b s a -> b (s a)"))
+            for s in range(8):
+                pt = pst.tile([P, BATCH], BF16, name="ptz", tag="t")
+                for m in range(MT):
+                    nc.tensor.transpose(pt[:, P * m:P * (m + 1)], raw[:, m, P * s:P * (s + 1)], ident_b[:])
+                copy_on(s % 2, zT[i][:, s, :], pt[:])
+
+        def prep_chunk(c):
+            q, j = divmod(c, CHUNKS)
+            s = 4 * q + j // 2
+            h0 = NT * (j % 2)
+            n0 = NT * j
+            raw = load_rows((w_ih, w_hh)[q][n0:n0 + NT, :])
+            small = []
+            for i, wsrc in enumerate((norm_alpha_w, bias_beta_w)):
+                sraw = abp.tile([P, 4, P], BF16, name="sraw%d" % i, tag="sraw%d" % i)
+                nc.sync.dma_start(out=sraw[:], in_=wsrc[s, h0:h0 + NT, :].rearrange("(b r) a -> r b a", r=P))
+                small.append(sraw)
+            bias = abp.tile([P, NT], BF16, name="bias", tag="bias")
+            nc.sync.dma_start(out=bias[:], in_=(b_ih, b_hh)[q][n0:n0 + NT].partition_broadcast(P))
+            codes = wq.tile([P, PASSES, NT], U32, name="wcodes", tag="wcodes", align_bytes=64)
+            scales = wq.tile([P, PASSES, NT], U8, name="wscales", tag="wscales", align_bytes=64)
+            transpose_quantize(raw, codes, scales, (0, 1, 0, 1) if q == 0 else (0, 0, 0, 0))
+            abT = []
+            for i in range(2):
+                pt = pst.tile([P, NT], BF16, name="pta", tag="t")
+                for b in range(4):
+                    nc.tensor.transpose(pt[:, P * b:P * (b + 1)], small[i][:, b, :], ident_b[:])
+                wT = abp.tile([P, NT], BF16, name="wT%d" % i, tag="wT%d" % i)
+                copy_on(1 - q, wT[:], pt[:])
+                abT.append(wT)
+            return codes, scales, abT, bias
+
+        def compute_chunk(c, prepared):
+            codes, scales, abT, bias = prepared
+            q, j = divmod(c, CHUNKS)
+            s = 4 * q + j // 2
+            n0 = NT * j
+            for m in range(MT):
+                rows = slice(P * m, P * (m + 1))
+                xh = psx.tile([P, NT], F32, name="xh", tag="xh")
+                for g in range(PASSES):
+                    nc.tensor.matmul_mx(
+                        out=xh[:],
+                        lhsT=xcodes[q][:, g, rows].bitcast(FP8X4),
+                        lhsT_scale=xscales[q][:, g, rows],
+                        rhs=codes[:, g, :].bitcast(FP8X4),
+                        rhs_scale=scales[:, g, :],
+                        start=(g == 0),
+                        stop=(g == PASSES - 1),
+                    )
+                alpha = psa.tile([P, NT], F32, name="alpha", tag="alpha")
+                nc.tensor.matmul(out=alpha[:], lhsT=zT[0][:, s, rows], rhs=abT[0][:], start=True, stop=True)
+                beta = psb.tile([P, NT], F32, name="beta", tag="beta")
+                nc.tensor.matmul(out=beta[:], lhsT=zT[1][:, s, rows], rhs=abT[1][:], start=True, stop=True)
+                al = work.tile([P, NT], F32, name="al", tag="al")
+                nc.scalar.copy(out=al[:], in_=alpha[:])
+                dst = gbuf[q][m][:, n0:n0 + NT]
+                nc.vector.tensor_tensor(out=dst, in0=xh[:], in1=al[:], op=ALU.mult)
+                nc.vector.scalar_tensor_tensor(out=dst, in0=dst, scalar=1.0, in1=beta[:], op0=ALU.mult,
+                                               op1=ALU.add, accum_out=sum_u[:, q, m, j:j + 1])
+                nc.gpsimd.tensor_tensor(out=dst, in0=dst, in1=bias[:], op=ALU.add)
+                junk = work.tile([P, NT], BF16, name="junk", tag="junk")
+                nc.scalar.activation(out=junk[:], in_=dst, func=ACT.Square, accum_out=sum_sq[:, q, m, j:j + 1])
+
+        def gate_stats(q, label):
+            s1 = keep.tile([P, MT], F32, name="s1" + label)
+            s2 = keep.tile([P, MT], F32, name="s2" + label)
+            nc.vector.tensor_reduce(out=s1[:], in_=sum_u[:, q, :, :], axis=AX.X, op=ALU.add)
+            nc.vector.tensor_reduce(out=s2[:], in_=sum_sq[:, q, :, :], axis=AX.X, op=ALU.add)
+            return finish_stats(s1, s2, bsum[:, q:q + 1], GATES, label)
+
+        def finish_stats(s1, s2, extra, count, label):
+            mean = keep.tile([P, MT], F32, name="mean" + label)
+            rstd = keep.tile([P, MT], F32, name="rstd" + label)
+            nc.vector.tensor_scalar(out=mean[:], in0=s1[:], scalar1=extra, scalar2=1.0 / count,
+                                    op0=ALU.add, op1=ALU.mult)
+            nc.vector.tensor_tensor(out=s1[:], in0=mean[:], in1=mean[:], op=ALU.mult)
+            nc.vector.scalar_tensor_tensor(out=s2[:], in0=s2[:], scalar=1.0 / count, in1=s1[:],
+                                           op0=ALU.mult, op1=ALU.subtract)
+            nc.vector.tensor_scalar(out=s2[:], in0=s2[:], scalar1=0.0, scalar2=EPS, op0=ALU.max, op1=ALU.add)
+            nc.gpsimd.tensor_tensor(out=rstd[:], in0=s2[:], in1=neg_half[:], op=ALU.pow)
+            return mean, rstd
+
+        def bcast(vec, lo, tag, bufs):
+            t = cst.tile([P, H], BF16, name=tag, tag=tag, bufs=bufs)
+            nc.sync.dma_start(out=t[:], in_=vec[lo:lo + H].partition_broadcast(P))
+            return t
+
+        bsm = keep.tile([P, 2, 32], BF16, name="bsm")
+        nc.sync.dma_start(out=bsm[:, 0, :], in_=b_ih.rearrange("(p c) -> p c", c=32))
+        nc.sync.dma_start(out=bsm[:, 1, :], in_=b_hh.rearrange("(p c) -> p c", c=32))
+
+        prep_x(0)
+        nxt = prep_chunk(0)
+        prep_z(0)
+        prep_z(1)
+
+        bpart = keep.tile([P, 2], F32, name="bpart")
+        nc.vector.tensor_reduce(out=bpart[:], in_=bsm[:], axis=AX.X, op=ALU.add)
+        pb = pst.tile([P, 2], F32, name="pb", tag="t")
+        nc.tensor.matmul(out=pb[:], lhsT=ones_f[:], rhs=bpart[:], start=True, stop=True)
+        nc.vector.tensor_copy(out=bsum[:], in_=pb[:])
+
+        stats = [None, None]
+        post_c = {}
+
+        def post_in(gi, ms):
+            cols = slice(H * gi, H * (gi + 1))
+            if gi not in post_c:
+                wi = bcast(ln_i_w, H * gi, "lnw", 2)
+                lbi = bcast(ln_i_b, H * gi, "lbi", 1)
+                lbh = bcast(ln_h_b, H * gi, "lbh", 1)
+                lb = cst.tile([P, H], F32, name="lb", tag="lb")
+                nc.gpsimd.tensor_tensor(out=lb[:], in0=lbi[:], in1=lbh[:], op=ALU.add)
+                post_c[gi] = (wi, lb)
+            wi, lb = post_c[gi]
+            mean, rstd = stats[0]
+            for m in ms:
+                t = gbuf[0][m][:, cols]
+                nc.vector.scalar_tensor_tensor(out=t, in0=t, scalar=mean[:, m:m + 1], in1=wi[:],
+                                               op0=ALU.subtract, op1=ALU.mult)
+                nc.vector.scalar_tensor_tensor(out=t, in0=t, scalar=rstd[:, m:m + 1], in1=lb[:],
+                                               op0=ALU.mult, op1=ALU.add)
+
+        for c in range(2 * CHUNKS):
+            cur = nxt
+            if c == 5:
+                prep_x(1)
+            if c + 1 < 2 * CHUNKS:
+                nxt = prep_chunk(c + 1)
+            compute_chunk(c, cur)
+            if c == CHUNKS - 1:
+                stats[0] = gate_stats(0, "i")
+            if c >= CHUNKS:
+                d = c - CHUNKS
+                post_in(d // 2, (0, 1) if d % 2 == 0 else (2, 3))
+
+        stats[1] = gate_stats(1, "h")
+        cxt = load_rows(cx)
+        wc = bcast(ln_c_w, 0, "wc", 1)
+        bc = bcast(ln_c_b, 0, "bc", 1)
+        mean_h, rstd_h = stats[1]
+        funcs = (ACT.Sigmoid, ACT.Tanh, ACT.Sigmoid, ACT.Sigmoid)
+        for gi in (2, 0, 1, 3):
+            cols = slice(H * gi, H * (gi + 1))
+            wh = bcast(ln_h_w, H * gi, "lnw", 2)
+            for m in range(MT):
+                t = gbuf[1][m][:, cols]
+                o = gbuf[0][m][:, cols]
+                nc.vector.scalar_tensor_tensor(out=t, in0=t, scalar=mean_h[:, m:m + 1], in1=wh[:],
+                                               op0=ALU.subtract, op1=ALU.mult)
+                nc.vector.scalar_tensor_tensor(out=o, in0=t, scalar=rstd_h[:, m:m + 1], in1=o,
+                                               op0=ALU.mult, op1=ALU.add)
+                nc.scalar.activation(out=o, in_=o, func=funcs[gi])
+
+        for m in range(MT):
+            gm = gbuf[0][m]
+            sc = gbuf[1][m]
+            nc.vector.tensor_tensor(out=sc[:, 0:H], in0=gm[:, 2 * H:3 * H], in1=cxt[:, m, :], op=ALU.mult)
+            nc.vector.tensor_tensor(out=sc[:, H:2 * H], in0=gm[:, 0:H], in1=gm[:, H:2 * H], op=ALU.mult)
+            nc.vector.scalar_tensor_tensor(out=sc[:, 2 * H:3 * H], in0=sc[:, 0:H], scalar=1.0, in1=sc[:, H:2 * H],
+                                           op0=ALU.mult, op1=ALU.add, accum_out=csum[:, m:m + 1])
+            nc.scalar.activation(out=sc[:, 3 * H:4 * H], in_=sc[:, 2 * H:3 * H], func=ACT.Square,
+                                 accum_out=csq[:, m:m + 1])
+        mean_c, rstd_c = finish_stats(csum, csq, 0.0, H, "c")
+        for m in range(MT):
+            gm = gbuf[0][m]
+            sc = gbuf[1][m]
+            rows = slice(P * m, P * (m + 1))
+            nc.vector.scalar_tensor_tensor(out=sc[:, 0:H], in0=sc[:, 2 * H:3 * H], scalar=mean_c[:, m:m + 1],
+                                           in1=wc[:], op0=ALU.subtract, op1=ALU.mult)
+            nc.vector.scalar_tensor_tensor(out=sc[:, H:2 * H], in0=sc[:, 0:H], scalar=rstd_c[:, m:m + 1],
+                                           in1=bc[:], op0=ALU.mult, op1=ALU.add)
+            nc.sync.dma_start(out=out_1[rows, :], in_=sc[:, H:2 * H])
+            nc.scalar.activation(out=sc[:, 3 * H:4 * H], in_=sc[:, H:2 * H], func=ACT.Tanh)
+            nc.vector.tensor_tensor(out=sc[:, 0:H], in0=sc[:, 3 * H:4 * H], in1=gm[:, 3 * H:4 * H], op=ALU.mult)
+            nc.sync.dma_start(out=out_0[rows, :], in_=sc[:, 0:H])

@@ -23,6 +23,13 @@ PASSES = 2
 CHUNKS = GATES // NT
 EPS = 1e-5
 
+W_COPY = ((0, 1), (0, 1))
+AB_COPY = (0, 0)
+Z_COPY = (0, 1)
+N_COPY = (0, 0)
+NORM_IN = (2, 2, 1, 1)
+TAIL_NORM = (1, 1, 0, 2)
+
 FLOPS = 2 * 2 * BATCH * GATES * K + 16 * 2 * BATCH * H * 128
 
 
@@ -33,12 +40,11 @@ def tile_adaptivelstmcell_pb_kernel(
     nc = tc.nc
     with ExitStack() as ctx:
         keep = ctx.enter_context(tc.tile_pool(name="keep", bufs=1))
-        rawp = ctx.enter_context(tc.tile_pool(name="rawp", bufs=2))
+        rawp = ctx.enter_context(tc.tile_pool(name="rawp", bufs=3))
         grp = ctx.enter_context(tc.tile_pool(name="grp", bufs=2))
         wq = ctx.enter_context(tc.tile_pool(name="wq", bufs=2))
         abp = ctx.enter_context(tc.tile_pool(name="abp", bufs=2))
         work = ctx.enter_context(tc.tile_pool(name="work", bufs=3))
-        cst = ctx.enter_context(tc.tile_pool(name="cst", bufs=2))
         pst = ctx.enter_context(tc.psum_pool(name="pst", bufs=2))
         psx = ctx.enter_context(tc.psum_pool(name="psx", bufs=2))
         psa = ctx.enter_context(tc.psum_pool(name="psa", bufs=2))
@@ -56,11 +62,13 @@ def tile_adaptivelstmcell_pb_kernel(
         xcodes = [keep.tile([P, PASSES, BATCH], U32, name="xcodes%d" % q, align_bytes=64) for q in range(2)]
         xscales = [keep.tile([P, PASSES, BATCH], U8, name="xscales%d" % q, align_bytes=64) for q in range(2)]
         zT = [keep.tile([P, 8, BATCH], BF16, name="zT%d" % i) for i in range(2)]
-        gbuf = [[keep.tile([P, GATES], F32, name="g%d_%d" % (q, m)) for m in range(MT)] for q in range(2)]
+        gbuf = [[keep.tile([P, MT, NT], F32, name="g%d_%d" % (q, d)) for d in range(CHUNKS)] for q in range(2)]
+        spare = keep.tile([P, MT, NT], F32, name="spare")
+        turned = [spare] + gbuf[0][0:CHUNKS - 1]
         sum_u = keep.tile([P, 2, MT, CHUNKS], F32, name="sum_u")
         sum_sq = keep.tile([P, 2, MT, CHUNKS], F32, name="sum_sq")
-        csum = keep.tile([P, MT], F32, name="csum")
-        csq = keep.tile([P, MT], F32, name="csq")
+        csum = keep.tile([P, MT, 2], F32, name="csum")
+        csq = keep.tile([P, MT, 2], F32, name="csq")
         bsum = keep.tile([P, 2], F32, name="bsum")
 
         def copy_on(eng, out, in_):
@@ -69,109 +77,107 @@ def tile_adaptivelstmcell_pb_kernel(
             else:
                 nc.vector.tensor_copy(out=out, in_=in_)
 
-        def transpose_quantize(raw, codes, scales, engines):
-            words = raw[:].bitcast(F32)
-            for g in range(PASSES):
-                grouped = grp.tile([P, 4 * NT], BF16, name="grouped", tag="grouped", align_bytes=64)
-                gw = grouped[:].bitcast(F32).rearrange("p (c u) -> p c u", u=2)
-                for half in range(2):
-                    pt = pst.tile([P, 2, 256], F32, name="pt", tag="t")
-                    for bb in range(2):
-                        for u in range(2):
-                            nc.tensor.transpose(
-                                pt[:, u, P * bb:P * (bb + 1)],
-                                words[:, 2 * half + bb, 256 * g + u:256 * (g + 1):2],
-                                ident_f[:],
-                            )
-                    copy_on(engines[2 * g + half], gw[:, 256 * half:256 * (half + 1), :],
-                            pt[:].rearrange("p u c -> p c u"))
-                nc.vector.quantize_mx(out=codes[:, g, :].bitcast(FP8X4), scales=scales[:, g, :], in_=grouped[:])
+        def k_run(words, codes, scales, g, engines):
+            grouped = grp.tile([P, 4 * NT], BF16, name="grouped", tag="grouped", align_bytes=64)
+            gw = grouped[:].bitcast(F32).rearrange("p (c u) -> p c u", u=2)
+            for half in range(2):
+                pt = pst.tile([P, 2, 256], F32, name="pt", tag="t")
+                for bb in range(2):
+                    for u in range(2):
+                        nc.tensor.transpose(
+                            pt[:, u, P * bb:P * (bb + 1)],
+                            words[:, 2 * half + bb, 256 * g + u:256 * (g + 1):2],
+                            ident_f[:],
+                        )
+                copy_on(engines[half], gw[:, 256 * half:256 * (half + 1), :], pt[:].rearrange("p u c -> p c u"))
+            nc.vector.quantize_mx(out=codes[:, g, :].bitcast(FP8X4), scales=scales[:, g, :], in_=grouped[:])
 
-        def load_rows(src2d):
-            raw = rawp.tile([P, 4, K], BF16, name="raw", tag="raw")
-            nc.sync.dma_start(out=raw[:], in_=src2d.rearrange("(b r) k -> r b k", r=P))
-            return raw
+        def rows_view(src2d):
+            return src2d.rearrange("(b r) k -> r b k", r=P)
 
-        def prep_x(q):
-            raw = load_rows((x, hx)[q])
-            transpose_quantize(raw, xcodes[q], xscales[q], (0, 1, 0, 1))
+        early = []
+        for i, src in enumerate((x, zw.rearrange("b s a -> b (s a)"), zb.rearrange("b s a -> b (s a)"), hx)):
+            view = gbuf[1][4 + i][:].bitcast(BF16)
+            early.append(view)
+        x_raw, zw_raw, zb_raw, hx_raw = early
 
-        def prep_z(i):
-            raw = load_rows((zw, zb)[i].rearrange("b s a -> b (s a)"))
-            for s in range(8):
-                pt = pst.tile([P, BATCH], BF16, name="ptz", tag="t")
-                for m in range(MT):
-                    nc.tensor.transpose(pt[:, P * m:P * (m + 1)], raw[:, m, P * s:P * (s + 1)], ident_b[:])
-                copy_on(s % 2, zT[i][:, s, :], pt[:])
-
-        def prep_chunk(c):
+        def load_chunk(c):
             q, j = divmod(c, CHUNKS)
             s = 4 * q + j // 2
             h0 = NT * (j % 2)
             n0 = NT * j
-            raw = load_rows((w_ih, w_hh)[q][n0:n0 + NT, :])
+            raw = rawp.tile([P, 4, K], BF16, name="raw", tag="raw")
+            nc.sync.dma_start(out=raw[:], in_=rows_view((w_ih, w_hh)[q][n0:n0 + NT, :]))
             small = []
             for i, wsrc in enumerate((norm_alpha_w, bias_beta_w)):
                 sraw = abp.tile([P, 4, P], BF16, name="sraw%d" % i, tag="sraw%d" % i)
                 nc.sync.dma_start(out=sraw[:], in_=wsrc[s, h0:h0 + NT, :].rearrange("(b r) a -> r b a", r=P))
                 small.append(sraw)
-            bias = abp.tile([P, NT], BF16, name="bias", tag="bias")
+            bias = abp.tile([P, NT], BF16, name="bias", tag="bias", bufs=4)
             nc.sync.dma_start(out=bias[:], in_=(b_ih, b_hh)[q][n0:n0 + NT].partition_broadcast(P))
-            codes = wq.tile([P, PASSES, NT], U32, name="wcodes", tag="wcodes", align_bytes=64)
-            scales = wq.tile([P, PASSES, NT], U8, name="wscales", tag="wscales", align_bytes=64)
-            transpose_quantize(raw, codes, scales, (0, 1, 0, 1) if q == 0 else (0, 0, 0, 0))
+            return {"raw": raw, "small": small, "bias": bias, "q": q}
+
+        def w_run(ch, g):
+            if g == 0:
+                ch["codes"] = wq.tile([P, PASSES, NT], U32, name="wcodes", tag="wcodes", align_bytes=64)
+                ch["scales"] = wq.tile([P, PASSES, NT], U8, name="wscales", tag="wscales", align_bytes=64)
+            k_run(ch["raw"][:].bitcast(F32), ch["codes"], ch["scales"], g, W_COPY[ch["q"]])
+
+        def ab_run(ch):
             abT = []
             for i in range(2):
                 pt = pst.tile([P, NT], BF16, name="pta", tag="t")
                 for b in range(4):
-                    nc.tensor.transpose(pt[:, P * b:P * (b + 1)], small[i][:, b, :], ident_b[:])
+                    nc.tensor.transpose(pt[:, P * b:P * (b + 1)], ch["small"][i][:, b, :], ident_b[:])
                 wT = abp.tile([P, NT], BF16, name="wT%d" % i, tag="wT%d" % i)
-                copy_on(1 - q, wT[:], pt[:])
+                copy_on(AB_COPY[i], wT[:], pt[:])
                 abT.append(wT)
-            return codes, scales, abT, bias
+            ch["abT"] = abT
 
-        def compute_chunk(c, prepared):
-            codes, scales, abT, bias = prepared
+        def z_run(s):
+            for i, raw in enumerate((zw_raw, zb_raw)):
+                pt = pst.tile([P, BATCH], BF16, name="ptz", tag="t")
+                for m in range(MT):
+                    nc.tensor.transpose(pt[:, P * m:P * (m + 1)], raw[:, m, P * s:P * (s + 1)], ident_b[:])
+                copy_on(Z_COPY[i], zT[i][:, s, :], pt[:])
+
+        def mm(c, ch, m):
             q, j = divmod(c, CHUNKS)
             s = 4 * q + j // 2
-            n0 = NT * j
-            for m in range(MT):
-                rows = slice(P * m, P * (m + 1))
-                xh = psx.tile([P, NT], F32, name="xh", tag="xh")
-                for g in range(PASSES):
-                    nc.tensor.matmul_mx(
-                        out=xh[:],
-                        lhsT=xcodes[q][:, g, rows].bitcast(FP8X4),
-                        lhsT_scale=xscales[q][:, g, rows],
-                        rhs=codes[:, g, :].bitcast(FP8X4),
-                        rhs_scale=scales[:, g, :],
-                        start=(g == 0),
-                        stop=(g == PASSES - 1),
-                    )
-                alpha = psa.tile([P, NT], F32, name="alpha", tag="alpha")
-                nc.tensor.matmul(out=alpha[:], lhsT=zT[0][:, s, rows], rhs=abT[0][:], start=True, stop=True)
-                beta = psb.tile([P, NT], F32, name="beta", tag="beta")
-                nc.tensor.matmul(out=beta[:], lhsT=zT[1][:, s, rows], rhs=abT[1][:], start=True, stop=True)
-                al = work.tile([P, NT], F32, name="al", tag="al")
-                nc.scalar.copy(out=al[:], in_=alpha[:])
-                dst = gbuf[q][m][:, n0:n0 + NT]
-                nc.vector.tensor_tensor(out=dst, in0=xh[:], in1=al[:], op=ALU.mult)
-                nc.vector.scalar_tensor_tensor(out=dst, in0=dst, scalar=1.0, in1=beta[:], op0=ALU.mult,
-                                               op1=ALU.add, accum_out=sum_u[:, q, m, j:j + 1])
-                nc.gpsimd.tensor_tensor(out=dst, in0=dst, in1=bias[:], op=ALU.add)
-                junk = work.tile([P, NT], BF16, name="junk", tag="junk")
-                nc.scalar.activation(out=junk[:], in_=dst, func=ACT.Square, accum_out=sum_sq[:, q, m, j:j + 1])
+            rows = slice(P * m, P * (m + 1))
+            alpha = psa.tile([P, NT], F32, name="alpha", tag="alpha")
+            nc.tensor.matmul(out=alpha[:], lhsT=zT[0][:, s, rows], rhs=ch["abT"][0][:], start=True, stop=True)
+            beta = psb.tile([P, NT], F32, name="beta", tag="beta")
+            nc.tensor.matmul(out=beta[:], lhsT=zT[1][:, s, rows], rhs=ch["abT"][1][:], start=True, stop=True)
+            xh = psx.tile([P, NT], F32, name="xh", tag="xh")
+            for g in range(PASSES):
+                nc.tensor.matmul_mx(
+                    out=xh[:],
+                    lhsT=xcodes[q][:, g, rows].bitcast(FP8X4),
+                    lhsT_scale=xscales[q][:, g, rows],
+                    rhs=ch["codes"][:, g, :].bitcast(FP8X4),
+                    rhs_scale=ch["scales"][:, g, :],
+                    start=(g == 0),
+                    stop=(g == PASSES - 1),
+                )
+            al = work.tile([P, NT], F32, name="al", tag="al")
+            nc.scalar.copy(out=al[:], in_=alpha[:])
+            dst = gbuf[q][j][:, m, :]
+            nc.vector.tensor_tensor(out=dst, in0=xh[:], in1=al[:], op=ALU.mult)
+            nc.vector.scalar_tensor_tensor(out=dst, in0=dst, scalar=1.0, in1=beta[:], op0=ALU.mult,
+                                           op1=ALU.add, accum_out=sum_u[:, q, m, j:j + 1])
+            nc.gpsimd.tensor_tensor(out=dst, in0=dst, in1=ch["bias"][:], op=ALU.add)
+            junk = work.tile([P, NT], BF16, name="junk", tag="junk")
+            nc.scalar.activation(out=junk[:], in_=dst, func=ACT.Square, accum_out=sum_sq[:, q, m, j:j + 1])
 
-        def gate_stats(q, label):
+        def finish_stats(sums, squares, extra, count, label):
             s1 = keep.tile([P, MT], F32, name="s1" + label)
             s2 = keep.tile([P, MT], F32, name="s2" + label)
-            nc.vector.tensor_reduce(out=s1[:], in_=sum_u[:, q, :, :], axis=AX.X, op=ALU.add)
-            nc.vector.tensor_reduce(out=s2[:], in_=sum_sq[:, q, :, :], axis=AX.X, op=ALU.add)
-            return finish_stats(s1, s2, bsum[:, q:q + 1], GATES, label)
-
-        def finish_stats(s1, s2, extra, count, label):
             mean = keep.tile([P, MT], F32, name="mean" + label)
             rstd = keep.tile([P, MT], F32, name="rstd" + label)
+            shift = keep.tile([P, MT], F32, name="shift" + label)
+            nc.vector.tensor_reduce(out=s1[:], in_=sums, axis=AX.X, op=ALU.add)
+            nc.vector.tensor_reduce(out=s2[:], in_=squares, axis=AX.X, op=ALU.add)
             nc.vector.tensor_scalar(out=mean[:], in0=s1[:], scalar1=extra, scalar2=1.0 / count,
                                     op0=ALU.add, op1=ALU.mult)
             nc.vector.tensor_tensor(out=s1[:], in0=mean[:], in1=mean[:], op=ALU.mult)
@@ -179,99 +185,179 @@ def tile_adaptivelstmcell_pb_kernel(
                                            op0=ALU.mult, op1=ALU.subtract)
             nc.vector.tensor_scalar(out=s2[:], in0=s2[:], scalar1=0.0, scalar2=EPS, op0=ALU.max, op1=ALU.add)
             nc.gpsimd.tensor_tensor(out=rstd[:], in0=s2[:], in1=neg_half[:], op=ALU.pow)
-            return mean, rstd
+            nc.vector.scalar_tensor_tensor(out=shift[:], in0=mean[:], scalar=-1.0, in1=rstd[:],
+                                           op0=ALU.mult, op1=ALU.mult)
+            return mean, rstd, shift
 
-        def bcast(vec, lo, tag, bufs):
-            t = cst.tile([P, H], BF16, name=tag, tag=tag, bufs=bufs)
-            nc.sync.dma_start(out=t[:], in_=vec[lo:lo + H].partition_broadcast(P))
-            return t
+        def normalise(eng, q, m, d, st):
+            reg = gbuf[q][d][:, m, :]
+            rs = st[1][:, m:m + 1]
+            sh = st[2][:, m:m + 1]
+            if eng == 0:
+                nc.scalar.activation(out=reg, in_=reg, func=ACT.Identity, bias=sh, scale=rs)
+            elif eng == 1:
+                nc.vector.tensor_scalar(out=reg, in0=reg, scalar1=rs, scalar2=sh, op0=ALU.mult, op1=ALU.add)
+            else:
+                nc.gpsimd.tensor_scalar(out=reg, in0=reg, scalar1=rs, scalar2=sh, op0=ALU.mult, op1=ALU.add)
 
+        def turn(q, cb):
+            pt = pst.tile([P, BATCH], F32, name="ptn", tag="t")
+            k = cb % 4
+            for m in range(MT):
+                nc.tensor.transpose(pt[:, P * m:P * (m + 1)], gbuf[q][cb // 4][:, m, P * k:P * (k + 1)], ident_f[:])
+            return pt
+
+        def region(cb):
+            return turned[cb // 4][:, cb % 4, :]
+
+        stats = [None, None]
+
+        def norm_in(d):
+            for m in range(MT):
+                normalise(NORM_IN[m], 0, m, d, stats[0])
+
+        def n_run(d, ks):
+            for i, k in enumerate(ks):
+                cb = 4 * d + k
+                pt = turn(0, cb)
+                if N_COPY[i] == 0:
+                    nc.scalar.activation(out=region(cb), in_=pt[:], func=ACT.Identity,
+                                         bias=lbT[:, cb:cb + 1], scale=prmT[:, cb:cb + 1])
+                else:
+                    nc.vector.tensor_scalar(out=region(cb), in0=pt[:], scalar1=prmT[:, cb:cb + 1],
+                                            scalar2=lbT[:, cb:cb + 1], op0=ALU.mult, op1=ALU.add)
+
+        nc.sync.dma_start(out=x_raw, in_=rows_view(x))
+        chunks = {0: load_chunk(0)}
+        nc.sync.dma_start(out=zw_raw, in_=rows_view(zw.rearrange("b s a -> b (s a)")))
+        nc.sync.dma_start(out=zb_raw, in_=rows_view(zb.rearrange("b s a -> b (s a)")))
+        chunks[1] = load_chunk(1)
         bsm = keep.tile([P, 2, 32], BF16, name="bsm")
         nc.sync.dma_start(out=bsm[:, 0, :], in_=b_ih.rearrange("(p c) -> p c", c=32))
         nc.sync.dma_start(out=bsm[:, 1, :], in_=b_hh.rearrange("(p c) -> p c", c=32))
-
-        prep_x(0)
-        nxt = prep_chunk(0)
-        prep_z(0)
-        prep_z(1)
-
+        prm = keep.tile([P, P], BF16, name="prm")
+        for i, vec in enumerate((ln_i_w, ln_h_w, ln_i_b, ln_h_b)):
+            nc.sync.dma_start(out=prm[32 * i:32 * (i + 1), :], in_=vec.rearrange("(c p) -> c p", p=P))
+        nc.sync.dma_start(out=hx_raw, in_=rows_view(hx))
         bpart = keep.tile([P, 2], F32, name="bpart")
-        nc.vector.tensor_reduce(out=bpart[:], in_=bsm[:], axis=AX.X, op=ALU.add)
-        pb = pst.tile([P, 2], F32, name="pb", tag="t")
-        nc.tensor.matmul(out=pb[:], lhsT=ones_f[:], rhs=bpart[:], start=True, stop=True)
-        nc.vector.tensor_copy(out=bsum[:], in_=pb[:])
+        prmT = keep.tile([P, P], F32, name="prmT")
+        lbT = keep.tile([P, 32], F32, name="lbT")
 
-        stats = [None, None]
-        post_c = {}
-
-        def post_in(gi, ms):
-            cols = slice(H * gi, H * (gi + 1))
-            if gi not in post_c:
-                wi = bcast(ln_i_w, H * gi, "lnw", 2)
-                lbi = bcast(ln_i_b, H * gi, "lbi", 1)
-                lbh = bcast(ln_h_b, H * gi, "lbh", 1)
-                lb = cst.tile([P, H], F32, name="lb", tag="lb")
-                nc.gpsimd.tensor_tensor(out=lb[:], in0=lbi[:], in1=lbh[:], op=ALU.add)
-                post_c[gi] = (wi, lb)
-            wi, lb = post_c[gi]
-            mean, rstd = stats[0]
-            for m in ms:
-                t = gbuf[0][m][:, cols]
-                nc.vector.scalar_tensor_tensor(out=t, in0=t, scalar=mean[:, m:m + 1], in1=wi[:],
-                                               op0=ALU.subtract, op1=ALU.mult)
-                nc.vector.scalar_tensor_tensor(out=t, in0=t, scalar=rstd[:, m:m + 1], in1=lb[:],
-                                               op0=ALU.mult, op1=ALU.add)
-
-        for c in range(2 * CHUNKS):
-            cur = nxt
-            if c == 5:
-                prep_x(1)
-            if c + 1 < 2 * CHUNKS:
-                nxt = prep_chunk(c + 1)
-            compute_chunk(c, cur)
-            if c == CHUNKS - 1:
-                stats[0] = gate_stats(0, "i")
-            if c >= CHUNKS:
+        with tc.manual_schedule(engines={mybir.EngineType.PE}):
+            k_run(x_raw.bitcast(F32), xcodes[0], xscales[0], 0, (0, 1))
+            k_run(x_raw.bitcast(F32), xcodes[0], xscales[0], 1, (0, 1))
+            w_run(chunks[0], 0)
+            w_run(chunks[0], 1)
+            ab_run(chunks[0])
+            z_run(0)
+            for c in range(2 * CHUNKS):
+                ch = chunks[c]
+                last = c + 1 == 2 * CHUNKS
                 d = c - CHUNKS
-                post_in(d // 2, (0, 1) if d % 2 == 0 else (2, 3))
+                if c + 2 < 2 * CHUNKS:
+                    chunks[c + 2] = load_chunk(c + 2)
+                if not last:
+                    w_run(chunks[c + 1], 0)
+                mm(c, ch, 0)
+                if not last:
+                    w_run(chunks[c + 1], 1)
+                mm(c, ch, 1)
+                if not last:
+                    ab_run(chunks[c + 1])
+                mm(c, ch, 2)
+                if c < 7:
+                    z_run(c + 1)
+                if c == 7:
+                    k_run(hx_raw.bitcast(F32), xcodes[1], xscales[1], 1, (0, 1))
+                if d >= 1:
+                    n_run(d - 1, (0, 1))
+                mm(c, ch, 3)
+                if c == 6:
+                    k_run(hx_raw.bitcast(F32), xcodes[1], xscales[1], 0, (0, 1))
+                if c == 0:
+                    nc.vector.tensor_reduce(out=bpart[:], in_=bsm[:], axis=AX.X, op=ALU.add)
+                    pb = pst.tile([P, 2], F32, name="pb", tag="t")
+                    nc.tensor.matmul(out=pb[:], lhsT=ones_f[:], rhs=bpart[:], start=True, stop=True)
+                    nc.vector.tensor_copy(out=bsum[:], in_=pb[:])
+                    pp = pst.tile([P, P], BF16, name="pp", tag="t")
+                    nc.tensor.transpose(pp[:], prm[:], ident_b[:])
+                    nc.vector.tensor_copy(out=prmT[:], in_=pp[:])
+                    nc.vector.tensor_tensor(out=lbT[:], in0=prmT[:, 64:96], in1=prmT[:, 96:128], op=ALU.add)
+                if d >= 1:
+                    n_run(d - 1, (2, 3))
+                if c == CHUNKS - 1:
+                    stats[0] = finish_stats(sum_u[:, 0, :, :], sum_sq[:, 0, :, :], bsum[:, 0:1], GATES, "i")
+                if d >= 0:
+                    norm_in(d)
+            n_run(CHUNKS - 1, (0, 1))
+            n_run(CHUNKS - 1, (2, 3))
 
-        stats[1] = gate_stats(1, "h")
-        cxt = load_rows(cx)
-        wc = bcast(ln_c_w, 0, "wc", 1)
-        bc = bcast(ln_c_b, 0, "bc", 1)
-        mean_h, rstd_h = stats[1]
-        funcs = (ACT.Sigmoid, ACT.Tanh, ACT.Sigmoid, ACT.Sigmoid)
-        for gi in (2, 0, 1, 3):
-            cols = slice(H * gi, H * (gi + 1))
-            wh = bcast(ln_h_w, H * gi, "lnw", 2)
+        stats[1] = finish_stats(sum_u[:, 1, :, :], sum_sq[:, 1, :, :], bsum[:, 1:2], GATES, "h")
+        cxt = rawp.tile([P, 4, K], BF16, name="raw", tag="raw")
+        nc.sync.dma_start(out=cxt[:], in_=rows_view(cx))
+        wc = keep.tile([P, H], BF16, name="wc")
+        nc.sync.dma_start(out=wc[:], in_=ln_c_w.partition_broadcast(P))
+        bc = keep.tile([P, H], BF16, name="bc")
+        nc.sync.dma_start(out=bc[:], in_=ln_c_b.partition_broadcast(P))
+
+        def gate(cb, func):
+            pt = turn(1, cb)
+            reg = region(cb)
+            nc.vector.scalar_tensor_tensor(out=reg, in0=pt[:], scalar=prmT[:, 32 + cb:33 + cb], in1=reg,
+                                           op0=ALU.mult, op1=ALU.add)
+            nc.scalar.activation(out=reg, in_=reg, func=func)
+            return reg
+
+        def norm_piece(d):
             for m in range(MT):
-                t = gbuf[1][m][:, cols]
-                o = gbuf[0][m][:, cols]
-                nc.vector.scalar_tensor_tensor(out=t, in0=t, scalar=mean_h[:, m:m + 1], in1=wh[:],
-                                               op0=ALU.subtract, op1=ALU.mult)
-                nc.vector.scalar_tensor_tensor(out=o, in0=t, scalar=rstd_h[:, m:m + 1], in1=o,
-                                               op0=ALU.mult, op1=ALU.add)
-                nc.scalar.activation(out=o, in_=o, func=funcs[gi])
+                normalise(TAIL_NORM[m], 1, m, d, stats[1])
 
+        back_pools = ((psx, "xh"), (psx, "xh"), (psa, "alpha"), (psa, "alpha"))
+        for half in range(2):
+            for gi in (2, 0, 1):
+                norm_piece(2 * gi + half)
+            for hb in range(4 * half, 4 * half + 4):
+                f_t = gate(16 + hb, ACT.Sigmoid)
+                i_t = gate(hb, ACT.Sigmoid)
+                j_t = gate(8 + hb, ACT.Tanh)
+                cxT = psb.tile([P, BATCH], BF16, name="cxT", tag="beta")
+                for m in range(MT):
+                    nc.tensor.transpose(cxT[:, P * m:P * (m + 1)], cxt[:, m, P * hb:P * (hb + 1)], ident_b[:])
+                nc.vector.tensor_tensor(out=f_t, in0=f_t, in1=cxT[:], op=ALU.mult)
+                nc.gpsimd.tensor_tensor(out=i_t, in0=i_t, in1=j_t, op=ALU.mult)
+                nc.vector.tensor_tensor(out=f_t, in0=f_t, in1=i_t, op=ALU.add)
+            for m in range(MT):
+                pool, tag = back_pools[m]
+                sb = pool.tile([P, NT], F32, name="sb", tag=tag)
+                for k in range(4):
+                    cb = 16 + 4 * half + k
+                    nc.tensor.transpose(sb[:, P * k:P * (k + 1)], region(cb)[:, P * m:P * (m + 1)], ident_f[:])
+                nc.scalar.activation(out=gbuf[1][half][:, m, :], in_=sb[:], func=ACT.Identity,
+                                     accum_out=csum[:, m, half:half + 1])
+                junk = work.tile([P, NT], BF16, name="junk", tag="junk")
+                nc.scalar.activation(out=junk[:], in_=sb[:], func=ACT.Square, accum_out=csq[:, m, half:half + 1])
+        for half in range(2):
+            norm_piece(6 + half)
+        for hb in range(8):
+            gate(24 + hb, ACT.Sigmoid)
+        st_c = finish_stats(csum[:], csq[:], 0.0, H, "c")
         for m in range(MT):
-            gm = gbuf[0][m]
-            sc = gbuf[1][m]
-            nc.vector.tensor_tensor(out=sc[:, 0:H], in0=gm[:, 2 * H:3 * H], in1=cxt[:, m, :], op=ALU.mult)
-            nc.vector.tensor_tensor(out=sc[:, H:2 * H], in0=gm[:, 0:H], in1=gm[:, H:2 * H], op=ALU.mult)
-            nc.vector.scalar_tensor_tensor(out=sc[:, 2 * H:3 * H], in0=sc[:, 0:H], scalar=1.0, in1=sc[:, H:2 * H],
-                                           op0=ALU.mult, op1=ALU.add, accum_out=csum[:, m:m + 1])
-            nc.scalar.activation(out=sc[:, 3 * H:4 * H], in_=sc[:, 2 * H:3 * H], func=ACT.Square,
-                                 accum_out=csq[:, m:m + 1])
-        mean_c, rstd_c = finish_stats(csum, csq, 0.0, H, "c")
-        for m in range(MT):
-            gm = gbuf[0][m]
-            sc = gbuf[1][m]
             rows = slice(P * m, P * (m + 1))
-            nc.vector.scalar_tensor_tensor(out=sc[:, 0:H], in0=sc[:, 2 * H:3 * H], scalar=mean_c[:, m:m + 1],
-                                           in1=wc[:], op0=ALU.subtract, op1=ALU.mult)
-            nc.vector.scalar_tensor_tensor(out=sc[:, H:2 * H], in0=sc[:, 0:H], scalar=rstd_c[:, m:m + 1],
-                                           in1=bc[:], op0=ALU.mult, op1=ALU.add)
-            nc.sync.dma_start(out=out_1[rows, :], in_=sc[:, H:2 * H])
-            nc.scalar.activation(out=sc[:, 3 * H:4 * H], in_=sc[:, H:2 * H], func=ACT.Tanh)
-            nc.vector.tensor_tensor(out=sc[:, 0:H], in0=sc[:, 3 * H:4 * H], in1=gm[:, 3 * H:4 * H], op=ALU.mult)
-            nc.sync.dma_start(out=out_0[rows, :], in_=sc[:, 0:H])
+            for half in range(2):
+                cols = slice(NT * half, NT * (half + 1))
+                s_t = gbuf[1][half][:, m, :]
+                cy_t = gbuf[1][2 + half][:, m, :]
+                th_t = gbuf[1][4 + half][:, m, :]
+                nc.vector.scalar_tensor_tensor(out=s_t, in0=s_t, scalar=st_c[0][:, m:m + 1], in1=wc[:, cols],
+                                               op0=ALU.subtract, op1=ALU.mult)
+                nc.vector.scalar_tensor_tensor(out=cy_t, in0=s_t, scalar=st_c[1][:, m:m + 1], in1=bc[:, cols],
+                                               op0=ALU.mult, op1=ALU.add)
+                nc.sync.dma_start(out=out_1[rows, cols], in_=cy_t)
+                nc.scalar.activation(out=th_t, in_=cy_t, func=ACT.Tanh)
+                pool, tag = back_pools[2 * half]
+                ob = pool.tile([P, NT], F32, name="ob", tag=tag)
+                for k in range(4):
+                    nc.tensor.transpose(ob[:, P * k:P * (k + 1)], region(24 + 4 * half + k)[:, P * m:P * (m + 1)],
+                                        ident_f[:])
+                nc.vector.tensor_tensor(out=s_t, in0=th_t, in1=ob[:], op=ALU.mult)
+                nc.sync.dma_start(out=out_0[rows, cols], in_=s_t)

@@ -23,11 +23,9 @@ PASSES = 2
 CHUNKS = GATES // NT
 EPS = 1e-5
 
-W_COPY = ((0, 1), (0, 1))
+W_COPY = (((0, 1), (0, 1)), ((1, 0), (1, 1)))
 AB_COPY = (0, 0)
-Z_COPY = (0, 1)
-N_COPY = (0, 0)
-NORM_IN = (2, 2, 1, 1)
+Z_COPY = (0, 0)
 TAIL_NORM = (1, 1, 0, 2)
 
 FLOPS = 2 * 2 * BATCH * GATES * K + 16 * 2 * BATCH * H * 128
@@ -41,7 +39,6 @@ def tile_adaptivelstmcell_pb_kernel(
     with ExitStack() as ctx:
         keep = ctx.enter_context(tc.tile_pool(name="keep", bufs=1))
         rawp = ctx.enter_context(tc.tile_pool(name="rawp", bufs=3))
-        grp = ctx.enter_context(tc.tile_pool(name="grp", bufs=2))
         wq = ctx.enter_context(tc.tile_pool(name="wq", bufs=2))
         abp = ctx.enter_context(tc.tile_pool(name="abp", bufs=2))
         work = ctx.enter_context(tc.tile_pool(name="work", bufs=3))
@@ -49,6 +46,7 @@ def tile_adaptivelstmcell_pb_kernel(
         psx = ctx.enter_context(tc.psum_pool(name="psx", bufs=2))
         psa = ctx.enter_context(tc.psum_pool(name="psa", bufs=2))
         psb = ctx.enter_context(tc.psum_pool(name="psb", bufs=2))
+        ctx.enter_context(tc.manual_schedule())
 
         ident_f = keep.tile([P, P], F32, name="ident_f")
         make_identity(nc, ident_f[:])
@@ -65,6 +63,7 @@ def tile_adaptivelstmcell_pb_kernel(
         gbuf = [[keep.tile([P, MT, NT], F32, name="g%d_%d" % (q, d)) for d in range(CHUNKS)] for q in range(2)]
         spare = keep.tile([P, MT, NT], F32, name="spare")
         turned = [spare] + gbuf[0][0:CHUNKS - 1]
+        grouped = keep.tile([P, PASSES, 4 * NT], BF16, name="grouped", align_bytes=64)
         sum_u = keep.tile([P, 2, MT, CHUNKS], F32, name="sum_u")
         sum_sq = keep.tile([P, 2, MT, CHUNKS], F32, name="sum_sq")
         csum = keep.tile([P, MT, 2], F32, name="csum")
@@ -77,9 +76,9 @@ def tile_adaptivelstmcell_pb_kernel(
             else:
                 nc.vector.tensor_copy(out=out, in_=in_)
 
-        def k_run(words, codes, scales, g, engines):
-            grouped = grp.tile([P, 4 * NT], BF16, name="grouped", tag="grouped", align_bytes=64)
-            gw = grouped[:].bitcast(F32).rearrange("p (c u) -> p c u", u=2)
+        def k_run(words, g, engines):
+            gw = grouped[:, g, :].bitcast(F32).rearrange("p (c u) -> p c u", u=2)
+            banks = []
             for half in range(2):
                 pt = pst.tile([P, 2, 256], F32, name="pt", tag="t")
                 for bb in range(2):
@@ -89,17 +88,23 @@ def tile_adaptivelstmcell_pb_kernel(
                             words[:, 2 * half + bb, 256 * g + u:256 * (g + 1):2],
                             ident_f[:],
                         )
-                copy_on(engines[half], gw[:, 256 * half:256 * (half + 1), :], pt[:].rearrange("p u c -> p c u"))
-            nc.vector.quantize_mx(out=codes[:, g, :].bitcast(FP8X4), scales=scales[:, g, :], in_=grouped[:])
+                banks.append(pt)
+            for half in range(2):
+                copy_on(engines[half], gw[:, 256 * half:256 * (half + 1), :],
+                        banks[half][:].rearrange("p u c -> p c u"))
+
+        def quantise(codes, scales):
+            nc.vector.quantize_mx(out=codes[:].rearrange("p g c -> p (g c)").bitcast(FP8X4),
+                                  scales=scales[:].rearrange("p g c -> p (g c)"),
+                                  in_=grouped[:].rearrange("p g c -> p (g c)"))
 
         def rows_view(src2d):
             return src2d.rearrange("(b r) k -> r b k", r=P)
 
-        early = []
-        for i, src in enumerate((x, zw.rearrange("b s a -> b (s a)"), zb.rearrange("b s a -> b (s a)"), hx)):
-            view = gbuf[1][4 + i][:].bitcast(BF16)
-            early.append(view)
-        x_raw, zw_raw, zb_raw, hx_raw = early
+        x_raw, zw_raw, zb_raw, hx_raw = [gbuf[1][4 + i][:].bitcast(BF16) for i in range(4)]
+        chunks = {}
+        als = {}
+        betas = {}
 
         def load_chunk(c):
             q, j = divmod(c, CHUNKS)
@@ -113,42 +118,68 @@ def tile_adaptivelstmcell_pb_kernel(
                 sraw = abp.tile([P, 4, P], BF16, name="sraw%d" % i, tag="sraw%d" % i)
                 nc.sync.dma_start(out=sraw[:], in_=wsrc[s, h0:h0 + NT, :].rearrange("(b r) a -> r b a", r=P))
                 small.append(sraw)
-            bias = abp.tile([P, NT], BF16, name="bias", tag="bias", bufs=4)
-            nc.sync.dma_start(out=bias[:], in_=(b_ih, b_hh)[q][n0:n0 + NT].partition_broadcast(P))
-            return {"raw": raw, "small": small, "bias": bias, "q": q}
+            if j % 2 == 0:
+                bias2 = abp.tile([P, 2, NT], BF16, name="bias", tag="bias", bufs=3)
+                nc.sync.dma_start(out=bias2[:].rearrange("p a n -> p (a n)"),
+                                  in_=(b_ih, b_hh)[q][n0:n0 + 2 * NT].partition_broadcast(P))
+            else:
+                bias2 = chunks[c - 1]["bias2"]
+            chunks[c] = {"raw": raw, "small": small, "bias2": bias2, "bias": bias2[:, j % 2, :], "q": q}
 
-        def w_run(ch, g):
-            if g == 0:
-                ch["codes"] = wq.tile([P, PASSES, NT], U32, name="wcodes", tag="wcodes", align_bytes=64)
-                ch["scales"] = wq.tile([P, PASSES, NT], U8, name="wscales", tag="wscales", align_bytes=64)
-            k_run(ch["raw"][:].bitcast(F32), ch["codes"], ch["scales"], g, W_COPY[ch["q"]])
+        def w_run(c, g):
+            ch = chunks[c]
+            k_run(ch["raw"][:].bitcast(F32), g, W_COPY[ch["q"]][g])
 
-        def ab_run(ch):
-            abT = []
+        def w_quantise(c):
+            ch = chunks[c]
+            ch["codes"] = wq.tile([P, PASSES, NT], U32, name="wcodes", tag="wcodes", align_bytes=64)
+            ch["scales"] = wq.tile([P, PASSES, NT], U8, name="wscales", tag="wscales", align_bytes=64)
+            quantise(ch["codes"], ch["scales"])
+
+        def ab_run(c):
+            ch = chunks[c]
+            banks = []
             for i in range(2):
                 pt = pst.tile([P, NT], BF16, name="pta", tag="t")
                 for b in range(4):
                     nc.tensor.transpose(pt[:, P * b:P * (b + 1)], ch["small"][i][:, b, :], ident_b[:])
+                banks.append(pt)
+            abT = []
+            for i in range(2):
                 wT = abp.tile([P, NT], BF16, name="wT%d" % i, tag="wT%d" % i)
-                copy_on(AB_COPY[i], wT[:], pt[:])
+                copy_on(AB_COPY[i], wT[:], banks[i][:])
                 abT.append(wT)
             ch["abT"] = abT
 
         def z_run(s):
-            for i, raw in enumerate((zw_raw, zb_raw)):
+            banks = []
+            for raw in (zw_raw, zb_raw):
                 pt = pst.tile([P, BATCH], BF16, name="ptz", tag="t")
                 for m in range(MT):
                     nc.tensor.transpose(pt[:, P * m:P * (m + 1)], raw[:, m, P * s:P * (s + 1)], ident_b[:])
-                copy_on(Z_COPY[i], zT[i][:, s, :], pt[:])
+                banks.append(pt)
+            for i in range(2):
+                copy_on(Z_COPY[i], zT[i][:, s, :], banks[i][:])
 
-        def mm(c, ch, m):
+        def where(t):
+            c, m = divmod(t, MT)
             q, j = divmod(c, CHUNKS)
-            s = 4 * q + j // 2
-            rows = slice(P * m, P * (m + 1))
+            return c, m, q, j, 4 * q + j // 2, slice(P * m, P * (m + 1))
+
+        def mm_alpha(t):
+            c, m, q, j, s, rows = where(t)
             alpha = psa.tile([P, NT], F32, name="alpha", tag="alpha")
-            nc.tensor.matmul(out=alpha[:], lhsT=zT[0][:, s, rows], rhs=ch["abT"][0][:], start=True, stop=True)
+            nc.tensor.matmul(out=alpha[:], lhsT=zT[0][:, s, rows], rhs=chunks[c]["abT"][0][:], start=True, stop=True)
+            al = work.tile([P, NT], F32, name="al", tag="al")
+            nc.scalar.copy(out=al[:], in_=alpha[:])
+            als[t] = al
+
+        def mm_rest(t):
+            c, m, q, j, s, rows = where(t)
+            ch = chunks[c]
             beta = psb.tile([P, NT], F32, name="beta", tag="beta")
             nc.tensor.matmul(out=beta[:], lhsT=zT[1][:, s, rows], rhs=ch["abT"][1][:], start=True, stop=True)
+            betas[t] = beta
             xh = psx.tile([P, NT], F32, name="xh", tag="xh")
             for g in range(PASSES):
                 nc.tensor.matmul_mx(
@@ -160,48 +191,52 @@ def tile_adaptivelstmcell_pb_kernel(
                     start=(g == 0),
                     stop=(g == PASSES - 1),
                 )
-            al = work.tile([P, NT], F32, name="al", tag="al")
-            nc.scalar.copy(out=al[:], in_=alpha[:])
+            nc.vector.tensor_tensor(out=gbuf[q][j][:, m, :], in0=xh[:], in1=als[t][:], op=ALU.mult)
+
+        def add_beta_bias(t):
+            c, m, q, j, s, rows = where(t)
             dst = gbuf[q][j][:, m, :]
-            nc.vector.tensor_tensor(out=dst, in0=xh[:], in1=al[:], op=ALU.mult)
-            nc.vector.scalar_tensor_tensor(out=dst, in0=dst, scalar=1.0, in1=beta[:], op0=ALU.mult,
+            nc.vector.scalar_tensor_tensor(out=dst, in0=dst, scalar=1.0, in1=betas[t][:], op0=ALU.mult,
                                            op1=ALU.add, accum_out=sum_u[:, q, m, j:j + 1])
-            nc.gpsimd.tensor_tensor(out=dst, in0=dst, in1=ch["bias"][:], op=ALU.add)
+            nc.gpsimd.tensor_tensor(out=dst, in0=dst, in1=chunks[c]["bias"], op=ALU.add)
+
+        def square(t):
+            c, m, q, j, s, rows = where(t)
             junk = work.tile([P, NT], BF16, name="junk", tag="junk")
-            nc.scalar.activation(out=junk[:], in_=dst, func=ACT.Square, accum_out=sum_sq[:, q, m, j:j + 1])
+            nc.scalar.activation(out=junk[:], in_=gbuf[q][j][:, m, :], func=ACT.Square,
+                                 accum_out=sum_sq[:, q, m, j:j + 1])
 
         def finish_stats(sums, squares, extra, count, label):
             s1 = keep.tile([P, MT], F32, name="s1" + label)
             s2 = keep.tile([P, MT], F32, name="s2" + label)
-            mean = keep.tile([P, MT], F32, name="mean" + label)
+            negmean = keep.tile([P, MT], F32, name="negmean" + label)
             rstd = keep.tile([P, MT], F32, name="rstd" + label)
             shift = keep.tile([P, MT], F32, name="shift" + label)
             nc.vector.tensor_reduce(out=s1[:], in_=sums, axis=AX.X, op=ALU.add)
             nc.vector.tensor_reduce(out=s2[:], in_=squares, axis=AX.X, op=ALU.add)
-            nc.vector.tensor_scalar(out=mean[:], in0=s1[:], scalar1=extra, scalar2=1.0 / count,
+            nc.vector.tensor_scalar(out=negmean[:], in0=s1[:], scalar1=extra, scalar2=-1.0 / count,
                                     op0=ALU.add, op1=ALU.mult)
-            nc.vector.tensor_tensor(out=s1[:], in0=mean[:], in1=mean[:], op=ALU.mult)
+            nc.vector.tensor_tensor(out=s1[:], in0=negmean[:], in1=negmean[:], op=ALU.mult)
             nc.vector.scalar_tensor_tensor(out=s2[:], in0=s2[:], scalar=1.0 / count, in1=s1[:],
                                            op0=ALU.mult, op1=ALU.subtract)
             nc.vector.tensor_scalar(out=s2[:], in0=s2[:], scalar1=0.0, scalar2=EPS, op0=ALU.max, op1=ALU.add)
             nc.gpsimd.tensor_tensor(out=rstd[:], in0=s2[:], in1=neg_half[:], op=ALU.pow)
-            nc.vector.scalar_tensor_tensor(out=shift[:], in0=mean[:], scalar=-1.0, in1=rstd[:],
-                                           op0=ALU.mult, op1=ALU.mult)
-            return mean, rstd, shift
+            nc.gpsimd.tensor_tensor(out=shift[:], in0=negmean[:], in1=rstd[:], op=ALU.mult)
+            return negmean, rstd, shift
 
         def normalise(eng, q, m, d, st):
             reg = gbuf[q][d][:, m, :]
+            nm = st[0][:, m:m + 1]
             rs = st[1][:, m:m + 1]
-            sh = st[2][:, m:m + 1]
             if eng == 0:
-                nc.scalar.activation(out=reg, in_=reg, func=ACT.Identity, bias=sh, scale=rs)
+                nc.scalar.activation(out=reg, in_=reg, func=ACT.Identity, bias=st[2][:, m:m + 1], scale=rs)
             elif eng == 1:
-                nc.vector.tensor_scalar(out=reg, in0=reg, scalar1=rs, scalar2=sh, op0=ALU.mult, op1=ALU.add)
+                nc.vector.tensor_scalar(out=reg, in0=reg, scalar1=nm, scalar2=rs, op0=ALU.add, op1=ALU.mult)
             else:
-                nc.gpsimd.tensor_scalar(out=reg, in0=reg, scalar1=rs, scalar2=sh, op0=ALU.mult, op1=ALU.add)
+                nc.gpsimd.tensor_scalar(out=reg, in0=reg, scalar1=nm, scalar2=rs, op0=ALU.add, op1=ALU.mult)
 
-        def turn(q, cb):
-            pt = pst.tile([P, BATCH], F32, name="ptn", tag="t")
+        def turn(q, cb, pool, tag):
+            pt = pool.tile([P, BATCH], F32, name="ptn", tag=tag)
             k = cb % 4
             for m in range(MT):
                 nc.tensor.transpose(pt[:, P * m:P * (m + 1)], gbuf[q][cb // 4][:, m, P * k:P * (k + 1)], ident_f[:])
@@ -212,152 +247,187 @@ def tile_adaptivelstmcell_pb_kernel(
 
         stats = [None, None]
 
-        def norm_in(d):
-            for m in range(MT):
-                normalise(NORM_IN[m], 0, m, d, stats[0])
-
         def n_run(d, ks):
+            banks = [turn(0, 4 * d + k, pst, "t") for k in ks]
             for i, k in enumerate(ks):
                 cb = 4 * d + k
-                pt = turn(0, cb)
-                if N_COPY[i] == 0:
-                    nc.scalar.activation(out=region(cb), in_=pt[:], func=ACT.Identity,
-                                         bias=lbT[:, cb:cb + 1], scale=prmT[:, cb:cb + 1])
-                else:
-                    nc.vector.tensor_scalar(out=region(cb), in0=pt[:], scalar1=prmT[:, cb:cb + 1],
-                                            scalar2=lbT[:, cb:cb + 1], op0=ALU.mult, op1=ALU.add)
+                nc.scalar.activation(out=region(cb), in_=banks[i][:], func=ACT.Identity,
+                                     bias=lbT[:, cb:cb + 1], scale=prmT[:, cb:cb + 1])
 
-        nc.sync.dma_start(out=x_raw, in_=rows_view(x))
-        chunks = {0: load_chunk(0)}
-        nc.sync.dma_start(out=zw_raw, in_=rows_view(zw.rearrange("b s a -> b (s a)")))
-        nc.sync.dma_start(out=zb_raw, in_=rows_view(zb.rearrange("b s a -> b (s a)")))
-        chunks[1] = load_chunk(1)
         bsm = keep.tile([P, 2, 32], BF16, name="bsm")
-        nc.sync.dma_start(out=bsm[:, 0, :], in_=b_ih.rearrange("(p c) -> p c", c=32))
-        nc.sync.dma_start(out=bsm[:, 1, :], in_=b_hh.rearrange("(p c) -> p c", c=32))
         prm = keep.tile([P, P], BF16, name="prm")
-        for i, vec in enumerate((ln_i_w, ln_h_w, ln_i_b, ln_h_b)):
-            nc.sync.dma_start(out=prm[32 * i:32 * (i + 1), :], in_=vec.rearrange("(c p) -> c p", p=P))
-        nc.sync.dma_start(out=hx_raw, in_=rows_view(hx))
         bpart = keep.tile([P, 2], F32, name="bpart")
         prmT = keep.tile([P, P], F32, name="prmT")
         lbT = keep.tile([P, 32], F32, name="lbT")
+        wc = keep.tile([P, H], BF16, name="wc")
+        bc = keep.tile([P, H], BF16, name="bc")
+        tiles = 2 * CHUNKS * MT
+        stats_at = CHUNKS * MT + 2
 
-        with tc.manual_schedule(engines={mybir.EngineType.PE}):
-            k_run(x_raw.bitcast(F32), xcodes[0], xscales[0], 0, (0, 1))
-            k_run(x_raw.bitcast(F32), xcodes[0], xscales[0], 1, (0, 1))
-            w_run(chunks[0], 0)
-            w_run(chunks[0], 1)
-            ab_run(chunks[0])
-            z_run(0)
-            for c in range(2 * CHUNKS):
-                ch = chunks[c]
-                last = c + 1 == 2 * CHUNKS
-                d = c - CHUNKS
-                if c + 2 < 2 * CHUNKS:
-                    chunks[c + 2] = load_chunk(c + 2)
-                if not last:
-                    w_run(chunks[c + 1], 0)
-                mm(c, ch, 0)
-                if not last:
-                    w_run(chunks[c + 1], 1)
-                mm(c, ch, 1)
-                if not last:
-                    ab_run(chunks[c + 1])
-                mm(c, ch, 2)
+        def norm_in_piece(i):
+            normalise(2, 0, i % MT, i // MT, stats[0])
+
+        nc.sync.dma_start(out=x_raw, in_=rows_view(x))
+        load_chunk(0)
+        nc.sync.dma_start(out=zw_raw, in_=rows_view(zw.rearrange("b s a -> b (s a)")))
+        nc.sync.dma_start(out=zb_raw, in_=rows_view(zb.rearrange("b s a -> b (s a)")))
+        load_chunk(1)
+        nc.sync.dma_start(out=bsm[:, 0, :], in_=b_ih.rearrange("(p c) -> p c", c=32))
+        nc.sync.dma_start(out=bsm[:, 1, :], in_=b_hh.rearrange("(p c) -> p c", c=32))
+        for i, vec in enumerate((ln_i_w, ln_h_w, ln_i_b, ln_h_b)):
+            nc.sync.dma_start(out=prm[32 * i:32 * (i + 1), :], in_=vec.rearrange("(c p) -> c p", p=P))
+        nc.sync.dma_start(out=hx_raw, in_=rows_view(hx))
+
+        k_run(x_raw.bitcast(F32), 0, (0, 1))
+        k_run(x_raw.bitcast(F32), 1, (0, 1))
+        z_run(0)
+        quantise(xcodes[0], xscales[0])
+        w_run(0, 0)
+        w_run(0, 1)
+        ab_run(0)
+        w_quantise(0)
+        mm_alpha(0)
+
+        for t in range(tiles + 1):
+            c, m = divmod(t, MT)
+            d = c - CHUNKS
+            more = c + 1 < 2 * CHUNKS
+            live = t < tiles
+            if live and m == 0 and c + 2 < 2 * CHUNKS:
+                load_chunk(c + 2)
+            if live and m < 2 and more:
+                w_run(c + 1, m)
+            if live and m == 2 and more:
+                ab_run(c + 1)
+            if live and m == 3:
                 if c < 7:
                     z_run(c + 1)
-                if c == 7:
-                    k_run(hx_raw.bitcast(F32), xcodes[1], xscales[1], 1, (0, 1))
                 if d >= 1:
                     n_run(d - 1, (0, 1))
-                mm(c, ch, 3)
+            if t + 1 < tiles:
+                mm_alpha(t + 1)
+            if live:
+                mm_rest(t)
+            if t >= 1:
+                add_beta_bias(t - 1)
+            if live and m == 2 and more:
+                w_quantise(c + 1)
+            if live and m == 3:
                 if c == 6:
-                    k_run(hx_raw.bitcast(F32), xcodes[1], xscales[1], 0, (0, 1))
-                if c == 0:
-                    nc.vector.tensor_reduce(out=bpart[:], in_=bsm[:], axis=AX.X, op=ALU.add)
-                    pb = pst.tile([P, 2], F32, name="pb", tag="t")
-                    nc.tensor.matmul(out=pb[:], lhsT=ones_f[:], rhs=bpart[:], start=True, stop=True)
-                    nc.vector.tensor_copy(out=bsum[:], in_=pb[:])
-                    pp = pst.tile([P, P], BF16, name="pp", tag="t")
-                    nc.tensor.transpose(pp[:], prm[:], ident_b[:])
-                    nc.vector.tensor_copy(out=prmT[:], in_=pp[:])
-                    nc.vector.tensor_tensor(out=lbT[:], in0=prmT[:, 64:96], in1=prmT[:, 96:128], op=ALU.add)
+                    k_run(hx_raw.bitcast(F32), 0, (0, 1))
+                    k_run(hx_raw.bitcast(F32), 1, (0, 1))
+                    quantise(xcodes[1], xscales[1])
                 if d >= 1:
                     n_run(d - 1, (2, 3))
-                if c == CHUNKS - 1:
-                    stats[0] = finish_stats(sum_u[:, 0, :, :], sum_sq[:, 0, :, :], bsum[:, 0:1], GATES, "i")
-                if d >= 0:
-                    norm_in(d)
-            n_run(CHUNKS - 1, (0, 1))
-            n_run(CHUNKS - 1, (2, 3))
-
-        stats[1] = finish_stats(sum_u[:, 1, :, :], sum_sq[:, 1, :, :], bsum[:, 1:2], GATES, "h")
+            if t == 3:
+                nc.vector.tensor_reduce(out=bpart[:], in_=bsm[:], axis=AX.X, op=ALU.add)
+                pb = pst.tile([P, 2], F32, name="pb", tag="t")
+                nc.tensor.matmul(out=pb[:], lhsT=ones_f[:], rhs=bpart[:], start=True, stop=True)
+                nc.vector.tensor_copy(out=bsum[:], in_=pb[:])
+                pp = pst.tile([P, P], BF16, name="pp", tag="t")
+                nc.tensor.transpose(pp[:], prm[:], ident_b[:])
+                nc.vector.tensor_copy(out=prmT[:], in_=pp[:])
+                nc.vector.tensor_tensor(out=lbT[:], in0=prmT[:, 64:96], in1=prmT[:, 96:128], op=ALU.add)
+            if t >= 3:
+                square(t - 3)
+            if t == stats_at:
+                stats[0] = finish_stats(sum_u[:, 0, :, :], sum_sq[:, 0, :, :], bsum[:, 0:1], GATES, "i")
+            if stats_at < t <= stats_at + 4:
+                norm_in_piece(2 * (t - stats_at - 1))
+                norm_in_piece(2 * (t - stats_at - 1) + 1)
+            if t > stats_at + 4 and t - stats_at + 3 < 32:
+                norm_in_piece(t - stats_at + 3)
         cxt = rawp.tile([P, 4, K], BF16, name="raw", tag="raw")
         nc.sync.dma_start(out=cxt[:], in_=rows_view(cx))
-        wc = keep.tile([P, H], BF16, name="wc")
         nc.sync.dma_start(out=wc[:], in_=ln_c_w.partition_broadcast(P))
-        bc = keep.tile([P, H], BF16, name="bc")
         nc.sync.dma_start(out=bc[:], in_=ln_c_b.partition_broadcast(P))
+        n_run(CHUNKS - 1, (0, 1))
+        for t in range(tiles + 1, tiles + 3):
+            square(t - 3)
+        n_run(CHUNKS - 1, (2, 3))
 
-        def gate(cb, func):
-            pt = turn(1, cb)
-            reg = region(cb)
-            nc.vector.scalar_tensor_tensor(out=reg, in0=pt[:], scalar=prmT[:, 32 + cb:33 + cb], in1=reg,
-                                           op0=ALU.mult, op1=ALU.add)
-            nc.scalar.activation(out=reg, in_=reg, func=func)
-            return reg
+        stats[1] = finish_stats(sum_u[:, 1, :, :], sum_sq[:, 1, :, :], bsum[:, 1:2], GATES, "h")
+        turn_pools = ((pst, "t"), (psx, "xh"), (pst, "t"), (psx, "xh"))
+        turns = [0]
+
+        def gates(cbs, funcs):
+            banks = []
+            for cb in cbs:
+                pool, tag = turn_pools[turns[0] % 4]
+                turns[0] += 1
+                banks.append(turn(1, cb, pool, tag))
+            for i, cb in enumerate(cbs):
+                nc.vector.scalar_tensor_tensor(out=region(cb), in0=banks[i][:], scalar=prmT[:, 32 + cb:33 + cb],
+                                               in1=region(cb), op0=ALU.mult, op1=ALU.add)
+                nc.scalar.activation(out=region(cb), in_=region(cb), func=funcs[i])
 
         def norm_piece(d):
             for m in range(MT):
                 normalise(TAIL_NORM[m], 1, m, d, stats[1])
 
-        back_pools = ((psx, "xh"), (psx, "xh"), (psa, "alpha"), (psa, "alpha"))
-        for half in range(2):
-            for gi in (2, 0, 1):
-                norm_piece(2 * gi + half)
-            for hb in range(4 * half, 4 * half + 4):
-                f_t = gate(16 + hb, ACT.Sigmoid)
-                i_t = gate(hb, ACT.Sigmoid)
-                j_t = gate(8 + hb, ACT.Tanh)
-                cxT = psb.tile([P, BATCH], BF16, name="cxT", tag="beta")
-                for m in range(MT):
-                    nc.tensor.transpose(cxT[:, P * m:P * (m + 1)], cxt[:, m, P * hb:P * (hb + 1)], ident_b[:])
-                nc.vector.tensor_tensor(out=f_t, in0=f_t, in1=cxT[:], op=ALU.mult)
-                nc.gpsimd.tensor_tensor(out=i_t, in0=i_t, in1=j_t, op=ALU.mult)
-                nc.vector.tensor_tensor(out=f_t, in0=f_t, in1=i_t, op=ALU.add)
+        def s_back(half):
             for m in range(MT):
-                pool, tag = back_pools[m]
-                sb = pool.tile([P, NT], F32, name="sb", tag=tag)
+                sb = psa.tile([P, NT], F32, name="sb", tag="alpha")
                 for k in range(4):
-                    cb = 16 + 4 * half + k
-                    nc.tensor.transpose(sb[:, P * k:P * (k + 1)], region(cb)[:, P * m:P * (m + 1)], ident_f[:])
+                    nc.tensor.transpose(sb[:, P * k:P * (k + 1)], region(16 + 4 * half + k)[:, P * m:P * (m + 1)],
+                                        ident_f[:])
                 nc.scalar.activation(out=gbuf[1][half][:, m, :], in_=sb[:], func=ACT.Identity,
                                      accum_out=csum[:, m, half:half + 1])
                 junk = work.tile([P, NT], BF16, name="junk", tag="junk")
                 nc.scalar.activation(out=junk[:], in_=sb[:], func=ACT.Square, accum_out=csq[:, m, half:half + 1])
-        for half in range(2):
-            norm_piece(6 + half)
+
+        for d in (4, 0, 2):
+            norm_piece(d)
         for hb in range(8):
-            gate(24 + hb, ACT.Sigmoid)
+            gates((16 + hb, hb, 8 + hb), (ACT.Sigmoid, ACT.Sigmoid, ACT.Tanh))
+            cxT = psb.tile([P, BATCH], BF16, name="cxT", tag="beta")
+            for m in range(MT):
+                nc.tensor.transpose(cxT[:, P * m:P * (m + 1)], cxt[:, m, P * hb:P * (hb + 1)], ident_b[:])
+            nc.vector.tensor_tensor(out=region(16 + hb), in0=region(16 + hb), in1=cxT[:], op=ALU.mult)
+            nc.gpsimd.tensor_tensor(out=region(hb), in0=region(hb), in1=region(8 + hb), op=ALU.mult)
+            nc.gpsimd.tensor_tensor(out=region(16 + hb), in0=region(16 + hb), in1=region(hb), op=ALU.add)
+            if hb == 1:
+                for d in (5, 1, 3):
+                    norm_piece(d)
+            if hb == 4:
+                for d in (6, 7):
+                    norm_piece(d)
+            if hb == 5:
+                s_back(0)
+        gates((24, 25, 26), (ACT.Sigmoid, ACT.Sigmoid, ACT.Sigmoid))
+        s_back(1)
+        gates((27, 28, 29), (ACT.Sigmoid, ACT.Sigmoid, ACT.Sigmoid))
+        gates((30, 31), (ACT.Sigmoid, ACT.Sigmoid))
         st_c = finish_stats(csum[:], csq[:], 0.0, H, "c")
-        for m in range(MT):
-            rows = slice(P * m, P * (m + 1))
+
+        def cy_part(m):
             for half in range(2):
                 cols = slice(NT * half, NT * (half + 1))
                 s_t = gbuf[1][half][:, m, :]
-                cy_t = gbuf[1][2 + half][:, m, :]
-                th_t = gbuf[1][4 + half][:, m, :]
                 nc.vector.scalar_tensor_tensor(out=s_t, in0=s_t, scalar=st_c[0][:, m:m + 1], in1=wc[:, cols],
-                                               op0=ALU.subtract, op1=ALU.mult)
-                nc.vector.scalar_tensor_tensor(out=cy_t, in0=s_t, scalar=st_c[1][:, m:m + 1], in1=bc[:, cols],
-                                               op0=ALU.mult, op1=ALU.add)
-                nc.sync.dma_start(out=out_1[rows, cols], in_=cy_t)
-                nc.scalar.activation(out=th_t, in_=cy_t, func=ACT.Tanh)
-                pool, tag = back_pools[2 * half]
+                                               op0=ALU.add, op1=ALU.mult)
+            for half in range(2):
+                cols = slice(NT * half, NT * (half + 1))
+                cy_t = gbuf[1][2 + half][:, m, :]
+                nc.vector.scalar_tensor_tensor(out=cy_t, in0=gbuf[1][half][:, m, :], scalar=st_c[1][:, m:m + 1],
+                                               in1=bc[:, cols], op0=ALU.mult, op1=ALU.add)
+                nc.sync.dma_start(out=out_1[P * m:P * (m + 1), cols], in_=cy_t)
+                nc.scalar.activation(out=gbuf[1][4 + half][:, m, :], in_=cy_t, func=ACT.Tanh)
+
+        def hy_part(m):
+            for half in range(2):
+                cols = slice(NT * half, NT * (half + 1))
+                pool, tag = ((psa, "alpha"), (psb, "beta"))[half]
                 ob = pool.tile([P, NT], F32, name="ob", tag=tag)
                 for k in range(4):
                     nc.tensor.transpose(ob[:, P * k:P * (k + 1)], region(24 + 4 * half + k)[:, P * m:P * (m + 1)],
                                         ident_f[:])
-                nc.vector.tensor_tensor(out=s_t, in0=th_t, in1=ob[:], op=ALU.mult)
-                nc.sync.dma_start(out=out_0[rows, cols], in_=s_t)
+                hy_t = gbuf[1][half][:, m, :]
+                nc.vector.tensor_tensor(out=hy_t, in0=gbuf[1][4 + half][:, m, :], in1=ob[:], op=ALU.mult)
+                nc.sync.dma_start(out=out_0[P * m:P * (m + 1), cols], in_=hy_t)
+
+        for m in range(MT + 1):
+            if m < MT:
+                cy_part(m)
+            if m >= 1:
+                hy_part(m - 1)

@@ -42,10 +42,7 @@ def tile_adaptivelstmcell_pb_kernel(
         wq = ctx.enter_context(tc.tile_pool(name="wq", bufs=2))
         abp = ctx.enter_context(tc.tile_pool(name="abp", bufs=2))
         work = ctx.enter_context(tc.tile_pool(name="work", bufs=3))
-        pst = ctx.enter_context(tc.psum_pool(name="pst", bufs=2))
-        psx = ctx.enter_context(tc.psum_pool(name="psx", bufs=2))
-        psa = ctx.enter_context(tc.psum_pool(name="psa", bufs=2))
-        psb = ctx.enter_context(tc.psum_pool(name="psb", bufs=2))
+        psum = ctx.enter_context(tc.psum_pool(name="psum", bufs=8))
         ctx.enter_context(tc.manual_schedule())
 
         ident_f = keep.tile([P, P], F32, name="ident_f")
@@ -80,7 +77,7 @@ def tile_adaptivelstmcell_pb_kernel(
             gw = grouped[:, g, :].bitcast(F32).rearrange("p (c u) -> p c u", u=2)
             banks = []
             for half in range(2):
-                pt = pst.tile([P, 2, 256], F32, name="pt", tag="t")
+                pt = psum.tile([P, 2, 256], F32, name="pt", tag="bank")
                 for bb in range(2):
                     for u in range(2):
                         nc.tensor.transpose(
@@ -140,7 +137,7 @@ def tile_adaptivelstmcell_pb_kernel(
             ch = chunks[c]
             banks = []
             for i in range(2):
-                pt = pst.tile([P, NT], BF16, name="pta", tag="t")
+                pt = psum.tile([P, NT], BF16, name="pta", tag="bank")
                 for b in range(4):
                     nc.tensor.transpose(pt[:, P * b:P * (b + 1)], ch["small"][i][:, b, :], ident_b[:])
                 banks.append(pt)
@@ -154,7 +151,7 @@ def tile_adaptivelstmcell_pb_kernel(
         def z_run(s):
             banks = []
             for raw in (zw_raw, zb_raw):
-                pt = pst.tile([P, BATCH], BF16, name="ptz", tag="t")
+                pt = psum.tile([P, BATCH], BF16, name="ptz", tag="bank")
                 for m in range(MT):
                     nc.tensor.transpose(pt[:, P * m:P * (m + 1)], raw[:, m, P * s:P * (s + 1)], ident_b[:])
                 banks.append(pt)
@@ -168,7 +165,7 @@ def tile_adaptivelstmcell_pb_kernel(
 
         def mm_alpha(t):
             c, m, q, j, s, rows = where(t)
-            alpha = psa.tile([P, NT], F32, name="alpha", tag="alpha")
+            alpha = psum.tile([P, NT], F32, name="alpha", tag="bank")
             nc.tensor.matmul(out=alpha[:], lhsT=zT[0][:, s, rows], rhs=chunks[c]["abT"][0][:], start=True, stop=True)
             al = work.tile([P, NT], F32, name="al", tag="al")
             nc.scalar.copy(out=al[:], in_=alpha[:])
@@ -177,10 +174,10 @@ def tile_adaptivelstmcell_pb_kernel(
         def mm_rest(t):
             c, m, q, j, s, rows = where(t)
             ch = chunks[c]
-            beta = psb.tile([P, NT], F32, name="beta", tag="beta")
+            beta = psum.tile([P, NT], F32, name="beta", tag="bank")
             nc.tensor.matmul(out=beta[:], lhsT=zT[1][:, s, rows], rhs=ch["abT"][1][:], start=True, stop=True)
             betas[t] = beta
-            xh = psx.tile([P, NT], F32, name="xh", tag="xh")
+            xh = psum.tile([P, NT], F32, name="xh", tag="bank")
             for g in range(PASSES):
                 nc.tensor.matmul_mx(
                     out=xh[:],
@@ -235,8 +232,8 @@ def tile_adaptivelstmcell_pb_kernel(
             else:
                 nc.gpsimd.tensor_scalar(out=reg, in0=reg, scalar1=nm, scalar2=rs, op0=ALU.add, op1=ALU.mult)
 
-        def turn(q, cb, pool, tag):
-            pt = pool.tile([P, BATCH], F32, name="ptn", tag=tag)
+        def turn(q, cb):
+            pt = psum.tile([P, BATCH], F32, name="ptn", tag="bank")
             k = cb % 4
             for m in range(MT):
                 nc.tensor.transpose(pt[:, P * m:P * (m + 1)], gbuf[q][cb // 4][:, m, P * k:P * (k + 1)], ident_f[:])
@@ -248,7 +245,7 @@ def tile_adaptivelstmcell_pb_kernel(
         stats = [None, None]
 
         def n_run(d, ks):
-            banks = [turn(0, 4 * d + k, pst, "t") for k in ks]
+            banks = [turn(0, 4 * d + k) for k in ks]
             for i, k in enumerate(ks):
                 cb = 4 * d + k
                 nc.scalar.activation(out=region(cb), in_=banks[i][:], func=ACT.Identity,
@@ -321,10 +318,10 @@ def tile_adaptivelstmcell_pb_kernel(
                     n_run(d - 1, (2, 3))
             if t == 3:
                 nc.vector.tensor_reduce(out=bpart[:], in_=bsm[:], axis=AX.X, op=ALU.add)
-                pb = pst.tile([P, 2], F32, name="pb", tag="t")
+                pb = psum.tile([P, 2], F32, name="pb", tag="bank")
                 nc.tensor.matmul(out=pb[:], lhsT=ones_f[:], rhs=bpart[:], start=True, stop=True)
                 nc.vector.tensor_copy(out=bsum[:], in_=pb[:])
-                pp = pst.tile([P, P], BF16, name="pp", tag="t")
+                pp = psum.tile([P, P], BF16, name="pp", tag="bank")
                 nc.tensor.transpose(pp[:], prm[:], ident_b[:])
                 nc.vector.tensor_copy(out=prmT[:], in_=pp[:])
                 nc.vector.tensor_tensor(out=lbT[:], in0=prmT[:, 64:96], in1=prmT[:, 96:128], op=ALU.add)
@@ -347,15 +344,11 @@ def tile_adaptivelstmcell_pb_kernel(
         n_run(CHUNKS - 1, (2, 3))
 
         stats[1] = finish_stats(sum_u[:, 1, :, :], sum_sq[:, 1, :, :], bsum[:, 1:2], GATES, "h")
-        turn_pools = ((pst, "t"), (psx, "xh"), (pst, "t"), (psx, "xh"))
-        turns = [0]
 
         def gates(cbs, funcs):
             banks = []
             for cb in cbs:
-                pool, tag = turn_pools[turns[0] % 4]
-                turns[0] += 1
-                banks.append(turn(1, cb, pool, tag))
+                banks.append(turn(1, cb))
             for i, cb in enumerate(cbs):
                 nc.vector.scalar_tensor_tensor(out=region(cb), in0=banks[i][:], scalar=prmT[:, 32 + cb:33 + cb],
                                                in1=region(cb), op0=ALU.mult, op1=ALU.add)
@@ -367,7 +360,7 @@ def tile_adaptivelstmcell_pb_kernel(
 
         def s_back(half):
             for m in range(MT):
-                sb = psa.tile([P, NT], F32, name="sb", tag="alpha")
+                sb = psum.tile([P, NT], F32, name="sb", tag="bank")
                 for k in range(4):
                     nc.tensor.transpose(sb[:, P * k:P * (k + 1)], region(16 + 4 * half + k)[:, P * m:P * (m + 1)],
                                         ident_f[:])
@@ -380,7 +373,7 @@ def tile_adaptivelstmcell_pb_kernel(
             norm_piece(d)
         for hb in range(8):
             gates((16 + hb, hb, 8 + hb), (ACT.Sigmoid, ACT.Sigmoid, ACT.Tanh))
-            cxT = psb.tile([P, BATCH], BF16, name="cxT", tag="beta")
+            cxT = psum.tile([P, BATCH], BF16, name="cxT", tag="bank")
             for m in range(MT):
                 nc.tensor.transpose(cxT[:, P * m:P * (m + 1)], cxt[:, m, P * hb:P * (hb + 1)], ident_b[:])
             nc.vector.tensor_tensor(out=region(16 + hb), in0=region(16 + hb), in1=cxT[:], op=ALU.mult)
@@ -417,8 +410,7 @@ def tile_adaptivelstmcell_pb_kernel(
         def hy_part(m):
             for half in range(2):
                 cols = slice(NT * half, NT * (half + 1))
-                pool, tag = ((psa, "alpha"), (psb, "beta"))[half]
-                ob = pool.tile([P, NT], F32, name="ob", tag=tag)
+                ob = psum.tile([P, NT], F32, name="ob", tag="bank")
                 for k in range(4):
                     nc.tensor.transpose(ob[:, P * k:P * (k + 1)], region(24 + 4 * half + k)[:, P * m:P * (m + 1)],
                                         ident_f[:])

@@ -174,9 +174,6 @@ def tile_adaptivelstmcell_pb_kernel(
         def mm_rest(t):
             c, m, q, j, s, rows = where(t)
             ch = chunks[c]
-            beta = psum.tile([P, NT], F32, name="beta", tag="bank")
-            nc.tensor.matmul(out=beta[:], lhsT=zT[1][:, s, rows], rhs=ch["abT"][1][:], start=True, stop=True)
-            betas[t] = beta
             xh = psum.tile([P, NT], F32, name="xh", tag="bank")
             for g in range(PASSES):
                 nc.tensor.matmul_mx(
@@ -188,6 +185,9 @@ def tile_adaptivelstmcell_pb_kernel(
                     start=(g == 0),
                     stop=(g == PASSES - 1),
                 )
+            beta = psum.tile([P, NT], F32, name="beta", tag="bank")
+            nc.tensor.matmul(out=beta[:], lhsT=zT[1][:, s, rows], rhs=ch["abT"][1][:], start=True, stop=True)
+            betas[t] = beta
             nc.vector.tensor_tensor(out=gbuf[q][j][:, m, :], in0=xh[:], in1=als[t][:], op=ALU.mult)
 
         def add_beta_bias(t):
@@ -264,7 +264,8 @@ def tile_adaptivelstmcell_pb_kernel(
         def norm_in_piece(i):
             normalise(2, 0, i % MT, i // MT, stats[0])
 
-        nc.sync.dma_start(out=x_raw, in_=rows_view(x))
+        for b in range(4):
+            nc.sync.dma_start(out=x_raw[:, b, :], in_=x[P * b:P * (b + 1), :])
         load_chunk(0)
         nc.sync.dma_start(out=zw_raw, in_=rows_view(zw.rearrange("b s a -> b (s a)")))
         nc.sync.dma_start(out=zb_raw, in_=rows_view(zb.rearrange("b s a -> b (s a)")))
@@ -294,13 +295,16 @@ def tile_adaptivelstmcell_pb_kernel(
                 load_chunk(c + 2)
             if live and m < 2 and more:
                 w_run(c + 1, m)
-            if live and m == 2 and more:
-                ab_run(c + 1)
+            if live and m == 2:
+                if more:
+                    ab_run(c + 1)
+                if d >= 1:
+                    n_run(d - 1, (0, 1))
             if live and m == 3:
                 if c < 7:
                     z_run(c + 1)
                 if d >= 1:
-                    n_run(d - 1, (0, 1))
+                    n_run(d - 1, (2, 3))
             if t + 1 < tiles:
                 mm_alpha(t + 1)
             if live:
@@ -314,8 +318,6 @@ def tile_adaptivelstmcell_pb_kernel(
                     k_run(hx_raw.bitcast(F32), 0, (0, 1))
                     k_run(hx_raw.bitcast(F32), 1, (0, 1))
                     quantise(xcodes[1], xscales[1])
-                if d >= 1:
-                    n_run(d - 1, (2, 3))
             if t == 3:
                 nc.vector.tensor_reduce(out=bpart[:], in_=bsm[:], axis=AX.X, op=ALU.add)
                 pb = psum.tile([P, 2], F32, name="pb", tag="bank")

@@ -95,10 +95,14 @@ def tile_adaptivelstmcell_pb_kernel(
                                   scales=scales[:].rearrange("p g c -> p (g c)"),
                                   in_=grouped[:].rearrange("p g c -> p (g c)"))
 
+        def quantise_pass(codes, scales, g):
+            nc.vector.quantize_mx(out=codes[:, g, :].bitcast(FP8X4), scales=scales[:, g, :], in_=grouped[:, g, :])
+
         def rows_view(src2d):
             return src2d.rearrange("(b r) k -> r b k", r=P)
 
         x_raw, zw_raw, zb_raw, hx_raw = [gbuf[1][4 + i][:].bitcast(BF16) for i in range(4)]
+        z_first = [keep.tile([P, MT, P], BF16, name="z_first%d" % i) for i in range(2)]
         chunks = {}
         als = {}
         betas = {}
@@ -133,7 +137,7 @@ def tile_adaptivelstmcell_pb_kernel(
             ch["scales"] = wq.tile([P, PASSES, NT], U8, name="wscales", tag="wscales", align_bytes=64)
             quantise(ch["codes"], ch["scales"])
 
-        def ab_run(c):
+        def ab_run(c, engines=AB_COPY):
             ch = chunks[c]
             banks = []
             for i in range(2):
@@ -144,19 +148,20 @@ def tile_adaptivelstmcell_pb_kernel(
             abT = []
             for i in range(2):
                 wT = abp.tile([P, NT], BF16, name="wT%d" % i, tag="wT%d" % i)
-                copy_on(AB_COPY[i], wT[:], banks[i][:])
+                copy_on(engines[i], wT[:], banks[i][:])
                 abT.append(wT)
             ch["abT"] = abT
 
-        def z_run(s):
+        def z_run(s, engines=Z_COPY):
             banks = []
-            for raw in (zw_raw, zb_raw):
+            for raw, first in ((zw_raw, z_first[0]), (zb_raw, z_first[1])):
                 pt = psum.tile([P, BATCH], BF16, name="ptz", tag="bank")
                 for m in range(MT):
-                    nc.tensor.transpose(pt[:, P * m:P * (m + 1)], raw[:, m, P * s:P * (s + 1)], ident_b[:])
+                    src = first[:, m, :] if s == 0 else raw[:, m, P * s:P * (s + 1)]
+                    nc.tensor.transpose(pt[:, P * m:P * (m + 1)], src, ident_b[:])
                 banks.append(pt)
             for i in range(2):
-                copy_on(Z_COPY[i], zT[i][:, s, :], banks[i][:])
+                copy_on(engines[i], zT[i][:, s, :], banks[i][:])
 
         def where(t):
             c, m = divmod(t, MT)
@@ -262,27 +267,28 @@ def tile_adaptivelstmcell_pb_kernel(
         stats_at = CHUNKS * MT + 2
 
         def norm_in_piece(i):
-            normalise(2, 0, i % MT, i // MT, stats[0])
+            normalise(1 if i < MT else 2, 0, i % MT, i // MT, stats[0])
 
         for b in range(4):
             nc.sync.dma_start(out=x_raw[:, b, :], in_=x[P * b:P * (b + 1), :])
         load_chunk(0)
+        nc.sync.dma_start(out=z_first[0][:], in_=rows_view(zw[:, 0, :]))
+        nc.sync.dma_start(out=z_first[1][:], in_=rows_view(zb[:, 0, :]))
+        load_chunk(1)
         nc.sync.dma_start(out=zw_raw, in_=rows_view(zw.rearrange("b s a -> b (s a)")))
         nc.sync.dma_start(out=zb_raw, in_=rows_view(zb.rearrange("b s a -> b (s a)")))
-        load_chunk(1)
         nc.sync.dma_start(out=bsm[:, 0, :], in_=b_ih.rearrange("(p c) -> p c", c=32))
         nc.sync.dma_start(out=bsm[:, 1, :], in_=b_hh.rearrange("(p c) -> p c", c=32))
         for i, vec in enumerate((ln_i_w, ln_h_w, ln_i_b, ln_h_b)):
             nc.sync.dma_start(out=prm[32 * i:32 * (i + 1), :], in_=vec.rearrange("(c p) -> c p", p=P))
-        nc.sync.dma_start(out=hx_raw, in_=rows_view(hx))
 
         k_run(x_raw.bitcast(F32), 0, (0, 1))
         k_run(x_raw.bitcast(F32), 1, (0, 1))
-        z_run(0)
         quantise(xcodes[0], xscales[0])
         w_run(0, 0)
         w_run(0, 1)
         ab_run(0)
+        z_run(0, (1, 1))
         w_quantise(0)
         mm_alpha(0)
 
@@ -293,6 +299,8 @@ def tile_adaptivelstmcell_pb_kernel(
             live = t < tiles
             if live and m == 0 and c + 2 < 2 * CHUNKS:
                 load_chunk(c + 2)
+            if t == MT:
+                nc.sync.dma_start(out=hx_raw, in_=rows_view(hx))
             if live and m < 2 and more:
                 w_run(c + 1, m)
             if live and m == 2:
@@ -320,11 +328,13 @@ def tile_adaptivelstmcell_pb_kernel(
                     quantise(xcodes[1], xscales[1])
             if t == 3:
                 nc.vector.tensor_reduce(out=bpart[:], in_=bsm[:], axis=AX.X, op=ALU.add)
+            if t == 5:
                 pb = psum.tile([P, 2], F32, name="pb", tag="bank")
                 nc.tensor.matmul(out=pb[:], lhsT=ones_f[:], rhs=bpart[:], start=True, stop=True)
-                nc.vector.tensor_copy(out=bsum[:], in_=pb[:])
                 pp = psum.tile([P, P], BF16, name="pp", tag="bank")
                 nc.tensor.transpose(pp[:], prm[:], ident_b[:])
+            if t == 6:
+                nc.vector.tensor_copy(out=bsum[:], in_=pb[:])
                 nc.vector.tensor_copy(out=prmT[:], in_=pp[:])
                 nc.vector.tensor_tensor(out=lbT[:], in0=prmT[:, 64:96], in1=prmT[:, 96:128], op=ALU.add)
             if t >= 3:

@@ -200,7 +200,7 @@ def tile_adaptivelstmcell_pb_kernel(
             dst = gbuf[q][j][:, m, :]
             nc.vector.scalar_tensor_tensor(out=dst, in0=dst, scalar=1.0, in1=betas[t][:], op0=ALU.mult,
                                            op1=ALU.add, accum_out=sum_u[:, q, m, j:j + 1])
-            nc.gpsimd.tensor_tensor(out=dst, in0=dst, in1=chunks[c]["bias"], op=ALU.add)
+            (nc.vector if t >= tiles - 2 else nc.gpsimd).tensor_tensor(out=dst, in0=dst, in1=chunks[c]["bias"], op=ALU.add)
 
         def square(t):
             c, m, q, j, s, rows = where(t)
@@ -267,7 +267,7 @@ def tile_adaptivelstmcell_pb_kernel(
         stats_at = CHUNKS * MT + 2
 
         def norm_in_piece(i):
-            normalise(1 if i < MT else 2, 0, i % MT, i // MT, stats[0])
+            normalise(1 if i >= 24 else 2, 0, i % MT, i // MT, stats[0])
 
         for b in range(4):
             nc.sync.dma_start(out=x_raw[:, b, :], in_=x[P * b:P * (b + 1), :])
@@ -301,25 +301,26 @@ def tile_adaptivelstmcell_pb_kernel(
                 load_chunk(c + 2)
             if t == MT:
                 nc.sync.dma_start(out=hx_raw, in_=rows_view(hx))
-            if live and m < 2 and more:
+            if live and c == 0 and m < 2:
                 w_run(c + 1, m)
+            if live and c > 0 and m == 0 and more:
+                w_run(c + 1, 0)
+                w_run(c + 1, 1)
             if live and m == 2:
                 if more:
                     ab_run(c + 1)
-                if d >= 1:
-                    n_run(d - 1, (0, 1))
-            if live and m == 3:
                 if c < 7:
                     z_run(c + 1)
-                if d >= 1:
-                    n_run(d - 1, (2, 3))
+                if d >= 2:
+                    n_run(d - 2, (0, 1))
+                    n_run(d - 2, (2, 3))
             if t + 1 < tiles:
                 mm_alpha(t + 1)
             if live:
                 mm_rest(t)
             if t >= 1:
                 add_beta_bias(t - 1)
-            if live and m == 2 and more:
+            if live and m == (2 if c == 0 else 1) and more:
                 w_quantise(c + 1)
             if live and m == 3:
                 if c == 6:
@@ -341,18 +342,20 @@ def tile_adaptivelstmcell_pb_kernel(
                 square(t - 3)
             if t == stats_at:
                 stats[0] = finish_stats(sum_u[:, 0, :, :], sum_sq[:, 0, :, :], bsum[:, 0:1], GATES, "i")
-            if stats_at < t <= stats_at + 4:
-                norm_in_piece(2 * (t - stats_at - 1))
-                norm_in_piece(2 * (t - stats_at - 1) + 1)
-            if t > stats_at + 4 and t - stats_at + 3 < 32:
-                norm_in_piece(t - stats_at + 3)
+            if t > stats_at:
+                norm_in_piece(t - stats_at - 1)
+            if t == tiles:
+                norm_in_piece(30)
+                norm_in_piece(31)
         cxt = rawp.tile([P, 4, K], BF16, name="raw", tag="raw")
         nc.sync.dma_start(out=cxt[:], in_=rows_view(cx))
         nc.sync.dma_start(out=wc[:], in_=ln_c_w.partition_broadcast(P))
         nc.sync.dma_start(out=bc[:], in_=ln_c_b.partition_broadcast(P))
-        n_run(CHUNKS - 1, (0, 1))
+        n_run(CHUNKS - 2, (0, 1))
+        n_run(CHUNKS - 2, (2, 3))
         for t in range(tiles + 1, tiles + 3):
             square(t - 3)
+        n_run(CHUNKS - 1, (0, 1))
         n_run(CHUNKS - 1, (2, 3))
 
         stats[1] = finish_stats(sum_u[:, 1, :, :], sum_sq[:, 1, :, :], bsum[:, 1:2], GATES, "h")

@@ -208,12 +208,12 @@ def tile_adaptivelstmcell_pb_kernel(
             nc.scalar.activation(out=junk[:], in_=gbuf[q][j][:, m, :], func=ACT.Square,
                                  accum_out=sum_sq[:, q, m, j:j + 1])
 
-        def finish_stats(sums, squares, extra, count, label):
-            s1 = keep.tile([P, MT], F32, name="s1" + label)
-            s2 = keep.tile([P, MT], F32, name="s2" + label)
-            negmean = keep.tile([P, MT], F32, name="negmean" + label)
-            rstd = keep.tile([P, MT], F32, name="rstd" + label)
-            shift = keep.tile([P, MT], F32, name="shift" + label)
+        def finish_stats(sums, squares, extra, count, label, width=MT):
+            s1 = keep.tile([P, width], F32, name="s1" + label)
+            s2 = keep.tile([P, width], F32, name="s2" + label)
+            negmean = keep.tile([P, width], F32, name="negmean" + label)
+            rstd = keep.tile([P, width], F32, name="rstd" + label)
+            shift = keep.tile([P, width], F32, name="shift" + label)
             nc.vector.tensor_reduce(out=s1[:], in_=sums, axis=AX.X, op=ALU.add)
             nc.vector.tensor_reduce(out=s2[:], in_=squares, axis=AX.X, op=ALU.add)
             nc.vector.tensor_scalar(out=negmean[:], in0=s1[:], scalar1=extra, scalar2=-1.0 / count,
@@ -222,7 +222,7 @@ def tile_adaptivelstmcell_pb_kernel(
             nc.vector.scalar_tensor_tensor(out=s2[:], in0=s2[:], scalar=1.0 / count, in1=s1[:],
                                            op0=ALU.mult, op1=ALU.subtract)
             nc.vector.tensor_scalar(out=s2[:], in0=s2[:], scalar1=0.0, scalar2=EPS, op0=ALU.max, op1=ALU.add)
-            nc.gpsimd.tensor_tensor(out=rstd[:], in0=s2[:], in1=neg_half[:], op=ALU.pow)
+            nc.gpsimd.tensor_tensor(out=rstd[:], in0=s2[:], in1=neg_half[:, 0:width], op=ALU.pow)
             nc.gpsimd.tensor_tensor(out=shift[:], in0=negmean[:], in1=rstd[:], op=ALU.mult)
             return negmean, rstd, shift
 
@@ -373,51 +373,37 @@ def tile_adaptivelstmcell_pb_kernel(
             for m in range(MT):
                 normalise(TAIL_NORM[m], 1, m, d, stats[1])
 
-        def s_back(half):
-            for m in range(MT):
-                sb = psum.tile([P, NT], F32, name="sb", tag="bank")
-                for k in range(4):
-                    nc.tensor.transpose(sb[:, P * k:P * (k + 1)], region(16 + 4 * half + k)[:, P * m:P * (m + 1)],
-                                        ident_f[:])
+        def s_back_m(half, m, copy_eng):
+            sb = psum.tile([P, NT], F32, name="sb", tag="bank")
+            for k in range(4):
+                nc.tensor.transpose(sb[:, P * k:P * (k + 1)], region(16 + 4 * half + k)[:, P * m:P * (m + 1)],
+                                    ident_f[:])
+            if copy_eng == 0:
                 nc.scalar.activation(out=gbuf[1][half][:, m, :], in_=sb[:], func=ACT.Identity,
                                      accum_out=csum[:, m, half:half + 1])
-                junk = work.tile([P, NT], BF16, name="junk", tag="junk")
-                nc.scalar.activation(out=junk[:], in_=sb[:], func=ACT.Square, accum_out=csq[:, m, half:half + 1])
+            else:
+                nc.vector.tensor_scalar(out=gbuf[1][half][:, m, :], in0=sb[:], scalar1=1.0, scalar2=0.0, op0=ALU.mult,
+                                        op1=ALU.add, accum_out=csum[:, m, half:half + 1])
+            junk = work.tile([P, NT], BF16, name="junk", tag="junk")
+            nc.scalar.activation(out=junk[:], in_=sb[:], func=ACT.Square, accum_out=csq[:, m, half:half + 1])
 
-        for d in (4, 0, 2):
-            norm_piece(d)
-        for hb in range(8):
-            gates((16 + hb, hb, 8 + hb), (ACT.Sigmoid, ACT.Sigmoid, ACT.Tanh))
-            cxT = psum.tile([P, BATCH], BF16, name="cxT", tag="bank")
-            for m in range(MT):
-                nc.tensor.transpose(cxT[:, P * m:P * (m + 1)], cxt[:, m, P * hb:P * (hb + 1)], ident_b[:])
-            nc.vector.tensor_tensor(out=region(16 + hb), in0=region(16 + hb), in1=cxT[:], op=ALU.mult)
-            nc.gpsimd.tensor_tensor(out=region(hb), in0=region(hb), in1=region(8 + hb), op=ALU.mult)
-            nc.gpsimd.tensor_tensor(out=region(16 + hb), in0=region(16 + hb), in1=region(hb), op=ALU.add)
-            if hb == 1:
-                for d in (5, 1, 3):
-                    norm_piece(d)
-            if hb == 4:
-                for d in (6, 7):
-                    norm_piece(d)
-            if hb == 5:
-                s_back(0)
-        gates((24, 25, 26), (ACT.Sigmoid, ACT.Sigmoid, ACT.Sigmoid))
-        s_back(1)
-        gates((27, 28, 29), (ACT.Sigmoid, ACT.Sigmoid, ACT.Sigmoid))
-        gates((30, 31), (ACT.Sigmoid, ACT.Sigmoid))
-        st_c = finish_stats(csum[:], csq[:], 0.0, H, "c")
+        st_c = [None, None]
+
+        def stats_c(p):
+            st_c[p] = finish_stats(csum[:, 2 * p:2 * p + 2, :], csq[:, 2 * p:2 * p + 2, :], 0.0, H, "c%d" % p, 2)
 
         def cy_part(m):
+            st = st_c[m // 2]
+            col = m % 2
             for half in range(2):
                 cols = slice(NT * half, NT * (half + 1))
                 s_t = gbuf[1][half][:, m, :]
-                nc.vector.scalar_tensor_tensor(out=s_t, in0=s_t, scalar=st_c[0][:, m:m + 1], in1=wc[:, cols],
+                nc.vector.scalar_tensor_tensor(out=s_t, in0=s_t, scalar=st[0][:, col:col + 1], in1=wc[:, cols],
                                                op0=ALU.add, op1=ALU.mult)
             for half in range(2):
                 cols = slice(NT * half, NT * (half + 1))
                 cy_t = gbuf[1][2 + half][:, m, :]
-                nc.vector.scalar_tensor_tensor(out=cy_t, in0=gbuf[1][half][:, m, :], scalar=st_c[1][:, m:m + 1],
+                nc.vector.scalar_tensor_tensor(out=cy_t, in0=gbuf[1][half][:, m, :], scalar=st[1][:, col:col + 1],
                                                in1=bc[:, cols], op0=ALU.mult, op1=ALU.add)
                 nc.sync.dma_start(out=out_1[P * m:P * (m + 1), cols], in_=cy_t)
                 nc.scalar.activation(out=gbuf[1][4 + half][:, m, :], in_=cy_t, func=ACT.Tanh)
@@ -433,8 +419,40 @@ def tile_adaptivelstmcell_pb_kernel(
                 nc.vector.tensor_tensor(out=hy_t, in0=gbuf[1][4 + half][:, m, :], in1=ob[:], op=ALU.mult)
                 nc.sync.dma_start(out=out_0[P * m:P * (m + 1), cols], in_=hy_t)
 
-        for m in range(MT + 1):
-            if m < MT:
-                cy_part(m)
-            if m >= 1:
-                hy_part(m - 1)
+        def cell(hb):
+            gates((16 + hb, hb, 8 + hb), (ACT.Sigmoid, ACT.Sigmoid, ACT.Tanh))
+            cxT = psum.tile([P, BATCH], BF16, name="cxT", tag="bank")
+            for m in range(MT):
+                nc.tensor.transpose(cxT[:, P * m:P * (m + 1)], cxt[:, m, P * hb:P * (hb + 1)], ident_b[:])
+            nc.vector.tensor_tensor(out=region(16 + hb), in0=region(16 + hb), in1=cxT[:], op=ALU.mult)
+            nc.gpsimd.tensor_tensor(out=region(hb), in0=region(hb), in1=region(8 + hb), op=ALU.mult)
+            nc.gpsimd.tensor_tensor(out=region(16 + hb), in0=region(16 + hb), in1=region(hb), op=ALU.add)
+
+        SIG = ACT.Sigmoid
+        for d in (4, 0, 2, 5, 1, 3, 6, 7):
+            norm_piece(d)
+        for hb in range(8):
+            cell(hb)
+            if hb == 5:
+                s_back_m(0, 0, 0)
+                s_back_m(0, 1, 0)
+            if hb == 6:
+                s_back_m(0, 2, 0)
+                s_back_m(0, 3, 0)
+        gates((24, 25, 26), (SIG, SIG, SIG))
+        gates((27, 28), (SIG, SIG))
+        s_back_m(1, 0, 1)
+        s_back_m(1, 1, 1)
+        stats_c(0)
+        s_back_m(1, 2, 1)
+        s_back_m(1, 3, 1)
+        gates((29, 30, 31), (SIG, SIG, SIG))
+        cy_part(0)
+        stats_c(1)
+        cy_part(1)
+        hy_part(0)
+        cy_part(2)
+        hy_part(1)
+        cy_part(3)
+        hy_part(2)
+        hy_part(3)

@@ -53,6 +53,8 @@ def tile_adaptivelstmcell_pb_kernel(
         nc.vector.memset(ones_f[:], 1.0)
         neg_half = keep.tile([P, MT], F32, name="neg_half")
         nc.vector.memset(neg_half[:], -0.5)
+        warm = keep.tile([P, 1], F32, name="warm")
+        nc.scalar.activation(out=warm[:], in_=neg_half[:, 0:1], func=ACT.Sigmoid)
 
         xcodes = [keep.tile([P, PASSES, BATCH], U32, name="xcodes%d" % q, align_bytes=64) for q in range(2)]
         xscales = [keep.tile([P, PASSES, BATCH], U8, name="xscales%d" % q, align_bytes=64) for q in range(2)]
@@ -342,23 +344,22 @@ def tile_adaptivelstmcell_pb_kernel(
                 square(t - 3)
             if t == stats_at:
                 stats[0] = finish_stats(sum_u[:, 0, :, :], sum_sq[:, 0, :, :], bsum[:, 0:1], GATES, "i")
-            if t > stats_at:
+            if stats_at < t < tiles - 1:
                 norm_in_piece(t - stats_at - 1)
-            if t == tiles:
-                norm_in_piece(30)
-                norm_in_piece(31)
         cxt = rawp.tile([P, 4, K], BF16, name="raw", tag="raw")
         nc.sync.dma_start(out=cxt[:], in_=rows_view(cx))
         nc.sync.dma_start(out=wc[:], in_=ln_c_w.partition_broadcast(P))
         nc.sync.dma_start(out=bc[:], in_=ln_c_b.partition_broadcast(P))
-        n_run(CHUNKS - 2, (0, 1))
-        n_run(CHUNKS - 2, (2, 3))
         for t in range(tiles + 1, tiles + 3):
             square(t - 3)
-        n_run(CHUNKS - 1, (0, 1))
-        n_run(CHUNKS - 1, (2, 3))
 
         stats[1] = finish_stats(sum_u[:, 1, :, :], sum_sq[:, 1, :, :], bsum[:, 1:2], GATES, "h")
+        for i in range(tiles - 2 - stats_at, 32):
+            norm_in_piece(i)
+        n_run(CHUNKS - 2, (0, 1))
+        n_run(CHUNKS - 2, (2, 3))
+        n_run(CHUNKS - 1, (0, 1))
+        n_run(CHUNKS - 1, (2, 3))
 
         def gates(cbs, funcs):
             banks = []
@@ -419,12 +420,17 @@ def tile_adaptivelstmcell_pb_kernel(
                 nc.vector.tensor_tensor(out=hy_t, in0=gbuf[1][4 + half][:, m, :], in1=ob[:], op=ALU.mult)
                 nc.sync.dma_start(out=out_0[P * m:P * (m + 1), cols], in_=hy_t)
 
-        def cell(hb):
+        cx_banks = {}
+
+        def cell_gates(hb):
             gates((16 + hb, hb, 8 + hb), (ACT.Sigmoid, ACT.Sigmoid, ACT.Tanh))
             cxT = psum.tile([P, BATCH], BF16, name="cxT", tag="bank")
             for m in range(MT):
                 nc.tensor.transpose(cxT[:, P * m:P * (m + 1)], cxt[:, m, P * hb:P * (hb + 1)], ident_b[:])
-            nc.vector.tensor_tensor(out=region(16 + hb), in0=region(16 + hb), in1=cxT[:], op=ALU.mult)
+            cx_banks[hb] = cxT
+
+        def cell_sum(hb):
+            nc.vector.tensor_tensor(out=region(16 + hb), in0=region(16 + hb), in1=cx_banks[hb][:], op=ALU.mult)
             nc.gpsimd.tensor_tensor(out=region(hb), in0=region(hb), in1=region(8 + hb), op=ALU.mult)
             nc.gpsimd.tensor_tensor(out=region(16 + hb), in0=region(16 + hb), in1=region(hb), op=ALU.add)
 
@@ -432,21 +438,24 @@ def tile_adaptivelstmcell_pb_kernel(
         for d in (4, 0, 2, 5, 1, 3, 6, 7):
             norm_piece(d)
         for hb in range(8):
-            cell(hb)
-            if hb == 5:
+            cell_gates(hb)
+            if hb >= 1:
+                cell_sum(hb - 1)
+            if hb == 6:
                 s_back_m(0, 0, 0)
                 s_back_m(0, 1, 0)
-            if hb == 6:
+            if hb == 7:
                 s_back_m(0, 2, 0)
                 s_back_m(0, 3, 0)
         gates((24, 25, 26), (SIG, SIG, SIG))
+        cell_sum(7)
         gates((27, 28), (SIG, SIG))
+        gates((29, 30, 31), (SIG, SIG, SIG))
         s_back_m(1, 0, 1)
         s_back_m(1, 1, 1)
-        stats_c(0)
         s_back_m(1, 2, 1)
         s_back_m(1, 3, 1)
-        gates((29, 30, 31), (SIG, SIG, SIG))
+        stats_c(0)
         cy_part(0)
         stats_c(1)
         cy_part(1)

@@ -115,7 +115,11 @@ def tile_adaptivelstmcell_pb_kernel(
             h0 = NT * (j % 2)
             n0 = NT * j
             raw = rawp.tile([P, 4, K], BF16, name="raw", tag="raw")
-            nc.sync.dma_start(out=raw[:], in_=rows_view((w_ih, w_hh)[q][n0:n0 + NT, :]))
+            if c == 0:
+                for b in range(4):
+                    nc.sync.dma_start(out=raw[:, b, :], in_=w_ih[P * b:P * (b + 1), :])
+            else:
+                nc.sync.dma_start(out=raw[:], in_=rows_view((w_ih, w_hh)[q][n0:n0 + NT, :]))
             small = []
             for i, wsrc in enumerate((norm_alpha_w, bias_beta_w)):
                 sraw = abp.tile([P, 4, P], BF16, name="sraw%d" % i, tag="sraw%d" % i)
@@ -269,7 +273,7 @@ def tile_adaptivelstmcell_pb_kernel(
         stats_at = CHUNKS * MT + 2
 
         def norm_in_piece(i):
-            normalise(1 if i >= 24 else 2, 0, i % MT, i // MT, stats[0])
+            normalise(1 if i >= 12 else 2, 0, i % MT, i // MT, stats[0])
 
         for b in range(4):
             nc.sync.dma_start(out=x_raw[:, b, :], in_=x[P * b:P * (b + 1), :])
@@ -286,11 +290,12 @@ def tile_adaptivelstmcell_pb_kernel(
 
         k_run(x_raw.bitcast(F32), 0, (0, 1))
         k_run(x_raw.bitcast(F32), 1, (0, 1))
-        quantise(xcodes[0], xscales[0])
+        quantise_pass(xcodes[0], xscales[0], 0)
+        quantise_pass(xcodes[0], xscales[0], 1)
         w_run(0, 0)
         w_run(0, 1)
         ab_run(0)
-        z_run(0, (1, 1))
+        z_run(0, (1, 0))
         w_quantise(0)
         mm_alpha(0)
 

@@ -27,6 +27,7 @@ W_COPY = (((0, 1), (0, 1)), ((1, 0), (1, 1)))
 AB_COPY = (0, 0)
 Z_COPY = (0, 0)
 TAIL_NORM = (1, 1, 0, 2)
+PE_BIAS = (3,)
 
 FLOPS = 2 * 2 * BATCH * GATES * K + 16 * 2 * BATCH * H * 128
 
@@ -53,6 +54,8 @@ def tile_adaptivelstmcell_pb_kernel(
         nc.vector.memset(ones_f[:], 1.0)
         neg_half = keep.tile([P, MT], F32, name="neg_half")
         nc.vector.memset(neg_half[:], -0.5)
+        brow = keep.tile([P, NT], BF16, name="brow")
+        nc.vector.memset(brow[:], 0.0)
         warm = keep.tile([P, 1], F32, name="warm")
         nc.scalar.activation(out=warm[:], in_=neg_half[:, 0:1], func=ACT.Sigmoid)
 
@@ -197,7 +200,11 @@ def tile_adaptivelstmcell_pb_kernel(
                     stop=(g == PASSES - 1),
                 )
             beta = psum.tile([P, NT], F32, name="beta", tag="bank")
-            nc.tensor.matmul(out=beta[:], lhsT=zT[1][:, s, rows], rhs=ch["abT"][1][:], start=True, stop=True)
+            on_pe = m in PE_BIAS
+            nc.tensor.matmul(out=beta[:], lhsT=zT[1][:, s, rows], rhs=ch["abT"][1][:], start=True, stop=not on_pe)
+            if on_pe:
+                nc.tensor.matmul(out=beta[:], lhsT=ident_b[:, c:c + 1].to_broadcast([P, P]), rhs=brow[:],
+                                 start=False, stop=True)
             betas[t] = beta
             nc.vector.tensor_tensor(out=gbuf[q][j][:, m, :], in0=xh[:], in1=als[t][:], op=ALU.mult)
 
@@ -206,7 +213,9 @@ def tile_adaptivelstmcell_pb_kernel(
             dst = gbuf[q][j][:, m, :]
             nc.vector.scalar_tensor_tensor(out=dst, in0=dst, scalar=1.0, in1=betas[t][:], op0=ALU.mult,
                                            op1=ALU.add, accum_out=sum_u[:, q, m, j:j + 1])
-            (nc.vector if t >= tiles - 2 else nc.gpsimd).tensor_tensor(out=dst, in0=dst, in1=chunks[c]["bias"], op=ALU.add)
+            if m not in PE_BIAS:
+                (nc.vector if t >= tiles - 2 else nc.gpsimd).tensor_tensor(out=dst, in0=dst, in1=chunks[c]["bias"],
+                                                                           op=ALU.add)
 
         def square(t):
             c, m, q, j, s, rows = where(t)
@@ -222,8 +231,12 @@ def tile_adaptivelstmcell_pb_kernel(
             shift = keep.tile([P, width], F32, name="shift" + label)
             nc.vector.tensor_reduce(out=s1[:], in_=sums, axis=AX.X, op=ALU.add)
             nc.vector.tensor_reduce(out=s2[:], in_=squares, axis=AX.X, op=ALU.add)
-            nc.vector.tensor_scalar(out=negmean[:], in0=s1[:], scalar1=extra, scalar2=-1.0 / count,
-                                    op0=ALU.add, op1=ALU.mult)
+            without = width if label[0] == "c" else min(PE_BIAS)
+            nc.vector.tensor_scalar(out=negmean[:, 0:without], in0=s1[:, 0:without], scalar1=extra,
+                                    scalar2=-1.0 / count, op0=ALU.add, op1=ALU.mult)
+            if without < width:
+                nc.vector.tensor_scalar(out=negmean[:, without:width], in0=s1[:, without:width], scalar1=0.0,
+                                        scalar2=-1.0 / count, op0=ALU.add, op1=ALU.mult)
             nc.vector.tensor_tensor(out=s1[:], in0=negmean[:], in1=negmean[:], op=ALU.mult)
             nc.vector.scalar_tensor_tensor(out=s2[:], in0=s2[:], scalar=1.0 / count, in1=s1[:],
                                            op0=ALU.mult, op1=ALU.subtract)
@@ -273,11 +286,13 @@ def tile_adaptivelstmcell_pb_kernel(
         stats_at = CHUNKS * MT + 2
 
         def norm_in_piece(i):
-            normalise(1 if i >= 12 else 2, 0, i % MT, i // MT, stats[0])
+            normalise(1 if i >= 4 else 2, 0, i % MT, i // MT, stats[0])
 
         for b in range(4):
             nc.sync.dma_start(out=x_raw[:, b, :], in_=x[P * b:P * (b + 1), :])
         load_chunk(0)
+        nc.sync.dma_start(out=brow[0:CHUNKS, :], in_=b_ih.rearrange("(c n) -> c n", n=NT))
+        nc.sync.dma_start(out=brow[CHUNKS:2 * CHUNKS, :], in_=b_hh.rearrange("(c n) -> c n", n=NT))
         nc.sync.dma_start(out=z_first[0][:], in_=rows_view(zw[:, 0, :]))
         nc.sync.dma_start(out=z_first[1][:], in_=rows_view(zb[:, 0, :]))
         load_chunk(1)

@@ -230,7 +230,6 @@ def tile_adaptivelstmcell_pb_kernel(
             rstd = keep.tile([P, width], F32, name="rstd" + label)
             shift = keep.tile([P, width], F32, name="shift" + label)
             nc.vector.tensor_reduce(out=s1[:], in_=sums, axis=AX.X, op=ALU.add)
-            nc.vector.tensor_reduce(out=s2[:], in_=squares, axis=AX.X, op=ALU.add)
             without = width if label[0] == "c" else min(PE_BIAS)
             nc.vector.tensor_scalar(out=negmean[:, 0:without], in0=s1[:, 0:without], scalar1=extra,
                                     scalar2=-1.0 / count, op0=ALU.add, op1=ALU.mult)
@@ -238,6 +237,7 @@ def tile_adaptivelstmcell_pb_kernel(
                 nc.vector.tensor_scalar(out=negmean[:, without:width], in0=s1[:, without:width], scalar1=0.0,
                                         scalar2=-1.0 / count, op0=ALU.add, op1=ALU.mult)
             nc.vector.tensor_tensor(out=s1[:], in0=negmean[:], in1=negmean[:], op=ALU.mult)
+            nc.vector.tensor_reduce(out=s2[:], in_=squares, axis=AX.X, op=ALU.add)
             nc.vector.scalar_tensor_tensor(out=s2[:], in0=s2[:], scalar=1.0 / count, in1=s1[:],
                                            op0=ALU.mult, op1=ALU.subtract)
             nc.vector.tensor_scalar(out=s2[:], in0=s2[:], scalar1=0.0, scalar2=EPS, op0=ALU.max, op1=ALU.add)
@@ -397,8 +397,9 @@ def tile_adaptivelstmcell_pb_kernel(
         def s_back_m(half, m, copy_eng):
             sb = psum.tile([P, NT], F32, name="sb", tag="bank")
             for k in range(4):
-                nc.tensor.transpose(sb[:, P * k:P * (k + 1)], region(16 + 4 * half + k)[:, P * m:P * (m + 1)],
-                                    ident_f[:])
+                for i, cb in enumerate((16 + 4 * half + k, 4 * half + k)):
+                    nc.tensor.matmul(out=sb[:, P * k:P * (k + 1)], lhsT=region(cb)[:, P * m:P * (m + 1)],
+                                     rhs=ident_f[:], is_transpose=True, start=(i == 0), stop=(i == 1))
             if copy_eng == 0:
                 nc.scalar.activation(out=gbuf[1][half][:, m, :], in_=sb[:], func=ACT.Identity,
                                      accum_out=csum[:, m, half:half + 1])
@@ -452,7 +453,6 @@ def tile_adaptivelstmcell_pb_kernel(
         def cell_sum(hb):
             nc.vector.tensor_tensor(out=region(16 + hb), in0=region(16 + hb), in1=cx_banks[hb][:], op=ALU.mult)
             nc.gpsimd.tensor_tensor(out=region(hb), in0=region(hb), in1=region(8 + hb), op=ALU.mult)
-            nc.gpsimd.tensor_tensor(out=region(16 + hb), in0=region(16 + hb), in1=region(hb), op=ALU.add)
 
         SIG = ACT.Sigmoid
         for d in (4, 0, 2, 5, 1, 3, 6, 7):

@@ -112,29 +112,35 @@ def tile_adaptivelstmcell_pb_kernel(
         als = {}
         betas = {}
 
-        def load_chunk(c):
+        bias_pairs = {}
+
+        def load_bias(c):
             q, j = divmod(c, CHUNKS)
-            s = 4 * q + j // 2
-            h0 = NT * (j % 2)
-            n0 = NT * j
+            bias2 = abp.tile([P, 2, NT], BF16, name="bias", tag="bias", bufs=3)
+            nc.sync.dma_start(out=bias2[:].rearrange("p a n -> p (a n)"),
+                              in_=(b_ih, b_hh)[q][NT * j:NT * (j + 2)].partition_broadcast(P))
+            bias_pairs[c // 2] = bias2
+
+        def load_raw(c):
+            q, j = divmod(c, CHUNKS)
             raw = rawp.tile([P, 4, K], BF16, name="raw", tag="raw")
             if c == 0:
                 for b in range(4):
                     nc.sync.dma_start(out=raw[:, b, :], in_=w_ih[P * b:P * (b + 1), :])
             else:
-                nc.sync.dma_start(out=raw[:], in_=rows_view((w_ih, w_hh)[q][n0:n0 + NT, :]))
+                nc.sync.dma_start(out=raw[:], in_=rows_view((w_ih, w_hh)[q][NT * j:NT * (j + 1), :]))
+            chunks[c] = {"raw": raw, "q": q}
+
+        def load_small(c):
+            q, j = divmod(c, CHUNKS)
+            s = 4 * q + j // 2
+            h0 = NT * (j % 2)
             small = []
             for i, wsrc in enumerate((norm_alpha_w, bias_beta_w)):
                 sraw = abp.tile([P, 4, P], BF16, name="sraw%d" % i, tag="sraw%d" % i)
                 nc.sync.dma_start(out=sraw[:], in_=wsrc[s, h0:h0 + NT, :].rearrange("(b r) a -> r b a", r=P))
                 small.append(sraw)
-            if j % 2 == 0:
-                bias2 = abp.tile([P, 2, NT], BF16, name="bias", tag="bias", bufs=3)
-                nc.sync.dma_start(out=bias2[:].rearrange("p a n -> p (a n)"),
-                                  in_=(b_ih, b_hh)[q][n0:n0 + 2 * NT].partition_broadcast(P))
-            else:
-                bias2 = chunks[c - 1]["bias2"]
-            chunks[c] = {"raw": raw, "small": small, "bias2": bias2, "bias": bias2[:, j % 2, :], "q": q}
+            chunks[c]["small"] = small
 
         def w_run(c, g):
             ch = chunks[c]
@@ -214,7 +220,7 @@ def tile_adaptivelstmcell_pb_kernel(
             nc.vector.scalar_tensor_tensor(out=dst, in0=dst, scalar=1.0, in1=betas[t][:], op0=ALU.mult,
                                            op1=ALU.add, accum_out=sum_u[:, q, m, j:j + 1])
             if m not in PE_BIAS:
-                (nc.vector if t >= tiles - 2 else nc.gpsimd).tensor_tensor(out=dst, in0=dst, in1=chunks[c]["bias"],
+                (nc.vector if t >= tiles - 2 else nc.gpsimd).tensor_tensor(out=dst, in0=dst, in1=bias_pairs[c // 2][:, c % 2, :],
                                                                            op=ALU.add)
 
         def square(t):
@@ -290,18 +296,22 @@ def tile_adaptivelstmcell_pb_kernel(
 
         for b in range(4):
             nc.sync.dma_start(out=x_raw[:, b, :], in_=x[P * b:P * (b + 1), :])
-        load_chunk(0)
-        nc.sync.dma_start(out=brow[0:CHUNKS, :], in_=b_ih.rearrange("(c n) -> c n", n=NT))
-        nc.sync.dma_start(out=brow[CHUNKS:2 * CHUNKS, :], in_=b_hh.rearrange("(c n) -> c n", n=NT))
+        load_raw(0)
+        load_small(0)
         nc.sync.dma_start(out=z_first[0][:], in_=rows_view(zw[:, 0, :]))
         nc.sync.dma_start(out=z_first[1][:], in_=rows_view(zb[:, 0, :]))
-        load_chunk(1)
-        nc.sync.dma_start(out=zw_raw, in_=rows_view(zw.rearrange("b s a -> b (s a)")))
-        nc.sync.dma_start(out=zb_raw, in_=rows_view(zb.rearrange("b s a -> b (s a)")))
+        load_raw(1)
+        load_small(1)
         nc.sync.dma_start(out=bsm[:, 0, :], in_=b_ih.rearrange("(p c) -> p c", c=32))
         nc.sync.dma_start(out=bsm[:, 1, :], in_=b_hh.rearrange("(p c) -> p c", c=32))
         for i, vec in enumerate((ln_i_w, ln_h_w, ln_i_b, ln_h_b)):
             nc.sync.dma_start(out=prm[32 * i:32 * (i + 1), :], in_=vec.rearrange("(c p) -> c p", p=P))
+        load_bias(0)
+        nc.sync.dma_start(out=brow[0:CHUNKS, :], in_=b_ih.rearrange("(c n) -> c n", n=NT))
+        nc.sync.dma_start(out=brow[CHUNKS:2 * CHUNKS, :], in_=b_hh.rearrange("(c n) -> c n", n=NT))
+        load_raw(2)
+        nc.sync.dma_start(out=zw_raw, in_=rows_view(zw.rearrange("b s a -> b (s a)")))
+        nc.sync.dma_start(out=zb_raw, in_=rows_view(zb.rearrange("b s a -> b (s a)")))
 
         k_run(x_raw.bitcast(F32), 0, (0, 1))
         k_run(x_raw.bitcast(F32), 1, (0, 1))
@@ -320,19 +330,21 @@ def tile_adaptivelstmcell_pb_kernel(
             more = c + 1 < 2 * CHUNKS
             live = t < tiles
             if live and m == 0 and c + 2 < 2 * CHUNKS:
-                load_chunk(c + 2)
-            if t == MT:
+                if c > 0:
+                    load_raw(c + 2)
+                load_small(c + 2)
+                if c % 2 == 0:
+                    load_bias(c + 2)
+            if t == 2 * MT:
                 nc.sync.dma_start(out=hx_raw, in_=rows_view(hx))
-            if live and c == 0 and m < 2:
-                w_run(c + 1, m)
             if live and c > 0 and m == 0 and more:
                 w_run(c + 1, 0)
                 w_run(c + 1, 1)
             if live and m == 2:
                 if more:
                     ab_run(c + 1)
-                if c < 7:
-                    z_run(c + 1)
+                if 1 <= c <= 7:
+                    z_run(c)
                 if d >= 2:
                     n_run(d - 2, (0, 1))
                     n_run(d - 2, (2, 3))
@@ -342,6 +354,8 @@ def tile_adaptivelstmcell_pb_kernel(
                 mm_rest(t)
             if t >= 1:
                 add_beta_bias(t - 1)
+            if live and c == 0 and m < 2:
+                w_run(c + 1, m)
             if live and m == (2 if c == 0 else 1) and more:
                 w_quantise(c + 1)
             if live and m == 3:

@@ -28,6 +28,7 @@ AB_COPY = (0, 0)
 Z_COPY = (0, 0)
 TAIL_NORM = (1, 1, 0, 2)
 PE_BIAS = (3,)
+PE_BIAS_CHUNKS = 2
 
 FLOPS = 2 * 2 * BATCH * GATES * K + 16 * 2 * BATCH * H * 128
 
@@ -62,7 +63,7 @@ def tile_adaptivelstmcell_pb_kernel(
         xcodes = [keep.tile([P, PASSES, BATCH], U32, name="xcodes%d" % q, align_bytes=64) for q in range(2)]
         xscales = [keep.tile([P, PASSES, BATCH], U8, name="xscales%d" % q, align_bytes=64) for q in range(2)]
         zT = [keep.tile([P, 8, BATCH], BF16, name="zT%d" % i) for i in range(2)]
-        gbuf = [[keep.tile([P, MT, NT], F32, name="g%d_%d" % (q, d)) for d in range(CHUNKS)] for q in range(2)]
+        gbuf = [[keep.tile([P, MT, NT], F32, name="g%d_%d" % (q, d), align_bytes=64) for d in range(CHUNKS)] for q in range(2)]
         spare = keep.tile([P, MT, NT], F32, name="spare")
         turned = [spare] + gbuf[0][0:CHUNKS - 1]
         grouped = keep.tile([P, PASSES, 4 * NT], BF16, name="grouped", align_bytes=64)
@@ -206,7 +207,7 @@ def tile_adaptivelstmcell_pb_kernel(
                     stop=(g == PASSES - 1),
                 )
             beta = psum.tile([P, NT], F32, name="beta", tag="bank")
-            on_pe = m in PE_BIAS
+            on_pe = m in PE_BIAS or c < PE_BIAS_CHUNKS
             nc.tensor.matmul(out=beta[:], lhsT=zT[1][:, s, rows], rhs=ch["abT"][1][:], start=True, stop=not on_pe)
             if on_pe:
                 nc.tensor.matmul(out=beta[:], lhsT=ident_b[:, c:c + 1].to_broadcast([P, P]), rhs=brow[:],
@@ -219,7 +220,7 @@ def tile_adaptivelstmcell_pb_kernel(
             dst = gbuf[q][j][:, m, :]
             nc.vector.scalar_tensor_tensor(out=dst, in0=dst, scalar=1.0, in1=betas[t][:], op0=ALU.mult,
                                            op1=ALU.add, accum_out=sum_u[:, q, m, j:j + 1])
-            if m not in PE_BIAS:
+            if m not in PE_BIAS and c >= PE_BIAS_CHUNKS:
                 (nc.vector if t >= tiles - 2 else nc.gpsimd).tensor_tensor(out=dst, in0=dst, in1=bias_pairs[c // 2][:, c % 2, :],
                                                                            op=ALU.add)
 
@@ -294,35 +295,68 @@ def tile_adaptivelstmcell_pb_kernel(
         def norm_in_piece(i):
             normalise(1 if i >= 4 else 2, 0, i % MT, i // MT, stats[0])
 
-        for b in range(4):
-            nc.sync.dma_start(out=x_raw[:, b, :], in_=x[P * b:P * (b + 1), :])
+        nc.sync.dma_start(out=x_raw[:, 0, :], in_=x[0:P, :])
         load_raw(0)
         load_small(0)
         nc.sync.dma_start(out=z_first[0][:], in_=rows_view(zw[:, 0, :]))
         nc.sync.dma_start(out=z_first[1][:], in_=rows_view(zb[:, 0, :]))
-        load_raw(1)
-        load_small(1)
-        nc.sync.dma_start(out=bsm[:, 0, :], in_=b_ih.rearrange("(p c) -> p c", c=32))
-        nc.sync.dma_start(out=bsm[:, 1, :], in_=b_hh.rearrange("(p c) -> p c", c=32))
-        for i, vec in enumerate((ln_i_w, ln_h_w, ln_i_b, ln_h_b)):
-            nc.sync.dma_start(out=prm[32 * i:32 * (i + 1), :], in_=vec.rearrange("(c p) -> c p", p=P))
-        load_bias(0)
         nc.sync.dma_start(out=brow[0:CHUNKS, :], in_=b_ih.rearrange("(c n) -> c n", n=NT))
         nc.sync.dma_start(out=brow[CHUNKS:2 * CHUNKS, :], in_=b_hh.rearrange("(c n) -> c n", n=NT))
+        for b in range(1, 4):
+            nc.sync.dma_start(out=x_raw[:, b, :], in_=x[P * b:P * (b + 1), :])
+        load_raw(1)
+        load_small(1)
         load_raw(2)
-        nc.sync.dma_start(out=zw_raw, in_=rows_view(zw.rearrange("b s a -> b (s a)")))
-        nc.sync.dma_start(out=zb_raw, in_=rows_view(zb.rearrange("b s a -> b (s a)")))
+        z_views = (rows_view(zw.rearrange("b s a -> b (s a)")), rows_view(zb.rearrange("b s a -> b (s a)")))
+        for raw, view in zip((zw_raw, zb_raw), z_views):
+            nc.sync.dma_start(out=raw[:, :, P:4 * P], in_=view[:, :, P:4 * P])
 
-        k_run(x_raw.bitcast(F32), 0, (0, 1))
-        k_run(x_raw.bitcast(F32), 1, (0, 1))
-        quantise_pass(xcodes[0], xscales[0], 0)
-        quantise_pass(xcodes[0], xscales[0], 1)
-        w_run(0, 0)
-        w_run(0, 1)
+        x_words = x_raw.bitcast(F32)
+        x_stage = gbuf[1][0]
+
+        def x_tile(m):
+            pt = psum.tile([P, PASSES, 2, P], F32, name="ptx", tag="bank")
+            for g in range(PASSES):
+                for u in range(2):
+                    nc.tensor.transpose(pt[:, g, u, :], x_words[:, m, 256 * g + u:256 * (g + 1):2], ident_f[:])
+            for g in range(PASSES):
+                copy_on(g, x_stage[:, 2 * g + m // 2, 256 * (m % 2):256 * (m % 2 + 1)].rearrange("p (c u) -> p c u", u=2),
+                        pt[:, g, :, :].rearrange("p u c -> p c u"))
+
+        def x_quantise(m):
+            for g in range(PASSES):
+                nc.vector.quantize_mx(
+                    out=xcodes[0][:, g, P * m:P * (m + 1)].bitcast(FP8X4), scales=xscales[0][:, g, P * m:P * (m + 1)],
+                    in_=x_stage[:].bitcast(BF16)[:, 2 * g + m // 2, NT * (m % 2):NT * (m % 2 + 1)])
+
+        def w_run_by_rows(c):
+            words = chunks[c]["raw"][:].bitcast(F32)
+            for half in range(2):
+                banks = []
+                for g in range(PASSES):
+                    pt = psum.tile([P, 2, 256], F32, name="pt", tag="bank")
+                    banks.append(pt)
+                for bb in range(2):
+                    for g in range(PASSES):
+                        for u in range(2):
+                            nc.tensor.transpose(banks[g][:, u, P * bb:P * (bb + 1)],
+                                                words[:, 2 * half + bb, 256 * g + u:256 * (g + 1):2], ident_f[:])
+                for g in range(PASSES):
+                    gw = grouped[:, g, :].bitcast(F32).rearrange("p (c u) -> p c u", u=2)
+                    copy_on(g, gw[:, 256 * half:256 * (half + 1), :], banks[g][:].rearrange("p u c -> p c u"))
+
+        x_tile(0)
+        x_quantise(0)
+        w_run_by_rows(0)
+        chunks[0]["codes"] = wq.tile([P, PASSES, NT], U32, name="wcodes", tag="wcodes", align_bytes=64)
+        chunks[0]["scales"] = wq.tile([P, PASSES, NT], U8, name="wscales", tag="wscales", align_bytes=64)
+        quantise_pass(chunks[0]["codes"], chunks[0]["scales"], 0)
+        quantise_pass(chunks[0]["codes"], chunks[0]["scales"], 1)
         ab_run(0)
-        z_run(0, (1, 0))
-        w_quantise(0)
+        z_run(0, (0, 0))
         mm_alpha(0)
+        x_tile(1)
+        x_quantise(1)
 
         for t in range(tiles + 1):
             c, m = divmod(t, MT)
@@ -335,8 +369,16 @@ def tile_adaptivelstmcell_pb_kernel(
                 load_small(c + 2)
                 if c % 2 == 0:
                     load_bias(c + 2)
-            if t == 2 * MT:
+            if t == 3 * MT:
+                for raw, view in zip((zw_raw, zb_raw), z_views):
+                    nc.sync.dma_start(out=raw[:, :, 4 * P:8 * P], in_=view[:, :, 4 * P:8 * P])
+            if t == 4 * MT:
                 nc.sync.dma_start(out=hx_raw, in_=rows_view(hx))
+            if t == 2 * MT:
+                nc.sync.dma_start(out=bsm[:, 0, :], in_=b_ih.rearrange("(p c) -> p c", c=32))
+                nc.sync.dma_start(out=bsm[:, 1, :], in_=b_hh.rearrange("(p c) -> p c", c=32))
+                for i, vec in enumerate((ln_i_w, ln_h_w, ln_i_b, ln_h_b)):
+                    nc.sync.dma_start(out=prm[32 * i:32 * (i + 1), :], in_=vec.rearrange("(c p) -> c p", p=P))
             if live and c > 0 and m == 0 and more:
                 w_run(c + 1, 0)
                 w_run(c + 1, 1)
@@ -354,6 +396,9 @@ def tile_adaptivelstmcell_pb_kernel(
                 mm_rest(t)
             if t >= 1:
                 add_beta_bias(t - 1)
+            if t < 2:
+                x_tile(t + 2)
+                x_quantise(t + 2)
             if live and c == 0 and m < 2:
                 w_run(c + 1, m)
             if live and m == (2 if c == 0 else 1) and more:
@@ -363,14 +408,15 @@ def tile_adaptivelstmcell_pb_kernel(
                     k_run(hx_raw.bitcast(F32), 0, (0, 1))
                     k_run(hx_raw.bitcast(F32), 1, (0, 1))
                     quantise(xcodes[1], xscales[1])
-            if t == 3:
+            if t == 15:
                 nc.vector.tensor_reduce(out=bpart[:], in_=bsm[:], axis=AX.X, op=ALU.add)
-            if t == 5:
+                nc.vector.memset(bpart[0:PE_BIAS_CHUNKS * NT // 32, 0:1], 0.0)
+            if t == 17:
                 pb = psum.tile([P, 2], F32, name="pb", tag="bank")
                 nc.tensor.matmul(out=pb[:], lhsT=ones_f[:], rhs=bpart[:], start=True, stop=True)
                 pp = psum.tile([P, P], BF16, name="pp", tag="bank")
                 nc.tensor.transpose(pp[:], prm[:], ident_b[:])
-            if t == 6:
+            if t == 18:
                 nc.vector.tensor_copy(out=bsum[:], in_=pb[:])
                 nc.vector.tensor_copy(out=prmT[:], in_=pp[:])
                 nc.vector.tensor_tensor(out=lbT[:], in0=prmT[:, 64:96], in1=prmT[:, 96:128], op=ALU.add)
@@ -402,7 +448,8 @@ def tile_adaptivelstmcell_pb_kernel(
             for i, cb in enumerate(cbs):
                 nc.vector.scalar_tensor_tensor(out=region(cb), in0=banks[i][:], scalar=prmT[:, 32 + cb:33 + cb],
                                                in1=region(cb), op0=ALU.mult, op1=ALU.add)
-                nc.scalar.activation(out=region(cb), in_=region(cb), func=funcs[i])
+                if funcs:
+                    nc.scalar.activation(out=region(cb), in_=region(cb), func=funcs[i])
 
         def norm_piece(d):
             for m in range(MT):
@@ -481,14 +528,16 @@ def tile_adaptivelstmcell_pb_kernel(
             if hb == 7:
                 s_back_m(0, 2, 0)
                 s_back_m(0, 3, 0)
-        gates((24, 25, 26), (SIG, SIG, SIG))
+        gates((24, 25, 26), ())
         cell_sum(7)
-        gates((27, 28), (SIG, SIG))
-        gates((29, 30, 31), (SIG, SIG, SIG))
+        gates((27, 28), ())
+        gates((29, 30, 31), ())
         s_back_m(1, 0, 1)
         s_back_m(1, 1, 1)
         s_back_m(1, 2, 1)
         s_back_m(1, 3, 1)
+        for cb in range(24, 32):
+            nc.scalar.activation(out=region(cb), in_=region(cb), func=SIG)
         stats_c(0)
         cy_part(0)
         stats_c(1)

@@ -125,9 +125,9 @@ def tile_adaptivelstmcell_pb_kernel(
         def load_raw(c):
             q, j = divmod(c, CHUNKS)
             raw = rawp.tile([P, 4, K], BF16, name="raw", tag="raw")
-            if c == 0:
+            if c < 2:
                 for b in range(4):
-                    nc.sync.dma_start(out=raw[:, b, :], in_=w_ih[P * b:P * (b + 1), :])
+                    nc.sync.dma_start(out=raw[:, b, :], in_=w_ih[NT * c + P * b:NT * c + P * (b + 1), :])
             else:
                 nc.sync.dma_start(out=raw[:], in_=rows_view((w_ih, w_hh)[q][NT * j:NT * (j + 1), :]))
             chunks[c] = {"raw": raw, "q": q}
@@ -307,9 +307,6 @@ def tile_adaptivelstmcell_pb_kernel(
         load_raw(1)
         load_small(1)
         load_raw(2)
-        z_views = (rows_view(zw.rearrange("b s a -> b (s a)")), rows_view(zb.rearrange("b s a -> b (s a)")))
-        for raw, view in zip((zw_raw, zb_raw), z_views):
-            nc.sync.dma_start(out=raw[:, :, P:4 * P], in_=view[:, :, P:4 * P])
 
         x_words = x_raw.bitcast(F32)
         x_stage = gbuf[1][0]
@@ -329,9 +326,9 @@ def tile_adaptivelstmcell_pb_kernel(
                     out=xcodes[0][:, g, P * m:P * (m + 1)].bitcast(FP8X4), scales=xscales[0][:, g, P * m:P * (m + 1)],
                     in_=x_stage[:].bitcast(BF16)[:, 2 * g + m // 2, NT * (m % 2):NT * (m % 2 + 1)])
 
-        def w_run_by_rows(c):
+        def w_run_by_rows(c, halves):
             words = chunks[c]["raw"][:].bitcast(F32)
-            for half in range(2):
+            for half in halves:
                 banks = []
                 for g in range(PASSES):
                     pt = psum.tile([P, 2, 256], F32, name="pt", tag="bank")
@@ -347,7 +344,7 @@ def tile_adaptivelstmcell_pb_kernel(
 
         x_tile(0)
         x_quantise(0)
-        w_run_by_rows(0)
+        w_run_by_rows(0, (0, 1))
         chunks[0]["codes"] = wq.tile([P, PASSES, NT], U32, name="wcodes", tag="wcodes", align_bytes=64)
         chunks[0]["scales"] = wq.tile([P, PASSES, NT], U8, name="wscales", tag="wscales", align_bytes=64)
         quantise_pass(chunks[0]["codes"], chunks[0]["scales"], 0)
@@ -357,18 +354,28 @@ def tile_adaptivelstmcell_pb_kernel(
         mm_alpha(0)
         x_tile(1)
         x_quantise(1)
+        load_small(2)
+        z_views = (rows_view(zw.rearrange("b s a -> b (s a)")), rows_view(zb.rearrange("b s a -> b (s a)")))
+        for raw, view in zip((zw_raw, zb_raw), z_views):
+            nc.sync.dma_start(out=raw[:, :, P:2 * P], in_=view[:, :, P:2 * P])
+        load_bias(2)
+        load_raw(3)
 
         for t in range(tiles + 1):
             c, m = divmod(t, MT)
             d = c - CHUNKS
             more = c + 1 < 2 * CHUNKS
             live = t < tiles
-            if live and m == 0 and c + 2 < 2 * CHUNKS:
-                if c > 0:
-                    load_raw(c + 2)
-                load_small(c + 2)
-                if c % 2 == 0:
-                    load_bias(c + 2)
+            if live and m == 0 and c > 0:
+                if c + 2 < 2 * CHUNKS:
+                    load_small(c + 2)
+                    if c % 2 == 0:
+                        load_bias(c + 2)
+                if c == 1:
+                    for raw, view in zip((zw_raw, zb_raw), z_views):
+                        nc.sync.dma_start(out=raw[:, :, 2 * P:4 * P], in_=view[:, :, 2 * P:4 * P])
+                if c + 3 < 2 * CHUNKS:
+                    load_raw(c + 3)
             if t == 3 * MT:
                 for raw, view in zip((zw_raw, zb_raw), z_views):
                     nc.sync.dma_start(out=raw[:, :, 4 * P:8 * P], in_=view[:, :, 4 * P:8 * P])
@@ -400,7 +407,7 @@ def tile_adaptivelstmcell_pb_kernel(
                 x_tile(t + 2)
                 x_quantise(t + 2)
             if live and c == 0 and m < 2:
-                w_run(c + 1, m)
+                w_run_by_rows(c + 1, (m,))
             if live and m == (2 if c == 0 else 1) and more:
                 w_quantise(c + 1)
             if live and m == 3:

@@ -23,7 +23,7 @@ PASSES = 2
 CHUNKS = GATES // NT
 EPS = 1e-5
 
-W_COPY = (((0, 1), (0, 1)), ((1, 0), (1, 1)))
+W_COPY = (((0, 1), (0, 1)), ((1, 0), (1, 0)))
 AB_COPY = (0, 0)
 Z_COPY = (0, 0)
 TAIL_NORM = (1, 1, 0, 2)
@@ -207,7 +207,7 @@ def tile_adaptivelstmcell_pb_kernel(
                     stop=(g == PASSES - 1),
                 )
             beta = psum.tile([P, NT], F32, name="beta", tag="bank")
-            on_pe = m in PE_BIAS or c < PE_BIAS_CHUNKS
+            on_pe = (m in PE_BIAS and q == 1) or c < PE_BIAS_CHUNKS or c >= 2 * CHUNKS - PE_BIAS_CHUNKS
             nc.tensor.matmul(out=beta[:], lhsT=zT[1][:, s, rows], rhs=ch["abT"][1][:], start=True, stop=not on_pe)
             if on_pe:
                 nc.tensor.matmul(out=beta[:], lhsT=ident_b[:, c:c + 1].to_broadcast([P, P]), rhs=brow[:],
@@ -220,7 +220,7 @@ def tile_adaptivelstmcell_pb_kernel(
             dst = gbuf[q][j][:, m, :]
             nc.vector.scalar_tensor_tensor(out=dst, in0=dst, scalar=1.0, in1=betas[t][:], op0=ALU.mult,
                                            op1=ALU.add, accum_out=sum_u[:, q, m, j:j + 1])
-            if m not in PE_BIAS and c >= PE_BIAS_CHUNKS:
+            if (m not in PE_BIAS or q == 0) and PE_BIAS_CHUNKS <= c < 2 * CHUNKS - PE_BIAS_CHUNKS:
                 (nc.vector if t >= tiles - 2 else nc.gpsimd).tensor_tensor(out=dst, in0=dst, in1=bias_pairs[c // 2][:, c % 2, :],
                                                                            op=ALU.add)
 
@@ -237,7 +237,7 @@ def tile_adaptivelstmcell_pb_kernel(
             rstd = keep.tile([P, width], F32, name="rstd" + label)
             shift = keep.tile([P, width], F32, name="shift" + label)
             nc.vector.tensor_reduce(out=s1[:], in_=sums, axis=AX.X, op=ALU.add)
-            without = width if label[0] == "c" else min(PE_BIAS)
+            without = min(PE_BIAS) if label[0] == "h" else width
             nc.vector.tensor_scalar(out=negmean[:, 0:without], in0=s1[:, 0:without], scalar1=extra,
                                     scalar2=-1.0 / count, op0=ALU.add, op1=ALU.mult)
             if without < width:
@@ -369,7 +369,7 @@ def tile_adaptivelstmcell_pb_kernel(
             if live and m == 0 and c > 0:
                 if c + 2 < 2 * CHUNKS:
                     load_small(c + 2)
-                    if c % 2 == 0:
+                    if c % 2 == 0 and c + 2 < 2 * CHUNKS - PE_BIAS_CHUNKS:
                         load_bias(c + 2)
                 if c == 1:
                     for raw, view in zip((zw_raw, zb_raw), z_views):
@@ -418,6 +418,7 @@ def tile_adaptivelstmcell_pb_kernel(
             if t == 15:
                 nc.vector.tensor_reduce(out=bpart[:], in_=bsm[:], axis=AX.X, op=ALU.add)
                 nc.vector.memset(bpart[0:PE_BIAS_CHUNKS * NT // 32, 0:1], 0.0)
+                nc.vector.memset(bpart[P - PE_BIAS_CHUNKS * NT // 32:P, 1:2], 0.0)
             if t == 17:
                 pb = psum.tile([P, 2], F32, name="pb", tag="bank")
                 nc.tensor.matmul(out=pb[:], lhsT=ones_f[:], rhs=bpart[:], start=True, stop=True)

@@ -207,7 +207,7 @@ def tile_adaptivelstmcell_pb_kernel(
                     stop=(g == PASSES - 1),
                 )
             beta = psum.tile([P, NT], F32, name="beta", tag="bank")
-            on_pe = (m in PE_BIAS and q == 1) or c < PE_BIAS_CHUNKS or c >= 2 * CHUNKS - PE_BIAS_CHUNKS
+            on_pe = m in PE_BIAS or c < PE_BIAS_CHUNKS or c >= 2 * CHUNKS - PE_BIAS_CHUNKS
             nc.tensor.matmul(out=beta[:], lhsT=zT[1][:, s, rows], rhs=ch["abT"][1][:], start=True, stop=not on_pe)
             if on_pe:
                 nc.tensor.matmul(out=beta[:], lhsT=ident_b[:, c:c + 1].to_broadcast([P, P]), rhs=brow[:],
@@ -220,7 +220,7 @@ def tile_adaptivelstmcell_pb_kernel(
             dst = gbuf[q][j][:, m, :]
             nc.vector.scalar_tensor_tensor(out=dst, in0=dst, scalar=1.0, in1=betas[t][:], op0=ALU.mult,
                                            op1=ALU.add, accum_out=sum_u[:, q, m, j:j + 1])
-            if (m not in PE_BIAS or q == 0) and PE_BIAS_CHUNKS <= c < 2 * CHUNKS - PE_BIAS_CHUNKS:
+            if m not in PE_BIAS and PE_BIAS_CHUNKS <= c < 2 * CHUNKS - PE_BIAS_CHUNKS:
                 (nc.vector if t >= tiles - 2 else nc.gpsimd).tensor_tensor(out=dst, in0=dst, in1=bias_pairs[c // 2][:, c % 2, :],
                                                                            op=ALU.add)
 
@@ -237,7 +237,7 @@ def tile_adaptivelstmcell_pb_kernel(
             rstd = keep.tile([P, width], F32, name="rstd" + label)
             shift = keep.tile([P, width], F32, name="shift" + label)
             nc.vector.tensor_reduce(out=s1[:], in_=sums, axis=AX.X, op=ALU.add)
-            without = min(PE_BIAS) if label[0] == "h" else width
+            without = width if label[0] == "c" else min(PE_BIAS)
             nc.vector.tensor_scalar(out=negmean[:, 0:without], in0=s1[:, 0:without], scalar1=extra,
                                     scalar2=-1.0 / count, op0=ALU.add, op1=ALU.mult)
             if without < width:

@@ -27,6 +27,7 @@ W_COPY = (((0, 1), (0, 1)), ((1, 0), (1, 0)))
 AB_COPY = (0, 0)
 Z_COPY = (0, 0)
 TAIL_NORM = (1, 1, 0, 2)
+TAIL_NORM_LATER = (1, 1, 2, 2)
 PE_BIAS = (3,)
 PE_BIAS_CHUNKS = 2
 
@@ -230,14 +231,14 @@ def tile_adaptivelstmcell_pb_kernel(
             nc.scalar.activation(out=junk[:], in_=gbuf[q][j][:, m, :], func=ACT.Square,
                                  accum_out=sum_sq[:, q, m, j:j + 1])
 
-        def finish_stats(sums, squares, extra, count, label, width=MT):
+        def finish_stats(sums, squares, extra, count, label, width=MT, without=MT):
             s1 = keep.tile([P, width], F32, name="s1" + label)
             s2 = keep.tile([P, width], F32, name="s2" + label)
             negmean = keep.tile([P, width], F32, name="negmean" + label)
             rstd = keep.tile([P, width], F32, name="rstd" + label)
             shift = keep.tile([P, width], F32, name="shift" + label)
             nc.vector.tensor_reduce(out=s1[:], in_=sums, axis=AX.X, op=ALU.add)
-            without = width if label[0] == "c" else min(PE_BIAS)
+            without = min(without, width)
             nc.vector.tensor_scalar(out=negmean[:, 0:without], in0=s1[:, 0:without], scalar1=extra,
                                     scalar2=-1.0 / count, op0=ALU.add, op1=ALU.mult)
             if without < width:
@@ -252,12 +253,12 @@ def tile_adaptivelstmcell_pb_kernel(
             nc.gpsimd.tensor_tensor(out=shift[:], in0=negmean[:], in1=rstd[:], op=ALU.mult)
             return negmean, rstd, shift
 
-        def normalise(eng, q, m, d, st):
+        def normalise(eng, q, m, d, st, col):
             reg = gbuf[q][d][:, m, :]
-            nm = st[0][:, m:m + 1]
-            rs = st[1][:, m:m + 1]
+            nm = st[0][:, col:col + 1]
+            rs = st[1][:, col:col + 1]
             if eng == 0:
-                nc.scalar.activation(out=reg, in_=reg, func=ACT.Identity, bias=st[2][:, m:m + 1], scale=rs)
+                nc.scalar.activation(out=reg, in_=reg, func=ACT.Identity, bias=st[2][:, col:col + 1], scale=rs)
             elif eng == 1:
                 nc.vector.tensor_scalar(out=reg, in0=reg, scalar1=nm, scalar2=rs, op0=ALU.add, op1=ALU.mult)
             else:
@@ -293,7 +294,7 @@ def tile_adaptivelstmcell_pb_kernel(
         stats_at = CHUNKS * MT + 2
 
         def norm_in_piece(i):
-            normalise(1 if i >= 4 else 2, 0, i % MT, i // MT, stats[0])
+            normalise(1 if 4 <= i < 24 else 2, 0, i % MT, i // MT, stats[0], i % MT)
 
         nc.sync.dma_start(out=x_raw[:, 0, :], in_=x[0:P, :])
         load_raw(0)
@@ -394,7 +395,7 @@ def tile_adaptivelstmcell_pb_kernel(
                     ab_run(c + 1)
                 if 1 <= c <= 7:
                     z_run(c)
-                if d >= 2:
+                if 2 <= d < CHUNKS - 1:
                     n_run(d - 2, (0, 1))
                     n_run(d - 2, (2, 3))
             if t + 1 < tiles:
@@ -431,23 +432,22 @@ def tile_adaptivelstmcell_pb_kernel(
             if t >= 3:
                 square(t - 3)
             if t == stats_at:
-                stats[0] = finish_stats(sum_u[:, 0, :, :], sum_sq[:, 0, :, :], bsum[:, 0:1], GATES, "i")
-            if stats_at < t < tiles - 1:
+                stats[0] = finish_stats(sum_u[:, 0, :, :], sum_sq[:, 0, :, :], bsum[:, 0:1], GATES, "i", MT, min(PE_BIAS))
+            if stats_at < t <= stats_at + 24:
                 norm_in_piece(t - stats_at - 1)
+            if tiles - 8 <= t < tiles:
+                norm_in_piece(24 + t - (tiles - 8))
         cxt = rawp.tile([P, 4, K], BF16, name="raw", tag="raw")
         nc.sync.dma_start(out=cxt[:], in_=rows_view(cx))
         nc.sync.dma_start(out=wc[:], in_=ln_c_w.partition_broadcast(P))
         nc.sync.dma_start(out=bc[:], in_=ln_c_b.partition_broadcast(P))
+        st_h = [finish_stats(sum_u[:, 1, 0:2, :], sum_sq[:, 1, 0:2, :], bsum[:, 1:2], GATES, "h0", 2)]
         for t in range(tiles + 1, tiles + 3):
             square(t - 3)
 
-        stats[1] = finish_stats(sum_u[:, 1, :, :], sum_sq[:, 1, :, :], bsum[:, 1:2], GATES, "h")
-        for i in range(tiles - 2 - stats_at, 32):
-            norm_in_piece(i)
-        n_run(CHUNKS - 2, (0, 1))
-        n_run(CHUNKS - 2, (2, 3))
-        n_run(CHUNKS - 1, (0, 1))
-        n_run(CHUNKS - 1, (2, 3))
+        st_h.append(finish_stats(sum_u[:, 1, 2:4, :], sum_sq[:, 1, 2:4, :], bsum[:, 1:2], GATES, "h1", 2, min(PE_BIAS) - 2))
+        n_run(CHUNKS - 3, (0, 1))
+        n_run(CHUNKS - 3, (2, 3))
 
         def gates(cbs, funcs):
             banks = []
@@ -461,7 +461,7 @@ def tile_adaptivelstmcell_pb_kernel(
 
         def norm_piece(d):
             for m in range(MT):
-                normalise(TAIL_NORM[m], 1, m, d, stats[1])
+                normalise((TAIL_NORM if d in (4, 0, 2) else TAIL_NORM_LATER)[m], 1, m, d, st_h[m // 2], m % 2)
 
         def s_back_m(half, m, copy_eng):
             sb = psum.tile([P, NT], F32, name="sb", tag="bank")
@@ -524,12 +524,20 @@ def tile_adaptivelstmcell_pb_kernel(
             nc.gpsimd.tensor_tensor(out=region(hb), in0=region(hb), in1=region(8 + hb), op=ALU.mult)
 
         SIG = ACT.Sigmoid
-        for d in (4, 0, 2, 5, 1, 3, 6, 7):
+        for d in (4, 0, 2):
+            norm_piece(d)
+        n_run(CHUNKS - 2, (0, 1))
+        n_run(CHUNKS - 2, (2, 3))
+        for d in (5, 1, 3):
             norm_piece(d)
         for hb in range(8):
             cell_gates(hb)
             if hb >= 1:
                 cell_sum(hb - 1)
+            if hb < 2:
+                norm_piece(6 + hb)
+            if 2 <= hb < 6:
+                n_run(CHUNKS - 1, (hb - 2,))
             if hb == 6:
                 s_back_m(0, 0, 0)
                 s_back_m(0, 1, 0)

@@ -499,15 +499,30 @@ def tile_adaptivelstmcell_pb_kernel(
                 nc.sync.dma_start(out=out_1[P * m:P * (m + 1), cols], in_=cy_t)
                 nc.scalar.activation(out=gbuf[1][4 + half][:, m, :], in_=cy_t, func=ACT.Tanh)
 
+        o_h = (gbuf[0][CHUNKS - 1], gbuf[1][6])
+        o_sb = (gbuf[0][1], gbuf[0][2])
+
+        def o_gate_h(group):
+            cbs = list(range(24 + 4 * group, 28 + 4 * group))
+            banks = [turn(1, cb) for cb in cbs]
+            for k, cb in enumerate(cbs):
+                nc.scalar.activation(out=o_h[group][:, k, :], in_=banks[k][:], func=ACT.Identity,
+                                     scale=prmT[:, 32 + cb:33 + cb])
+
+        def o_back(m):
+            for half in range(2):
+                ob = psum.tile([P, NT], F32, name="ob", tag="bank")
+                for k in range(4):
+                    for i, part in enumerate((region(24 + 4 * half + k), o_h[half][:, k, :])):
+                        nc.tensor.matmul(out=ob[:, P * k:P * (k + 1)], lhsT=part[:, P * m:P * (m + 1)],
+                                         rhs=ident_f[:], is_transpose=True, start=(i == 0), stop=(i == 1))
+                nc.scalar.activation(out=o_sb[half][:, m, :], in_=ob[:], func=ACT.Sigmoid)
+
         def hy_part(m):
             for half in range(2):
                 cols = slice(NT * half, NT * (half + 1))
-                ob = psum.tile([P, NT], F32, name="ob", tag="bank")
-                for k in range(4):
-                    nc.tensor.transpose(ob[:, P * k:P * (k + 1)], region(24 + 4 * half + k)[:, P * m:P * (m + 1)],
-                                        ident_f[:])
                 hy_t = gbuf[1][half][:, m, :]
-                nc.vector.tensor_tensor(out=hy_t, in0=gbuf[1][4 + half][:, m, :], in1=ob[:], op=ALU.mult)
+                nc.vector.tensor_tensor(out=hy_t, in0=gbuf[1][4 + half][:, m, :], in1=o_sb[half][:, m, :], op=ALU.mult)
                 nc.sync.dma_start(out=out_0[P * m:P * (m + 1), cols], in_=hy_t)
 
         cx_banks = {}
@@ -523,7 +538,6 @@ def tile_adaptivelstmcell_pb_kernel(
             nc.vector.tensor_tensor(out=region(16 + hb), in0=region(16 + hb), in1=cx_banks[hb][:], op=ALU.mult)
             nc.gpsimd.tensor_tensor(out=region(hb), in0=region(hb), in1=region(8 + hb), op=ALU.mult)
 
-        SIG = ACT.Sigmoid
         for d in (4, 0, 2):
             norm_piece(d)
         n_run(CHUNKS - 2, (0, 1))
@@ -544,23 +558,24 @@ def tile_adaptivelstmcell_pb_kernel(
             if hb == 7:
                 s_back_m(0, 2, 0)
                 s_back_m(0, 3, 0)
-        gates((24, 25, 26), ())
+        o_gate_h(0)
         cell_sum(7)
-        gates((27, 28), ())
-        gates((29, 30, 31), ())
         s_back_m(1, 0, 1)
         s_back_m(1, 1, 1)
         s_back_m(1, 2, 1)
         s_back_m(1, 3, 1)
-        for cb in range(24, 32):
-            nc.scalar.activation(out=region(cb), in_=region(cb), func=SIG)
+        o_gate_h(1)
         stats_c(0)
+        o_back(0)
         cy_part(0)
         stats_c(1)
+        o_back(1)
         cy_part(1)
         hy_part(0)
+        o_back(2)
         cy_part(2)
         hy_part(1)
+        o_back(3)
         cy_part(3)
         hy_part(2)
         hy_part(3)

@@ -207,6 +207,11 @@ def tile_adaptivelstmcell_pb_kernel(
                     start=(g == 0),
                     stop=(g == PASSES - 1),
                 )
+            nc.vector.tensor_tensor(out=gbuf[q][j][:, m, :], in0=xh[:], in1=als[t][:], op=ALU.mult)
+
+        def mm_beta(t):
+            c, m, q, j, s, rows = where(t)
+            ch = chunks[c]
             beta = psum.tile([P, NT], F32, name="beta", tag="bank")
             on_pe = m in PE_BIAS or c < PE_BIAS_CHUNKS or c >= 2 * CHUNKS - PE_BIAS_CHUNKS
             nc.tensor.matmul(out=beta[:], lhsT=zT[1][:, s, rows], rhs=ch["abT"][1][:], start=True, stop=not on_pe)
@@ -214,7 +219,6 @@ def tile_adaptivelstmcell_pb_kernel(
                 nc.tensor.matmul(out=beta[:], lhsT=ident_b[:, c:c + 1].to_broadcast([P, P]), rhs=brow[:],
                                  start=False, stop=True)
             betas[t] = beta
-            nc.vector.tensor_tensor(out=gbuf[q][j][:, m, :], in0=xh[:], in1=als[t][:], op=ALU.mult)
 
         def add_beta_bias(t):
             c, m, q, j, s, rows = where(t)
@@ -403,6 +407,7 @@ def tile_adaptivelstmcell_pb_kernel(
             if live:
                 mm_rest(t)
             if t >= 1:
+                mm_beta(t - 1)
                 add_beta_bias(t - 1)
             if t < 2:
                 x_tile(t + 2)

@@ -558,11 +558,11 @@ def tile_adaptivelstmcell_pb_kernel(
             if 2 <= hb < 6:
                 n_run(CHUNKS - 1, (hb - 2,))
             if hb == 6:
-                s_back_m(0, 0, 0)
-                s_back_m(0, 1, 0)
+                s_back_m(0, 0, 1)
+                s_back_m(0, 1, 1)
             if hb == 7:
-                s_back_m(0, 2, 0)
-                s_back_m(0, 3, 0)
+                s_back_m(0, 2, 1)
+                s_back_m(0, 3, 1)
         o_gate_h(0)
         cell_sum(7)
         s_back_m(1, 0, 1)

@@ -347,14 +347,26 @@ def tile_adaptivelstmcell_pb_kernel(
                     gw = grouped[:, g, :].bitcast(F32).rearrange("p (c u) -> p c u", u=2)
                     copy_on(g, gw[:, 256 * half:256 * (half + 1), :], banks[g][:].rearrange("p u c -> p c u"))
 
+        warm_bank = psum.tile([P, P], F32, name="warmp", tag="bank")
+
+        def keep_warm(n):
+            for i in range(n):
+                nc.tensor.matmul(out=warm_bank[:], lhsT=ones_f[:], rhs=ones_f[:], start=True, stop=True)
+
+        keep_warm(4)
         x_tile(0)
         x_quantise(0)
-        w_run_by_rows(0, (0, 1))
+        keep_warm(1)
+        w_run_by_rows(0, (0,))
+        keep_warm(1)
+        w_run_by_rows(0, (1,))
+        keep_warm(1)
         chunks[0]["codes"] = wq.tile([P, PASSES, NT], U32, name="wcodes", tag="wcodes", align_bytes=64)
         chunks[0]["scales"] = wq.tile([P, PASSES, NT], U8, name="wscales", tag="wscales", align_bytes=64)
         quantise_pass(chunks[0]["codes"], chunks[0]["scales"], 0)
         quantise_pass(chunks[0]["codes"], chunks[0]["scales"], 1)
         ab_run(0)
+        keep_warm(1)
         z_run(0, (0, 0))
         mm_alpha(0)
         x_tile(1)

@@ -70,8 +70,10 @@ def tile_adaptivelstmcell_pb_kernel(
         grouped = keep.tile([P, PASSES, 4 * NT], BF16, name="grouped", align_bytes=64)
         sum_u = keep.tile([P, 2, MT, CHUNKS], F32, name="sum_u")
         sum_sq = keep.tile([P, 2, MT, CHUNKS], F32, name="sum_sq")
-        csum = keep.tile([P, MT, 2], F32, name="csum")
-        csq = keep.tile([P, MT, 2], F32, name="csq")
+        cbn = keep.tile([P, MT, 2, 6], F32, name="cbn")
+        cmv = keep.tile([P, MT, 2], F32, name="cmv")
+        cve = keep.tile([P, MT], F32, name="cve")
+        crs = keep.tile([P, MT], F32, name="crs")
         bsum = keep.tile([P, 2], F32, name="bsum")
 
         def copy_on(eng, out, in_):
@@ -480,38 +482,38 @@ def tile_adaptivelstmcell_pb_kernel(
             for m in range(MT):
                 normalise((TAIL_NORM if d in (4, 0, 2) else TAIL_NORM_LATER)[m], 1, m, d, st_h[m // 2], m % 2)
 
+        s_banks = {}
+
         def s_back_m(half, m, copy_eng):
             sb = psum.tile([P, NT], F32, name="sb", tag="bank")
             for k in range(4):
                 for i, cb in enumerate((16 + 4 * half + k, 4 * half + k)):
                     nc.tensor.matmul(out=sb[:, P * k:P * (k + 1)], lhsT=region(cb)[:, P * m:P * (m + 1)],
                                      rhs=ident_f[:], is_transpose=True, start=(i == 0), stop=(i == 1))
-            if copy_eng == 0:
-                nc.scalar.activation(out=gbuf[1][half][:, m, :], in_=sb[:], func=ACT.Identity,
-                                     accum_out=csum[:, m, half:half + 1])
+            nc.vector.bn_stats(out=cbn[:, m, half, :], in_=sb[:])
+            if half == 0:
+                nc.scalar.copy(out=gbuf[1][half][:, m, :], in_=sb[:])
             else:
-                nc.vector.tensor_scalar(out=gbuf[1][half][:, m, :], in0=sb[:], scalar1=1.0, scalar2=0.0, op0=ALU.mult,
-                                        op1=ALU.add, accum_out=csum[:, m, half:half + 1])
-            junk = work.tile([P, NT], BF16, name="junk", tag="junk")
-            nc.scalar.activation(out=junk[:], in_=sb[:], func=ACT.Square, accum_out=csq[:, m, half:half + 1])
-
-        st_c = [None, None]
+                s_banks[m] = sb
 
         def stats_c(p):
-            st_c[p] = finish_stats(csum[:, 2 * p:2 * p + 2, :], csq[:, 2 * p:2 * p + 2, :], 0.0, H, "c%d" % p, 2)
+            pair = slice(2 * p, 2 * p + 2)
+            for m in (2 * p, 2 * p + 1):
+                nc.vector.bn_aggr(out=cmv[:, m, :], in_=cbn[:, m, :, :].rearrange("p a b -> p (a b)"))
+            nc.vector.tensor_scalar(out=cve[:, pair], in0=cmv[:, pair, 1], scalar1=1.0, scalar2=EPS, op0=ALU.mult,
+                                    op1=ALU.add)
+            nc.gpsimd.tensor_tensor(out=crs[:, pair], in0=cve[:, pair], in1=neg_half[:, 0:2], op=ALU.pow)
 
         def cy_part(m):
-            st = st_c[m // 2]
-            col = m % 2
             for half in range(2):
                 cols = slice(NT * half, NT * (half + 1))
-                s_t = gbuf[1][half][:, m, :]
-                nc.vector.scalar_tensor_tensor(out=s_t, in0=s_t, scalar=st[0][:, col:col + 1], in1=wc[:, cols],
-                                               op0=ALU.add, op1=ALU.mult)
+                nc.vector.scalar_tensor_tensor(out=gbuf[1][half][:, m, :],
+                                               in0=gbuf[1][half][:, m, :] if half == 0 else s_banks[m][:],
+                                               scalar=cmv[:, m, 0:1], in1=wc[:, cols], op0=ALU.subtract, op1=ALU.mult)
             for half in range(2):
                 cols = slice(NT * half, NT * (half + 1))
                 cy_t = gbuf[1][2 + half][:, m, :]
-                nc.vector.scalar_tensor_tensor(out=cy_t, in0=gbuf[1][half][:, m, :], scalar=st[1][:, col:col + 1],
+                nc.vector.scalar_tensor_tensor(out=cy_t, in0=gbuf[1][half][:, m, :], scalar=crs[:, m:m + 1],
                                                in1=bc[:, cols], op0=ALU.mult, op1=ALU.add)
                 nc.sync.dma_start(out=out_1[P * m:P * (m + 1), cols], in_=cy_t)
                 nc.scalar.activation(out=gbuf[1][4 + half][:, m, :], in_=cy_t, func=ACT.Tanh)

@@ -478,9 +478,9 @@ def tile_adaptivelstmcell_pb_kernel(
                 if funcs:
                     nc.scalar.activation(out=region(cb), in_=region(cb), func=funcs[i])
 
-        def norm_piece(d):
-            for m in range(MT):
-                normalise((TAIL_NORM if d in (4, 0, 2) else TAIL_NORM_LATER)[m], 1, m, d, st_h[m // 2], m % 2)
+        def norm_piece(d, ms=(0, 1, 2, 3), engines=None):
+            for m in ms:
+                normalise((engines or (TAIL_NORM if d in (4, 0, 2) else TAIL_NORM_LATER))[m], 1, m, d, st_h[m // 2], m % 2)
 
         s_banks = {}
 
@@ -568,7 +568,7 @@ def tile_adaptivelstmcell_pb_kernel(
             if hb >= 1:
                 cell_sum(hb - 1)
             if hb < 2:
-                norm_piece(6 + hb)
+                norm_piece(6 + hb, (2, 3))
             if 2 <= hb < 6:
                 n_run(CHUNKS - 1, (hb - 2,))
             if hb == 6:
@@ -577,12 +577,14 @@ def tile_adaptivelstmcell_pb_kernel(
             if hb == 7:
                 s_back_m(0, 2, 1)
                 s_back_m(0, 3, 1)
-        o_gate_h(0)
         cell_sum(7)
         s_back_m(1, 0, 1)
         s_back_m(1, 1, 1)
         s_back_m(1, 2, 1)
         s_back_m(1, 3, 1)
+        norm_piece(6, (0, 1), (0, 0))
+        norm_piece(7, (0, 1), (0, 0))
+        o_gate_h(0)
         o_gate_h(1)
         stats_c(0)
         o_back(0)
@@ -590,11 +592,11 @@ def tile_adaptivelstmcell_pb_kernel(
         stats_c(1)
         o_back(1)
         cy_part(1)
-        hy_part(0)
         o_back(2)
         cy_part(2)
-        hy_part(1)
+        hy_part(0)
         o_back(3)
         cy_part(3)
+        hy_part(1)
         hy_part(2)
         hy_part(3)

@@ -29,7 +29,7 @@ Z_COPY = (0, 0)
 TAIL_NORM = (1, 1, 0, 2)
 TAIL_NORM_LATER = (1, 1, 2, 2)
 PE_BIAS = (3,)
-PE_BIAS_CHUNKS = 2
+PE_BIAS_CHUNKS = 1
 
 FLOPS = 2 * 2 * BATCH * GATES * K + 16 * 2 * BATCH * H * 128
 
@@ -377,6 +377,7 @@ def tile_adaptivelstmcell_pb_kernel(
         z_views = (rows_view(zw.rearrange("b s a -> b (s a)")), rows_view(zb.rearrange("b s a -> b (s a)")))
         for raw, view in zip((zw_raw, zb_raw), z_views):
             nc.sync.dma_start(out=raw[:, :, P:2 * P], in_=view[:, :, P:2 * P])
+        load_bias(0)
         load_bias(2)
         load_raw(3)
 
@@ -388,7 +389,7 @@ def tile_adaptivelstmcell_pb_kernel(
             if live and m == 0 and c > 0:
                 if c + 2 < 2 * CHUNKS:
                     load_small(c + 2)
-                    if c % 2 == 0 and c + 2 < 2 * CHUNKS - PE_BIAS_CHUNKS:
+                    if c % 2 == 0:
                         load_bias(c + 2)
                 if c == 1:
                     for raw, view in zip((zw_raw, zb_raw), z_views):
@@ -402,7 +403,9 @@ def tile_adaptivelstmcell_pb_kernel(
                 nc.sync.dma_start(out=hx_raw, in_=rows_view(hx))
             if t == 2 * MT:
                 nc.sync.dma_start(out=bsm[:, 0, :], in_=b_ih.rearrange("(p c) -> p c", c=32))
-                nc.sync.dma_start(out=bsm[:, 1, :], in_=b_hh.rearrange("(p c) -> p c", c=32))
+                edge = PE_BIAS_CHUNKS * NT // 32
+                nc.sync.dma_start(out=bsm[0:edge, 1, :], in_=b_hh[GATES - 32 * edge:GATES].rearrange("(p c) -> p c", c=32))
+                nc.sync.dma_start(out=bsm[edge:P, 1, :], in_=b_hh[0:GATES - 32 * edge].rearrange("(p c) -> p c", c=32))
                 for i, vec in enumerate((ln_i_w, ln_h_w, ln_i_b, ln_h_b)):
                     nc.sync.dma_start(out=prm[32 * i:32 * (i + 1), :], in_=vec.rearrange("(c p) -> c p", p=P))
             if live and c > 0 and m == 0 and more:
@@ -437,8 +440,7 @@ def tile_adaptivelstmcell_pb_kernel(
                     quantise(xcodes[1], xscales[1])
             if t == 15:
                 nc.vector.tensor_reduce(out=bpart[:], in_=bsm[:], axis=AX.X, op=ALU.add)
-                nc.vector.memset(bpart[0:PE_BIAS_CHUNKS * NT // 32, 0:1], 0.0)
-                nc.vector.memset(bpart[P - PE_BIAS_CHUNKS * NT // 32:P, 1:2], 0.0)
+                nc.vector.memset(bpart[0:PE_BIAS_CHUNKS * NT // 32, :], 0.0)
             if t == 17:
                 pb = psum.tile([P, 2], F32, name="pb", tag="bank")
                 nc.tensor.matmul(out=pb[:], lhsT=ones_f[:], rhs=bpart[:], start=True, stop=True)

@@ -550,6 +550,8 @@ def tile_adaptivelstmcell_pb_kernel(
 
         def cell_gates(hb):
             gates((16 + hb, hb, 8 + hb), (ACT.Sigmoid, ACT.Sigmoid, ACT.Tanh))
+
+        def cx_turn(hb):
             cxT = psum.tile([P, BATCH], BF16, name="cxT", tag="bank")
             for m in range(MT):
                 nc.tensor.transpose(cxT[:, P * m:P * (m + 1)], cxt[:, m, P * hb:P * (hb + 1)], ident_b[:])
@@ -568,6 +570,7 @@ def tile_adaptivelstmcell_pb_kernel(
         for hb in range(8):
             cell_gates(hb)
             if hb >= 1:
+                cx_turn(hb - 1)
                 cell_sum(hb - 1)
             if hb < 2:
                 norm_piece(6 + hb, (2, 3))
@@ -579,6 +582,7 @@ def tile_adaptivelstmcell_pb_kernel(
             if hb == 7:
                 s_back_m(0, 2, 1)
                 s_back_m(0, 3, 1)
+        cx_turn(7)
         cell_sum(7)
         s_back_m(1, 0, 1)
         s_back_m(1, 1, 1)

@@ -506,12 +506,13 @@ def tile_adaptivelstmcell_pb_kernel(
                                     op1=ALU.add)
             nc.gpsimd.tensor_tensor(out=crs[:, pair], in0=cve[:, pair], in1=neg_half[:, 0:2], op=ALU.pow)
 
-        def cy_part(m):
-            for half in range(2):
-                cols = slice(NT * half, NT * (half + 1))
-                nc.vector.scalar_tensor_tensor(out=gbuf[1][half][:, m, :],
-                                               in0=gbuf[1][half][:, m, :] if half == 0 else s_banks[m][:],
-                                               scalar=cmv[:, m, 0:1], in1=wc[:, cols], op0=ALU.subtract, op1=ALU.mult)
+        def cy_centre(m, half):
+            cols = slice(NT * half, NT * (half + 1))
+            nc.vector.scalar_tensor_tensor(out=gbuf[1][half][:, m, :],
+                                           in0=gbuf[1][half][:, m, :] if half == 0 else s_banks[m][:],
+                                           scalar=cmv[:, m, 0:1], in1=wc[:, cols], op0=ALU.subtract, op1=ALU.mult)
+
+        def cy_finish(m):
             for half in range(2):
                 cols = slice(NT * half, NT * (half + 1))
                 cy_t = gbuf[1][2 + half][:, m, :]
@@ -594,15 +595,23 @@ def tile_adaptivelstmcell_pb_kernel(
         o_gate_h(1)
         stats_c(0)
         o_back(0)
-        cy_part(0)
+        cy_centre(0, 0)
+        cy_centre(0, 1)
+        cy_centre(1, 1)
         stats_c(1)
+        cy_finish(0)
         o_back(1)
-        cy_part(1)
+        cy_centre(1, 0)
+        cy_centre(2, 1)
+        cy_centre(3, 1)
+        cy_finish(1)
         o_back(2)
-        cy_part(2)
+        cy_centre(2, 0)
+        cy_centre(3, 0)
+        cy_finish(2)
         hy_part(0)
         o_back(3)
-        cy_part(3)
+        cy_finish(3)
         hy_part(1)
         hy_part(2)
         hy_part(3)

@@ -19,17 +19,20 @@ H = 1024
 GATES = 4096
 NT = 512
 MT = BATCH // P
-PASSES = 2
+PASSES = K // 512
 CHUNKS = GATES // NT
+PATCHES = 2 * CHUNKS * MT
+PANELS = GATES // P
 EPS = 1e-5
 
-W_COPY = (((0, 1), (0, 1)), ((1, 0), (1, 0)))
-AB_COPY = (0, 0)
-Z_COPY = (0, 0)
-TAIL_NORM = (1, 1, 0, 2)
-TAIL_NORM_LATER = (1, 1, 2, 2)
-PE_BIAS = (3,)
-PE_BIAS_CHUNKS = 1
+SCALAR = 0
+VECTOR = 1
+GPSIMD = 2
+
+WEIGHT_BANK_ENGINES = ((SCALAR, VECTOR), (VECTOR, SCALAR))
+TENSOR_BIAS_TILE = 3
+FIRST_NORM_ENGINES = (VECTOR, VECTOR, SCALAR, GPSIMD)
+LATER_NORM_ENGINES = (VECTOR, VECTOR, GPSIMD, GPSIMD)
 
 FLOPS = 2 * 2 * BATCH * GATES * K + 16 * 2 * BATCH * H * 128
 
@@ -56,48 +59,51 @@ def tile_adaptivelstmcell_pb_kernel(
         nc.vector.memset(ones_f[:], 1.0)
         neg_half = keep.tile([P, MT], F32, name="neg_half")
         nc.vector.memset(neg_half[:], -0.5)
-        brow = keep.tile([P, NT], BF16, name="brow")
-        nc.vector.memset(brow[:], 0.0)
+        bias_rows = keep.tile([P, NT], BF16, name="brow")
+        nc.vector.memset(bias_rows[:], 0.0)
         warm = keep.tile([P, 1], F32, name="warm")
         nc.scalar.activation(out=warm[:], in_=neg_half[:, 0:1], func=ACT.Sigmoid)
 
         xcodes = [keep.tile([P, PASSES, BATCH], U32, name="xcodes%d" % q, align_bytes=64) for q in range(2)]
         xscales = [keep.tile([P, PASSES, BATCH], U8, name="xscales%d" % q, align_bytes=64) for q in range(2)]
         zT = [keep.tile([P, 8, BATCH], BF16, name="zT%d" % i) for i in range(2)]
-        gbuf = [[keep.tile([P, MT, NT], F32, name="g%d_%d" % (q, d), align_bytes=64) for d in range(CHUNKS)] for q in range(2)]
+        patches = [[keep.tile([P, MT, NT], F32, name="g%d_%d" % (q, j), align_bytes=64) for j in range(CHUNKS)]
+                   for q in range(2)]
         spare = keep.tile([P, MT, NT], F32, name="spare")
-        turned = [spare] + gbuf[0][0:CHUNKS - 1]
+        panel_tiles = [spare] + patches[0][0:CHUNKS - 1]
         grouped = keep.tile([P, PASSES, 4 * NT], BF16, name="grouped", align_bytes=64)
         sum_u = keep.tile([P, 2, MT, CHUNKS], F32, name="sum_u")
         sum_sq = keep.tile([P, 2, MT, CHUNKS], F32, name="sum_sq")
-        cbn = keep.tile([P, MT, 2, 6], F32, name="cbn")
-        cmv = keep.tile([P, MT, 2], F32, name="cmv")
-        cve = keep.tile([P, MT], F32, name="cve")
-        crs = keep.tile([P, MT], F32, name="crs")
-        bsum = keep.tile([P, 2], F32, name="bsum")
+        cell_bn = keep.tile([P, MT, 2, 6], F32, name="cbn")
+        cell_mv = keep.tile([P, MT, 2], F32, name="cmv")
+        cell_ve = keep.tile([P, MT], F32, name="cve")
+        cell_rstd = keep.tile([P, MT], F32, name="crs")
+        bias_sum = keep.tile([P, 2], F32, name="bsum")
 
-        def copy_on(eng, out, in_):
-            if eng == 0:
+        def copy_on(engine, out, in_):
+            if engine == SCALAR:
                 nc.scalar.copy(out=out, in_=in_)
             else:
                 nc.vector.tensor_copy(out=out, in_=in_)
 
-        def k_run(words, g, engines):
-            gw = grouped[:, g, :].bitcast(F32).rearrange("p (c u) -> p c u", u=2)
+        def interleaved(g):
+            return grouped[:, g, :].bitcast(F32).rearrange("p (c u) -> p c u", u=2)
+
+        def turn_pass(words, g, engines):
             banks = []
-            for half in range(2):
-                pt = psum.tile([P, 2, 256], F32, name="pt", tag="bank")
+            for duo in range(2):
+                bank = psum.tile([P, 2, 256], F32, name="pt", tag="bank")
                 for bb in range(2):
                     for u in range(2):
                         nc.tensor.transpose(
-                            pt[:, u, P * bb:P * (bb + 1)],
-                            words[:, 2 * half + bb, 256 * g + u:256 * (g + 1):2],
+                            bank[:, u, P * bb:P * (bb + 1)],
+                            words[:, 2 * duo + bb, 256 * g + u:256 * (g + 1):2],
                             ident_f[:],
                         )
-                banks.append(pt)
-            for half in range(2):
-                copy_on(engines[half], gw[:, 256 * half:256 * (half + 1), :],
-                        banks[half][:].rearrange("p u c -> p c u"))
+                banks.append(bank)
+            for duo in range(2):
+                copy_on(engines[duo], interleaved(g)[:, 256 * duo:256 * (duo + 1), :],
+                        banks[duo][:].rearrange("p u c -> p c u"))
 
         def quantise(codes, scales):
             nc.vector.quantize_mx(out=codes[:].rearrange("p g c -> p (g c)").bitcast(FP8X4),
@@ -110,20 +116,19 @@ def tile_adaptivelstmcell_pb_kernel(
         def rows_view(src2d):
             return src2d.rearrange("(b r) k -> r b k", r=P)
 
-        x_raw, zw_raw, zb_raw, hx_raw = [gbuf[1][4 + i][:].bitcast(BF16) for i in range(4)]
+        x_raw, zw_raw, zb_raw, hx_raw = [patches[1][4 + i][:].bitcast(BF16) for i in range(4)]
         z_first = [keep.tile([P, MT, P], BF16, name="z_first%d" % i) for i in range(2)]
         chunks = {}
-        als = {}
-        betas = {}
-
-        bias_pairs = {}
+        alpha_copies = {}
+        beta_banks = {}
+        bias_tiles = {}
 
         def load_bias(c):
             q, j = divmod(c, CHUNKS)
-            bias2 = abp.tile([P, 2, NT], BF16, name="bias", tag="bias", bufs=3)
-            nc.sync.dma_start(out=bias2[:].rearrange("p a n -> p (a n)"),
+            spread = abp.tile([P, 2, NT], BF16, name="bias", tag="bias", bufs=3)
+            nc.sync.dma_start(out=spread[:].rearrange("p a n -> p (a n)"),
                               in_=(b_ih, b_hh)[q][NT * j:NT * (j + 2)].partition_broadcast(P))
-            bias_pairs[c // 2] = bias2
+            bias_tiles[c // 2] = spread
 
         def load_raw(c):
             q, j = divmod(c, CHUNKS)
@@ -137,71 +142,75 @@ def tile_adaptivelstmcell_pb_kernel(
 
         def load_small(c):
             q, j = divmod(c, CHUNKS)
-            s = 4 * q + j // 2
+            slot = 4 * q + j // 2
             h0 = NT * (j % 2)
             small = []
             for i, wsrc in enumerate((norm_alpha_w, bias_beta_w)):
                 sraw = abp.tile([P, 4, P], BF16, name="sraw%d" % i, tag="sraw%d" % i)
-                nc.sync.dma_start(out=sraw[:], in_=wsrc[s, h0:h0 + NT, :].rearrange("(b r) a -> r b a", r=P))
+                nc.sync.dma_start(out=sraw[:], in_=wsrc[slot, h0:h0 + NT, :].rearrange("(b r) a -> r b a", r=P))
                 small.append(sraw)
             chunks[c]["small"] = small
 
-        def w_run(c, g):
+        def turn_weights(c, g):
             ch = chunks[c]
-            k_run(ch["raw"][:].bitcast(F32), g, W_COPY[ch["q"]][g])
+            turn_pass(ch["raw"][:].bitcast(F32), g, WEIGHT_BANK_ENGINES[ch["q"]])
 
-        def w_quantise(c):
-            ch = chunks[c]
-            ch["codes"] = wq.tile([P, PASSES, NT], U32, name="wcodes", tag="wcodes", align_bytes=64)
-            ch["scales"] = wq.tile([P, PASSES, NT], U8, name="wscales", tag="wscales", align_bytes=64)
-            quantise(ch["codes"], ch["scales"])
+        def new_codes(c):
+            chunks[c]["codes"] = wq.tile([P, PASSES, NT], U32, name="wcodes", tag="wcodes", align_bytes=64)
+            chunks[c]["scales"] = wq.tile([P, PASSES, NT], U8, name="wscales", tag="wscales", align_bytes=64)
 
-        def ab_run(c, engines=AB_COPY):
+        def quantise_weights(c):
+            new_codes(c)
+            quantise(chunks[c]["codes"], chunks[c]["scales"])
+
+        def turn_small(c):
             ch = chunks[c]
             banks = []
             for i in range(2):
-                pt = psum.tile([P, NT], BF16, name="pta", tag="bank")
+                bank = psum.tile([P, NT], BF16, name="pta", tag="bank")
                 for b in range(4):
-                    nc.tensor.transpose(pt[:, P * b:P * (b + 1)], ch["small"][i][:, b, :], ident_b[:])
-                banks.append(pt)
-            abT = []
+                    nc.tensor.transpose(bank[:, P * b:P * (b + 1)], ch["small"][i][:, b, :], ident_b[:])
+                banks.append(bank)
+            ch["smallT"] = []
             for i in range(2):
                 wT = abp.tile([P, NT], BF16, name="wT%d" % i, tag="wT%d" % i)
-                copy_on(engines[i], wT[:], banks[i][:])
-                abT.append(wT)
-            ch["abT"] = abT
+                nc.scalar.copy(out=wT[:], in_=banks[i][:])
+                ch["smallT"].append(wT)
 
-        def z_run(s, engines=Z_COPY):
+        def turn_z(slot):
             banks = []
             for raw, first in ((zw_raw, z_first[0]), (zb_raw, z_first[1])):
-                pt = psum.tile([P, BATCH], BF16, name="ptz", tag="bank")
+                bank = psum.tile([P, BATCH], BF16, name="ptz", tag="bank")
                 for m in range(MT):
-                    src = first[:, m, :] if s == 0 else raw[:, m, P * s:P * (s + 1)]
-                    nc.tensor.transpose(pt[:, P * m:P * (m + 1)], src, ident_b[:])
-                banks.append(pt)
+                    src = first[:, m, :] if slot == 0 else raw[:, m, P * slot:P * (slot + 1)]
+                    nc.tensor.transpose(bank[:, P * m:P * (m + 1)], src, ident_b[:])
+                banks.append(bank)
             for i in range(2):
-                copy_on(engines[i], zT[i][:, s, :], banks[i][:])
+                nc.scalar.copy(out=zT[i][:, slot, :], in_=banks[i][:])
 
         def where(t):
             c, m = divmod(t, MT)
             q, j = divmod(c, CHUNKS)
             return c, m, q, j, 4 * q + j // 2, slice(P * m, P * (m + 1))
 
-        def mm_alpha(t):
-            c, m, q, j, s, rows = where(t)
+        def bias_on_tensor(c, m):
+            return m == TENSOR_BIAS_TILE or c == 0 or c == 2 * CHUNKS - 1
+
+        def alpha_of(t):
+            c, m, q, j, slot, rows = where(t)
             alpha = psum.tile([P, NT], F32, name="alpha", tag="bank")
-            nc.tensor.matmul(out=alpha[:], lhsT=zT[0][:, s, rows], rhs=chunks[c]["abT"][0][:], start=True, stop=True)
+            nc.tensor.matmul(out=alpha[:], lhsT=zT[0][:, slot, rows], rhs=chunks[c]["smallT"][0][:], start=True, stop=True)
             al = work.tile([P, NT], F32, name="al", tag="al")
             nc.scalar.copy(out=al[:], in_=alpha[:])
-            als[t] = al
+            alpha_copies[t] = al
 
-        def mm_rest(t):
-            c, m, q, j, s, rows = where(t)
+        def product_of(t):
+            c, m, q, j, slot, rows = where(t)
             ch = chunks[c]
-            xh = psum.tile([P, NT], F32, name="xh", tag="bank")
+            acc = psum.tile([P, NT], F32, name="xh", tag="bank")
             for g in range(PASSES):
                 nc.tensor.matmul_mx(
-                    out=xh[:],
+                    out=acc[:],
                     lhsT=xcodes[q][:, g, rows].bitcast(FP8X4),
                     lhsT_scale=xscales[q][:, g, rows],
                     rhs=ch["codes"][:, g, :].bitcast(FP8X4),
@@ -209,106 +218,108 @@ def tile_adaptivelstmcell_pb_kernel(
                     start=(g == 0),
                     stop=(g == PASSES - 1),
                 )
-            nc.vector.tensor_tensor(out=gbuf[q][j][:, m, :], in0=xh[:], in1=als[t][:], op=ALU.mult)
+            nc.vector.tensor_tensor(out=patches[q][j][:, m, :], in0=acc[:], in1=alpha_copies[t][:], op=ALU.mult)
 
-        def mm_beta(t):
-            c, m, q, j, s, rows = where(t)
-            ch = chunks[c]
+        def beta_of(t):
+            c, m, q, j, slot, rows = where(t)
             beta = psum.tile([P, NT], F32, name="beta", tag="bank")
-            on_pe = m in PE_BIAS or c < PE_BIAS_CHUNKS or c >= 2 * CHUNKS - PE_BIAS_CHUNKS
-            nc.tensor.matmul(out=beta[:], lhsT=zT[1][:, s, rows], rhs=ch["abT"][1][:], start=True, stop=not on_pe)
-            if on_pe:
-                nc.tensor.matmul(out=beta[:], lhsT=ident_b[:, c:c + 1].to_broadcast([P, P]), rhs=brow[:],
+            with_bias = bias_on_tensor(c, m)
+            nc.tensor.matmul(out=beta[:], lhsT=zT[1][:, slot, rows], rhs=chunks[c]["smallT"][1][:], start=True,
+                             stop=not with_bias)
+            if with_bias:
+                nc.tensor.matmul(out=beta[:], lhsT=ident_b[:, c:c + 1].to_broadcast([P, P]), rhs=bias_rows[:],
                                  start=False, stop=True)
-            betas[t] = beta
+            beta_banks[t] = beta
 
-        def add_beta_bias(t):
-            c, m, q, j, s, rows = where(t)
-            dst = gbuf[q][j][:, m, :]
-            nc.vector.scalar_tensor_tensor(out=dst, in0=dst, scalar=1.0, in1=betas[t][:], op0=ALU.mult,
+        def add_beta_and_bias(t):
+            c, m, q, j, slot, rows = where(t)
+            patch = patches[q][j][:, m, :]
+            nc.vector.scalar_tensor_tensor(out=patch, in0=patch, scalar=1.0, in1=beta_banks[t][:], op0=ALU.mult,
                                            op1=ALU.add, accum_out=sum_u[:, q, m, j:j + 1])
-            if m not in PE_BIAS and PE_BIAS_CHUNKS <= c < 2 * CHUNKS - PE_BIAS_CHUNKS:
-                (nc.vector if t >= tiles - 2 else nc.gpsimd).tensor_tensor(out=dst, in0=dst, in1=bias_pairs[c // 2][:, c % 2, :],
-                                                                           op=ALU.add)
+            if not bias_on_tensor(c, m):
+                nc.gpsimd.tensor_tensor(out=patch, in0=patch, in1=bias_tiles[c // 2][:, c % 2, :], op=ALU.add)
 
         def square(t):
-            c, m, q, j, s, rows = where(t)
-            junk = work.tile([P, NT], BF16, name="junk", tag="junk")
-            nc.scalar.activation(out=junk[:], in_=gbuf[q][j][:, m, :], func=ACT.Square,
+            c, m, q, j, slot, rows = where(t)
+            unread = work.tile([P, NT], BF16, name="junk", tag="junk")
+            nc.scalar.activation(out=unread[:], in_=patches[q][j][:, m, :], func=ACT.Square,
                                  accum_out=sum_sq[:, q, m, j:j + 1])
 
-        def finish_stats(sums, squares, extra, count, label, width=MT, without=MT):
+        def finish_stats(q, first, width, label, for_scalar):
             s1 = keep.tile([P, width], F32, name="s1" + label)
             s2 = keep.tile([P, width], F32, name="s2" + label)
             negmean = keep.tile([P, width], F32, name="negmean" + label)
             rstd = keep.tile([P, width], F32, name="rstd" + label)
-            shift = keep.tile([P, width], F32, name="shift" + label)
-            nc.vector.tensor_reduce(out=s1[:], in_=sums, axis=AX.X, op=ALU.add)
-            without = min(without, width)
-            nc.vector.tensor_scalar(out=negmean[:, 0:without], in0=s1[:, 0:without], scalar1=extra,
-                                    scalar2=-1.0 / count, op0=ALU.add, op1=ALU.mult)
-            if without < width:
-                nc.vector.tensor_scalar(out=negmean[:, without:width], in0=s1[:, without:width], scalar1=0.0,
-                                        scalar2=-1.0 / count, op0=ALU.add, op1=ALU.mult)
+            nc.vector.tensor_reduce(out=s1[:], in_=sum_u[:, q, first:first + width, :], axis=AX.X, op=ALU.add)
+            lacking = min(TENSOR_BIAS_TILE - first, width)
+            nc.vector.tensor_scalar(out=negmean[:, 0:lacking], in0=s1[:, 0:lacking], scalar1=bias_sum[:, q:q + 1],
+                                    scalar2=-1.0 / GATES, op0=ALU.add, op1=ALU.mult)
+            if lacking < width:
+                nc.vector.tensor_scalar(out=negmean[:, lacking:width], in0=s1[:, lacking:width], scalar1=0.0,
+                                        scalar2=-1.0 / GATES, op0=ALU.add, op1=ALU.mult)
             nc.vector.tensor_tensor(out=s1[:], in0=negmean[:], in1=negmean[:], op=ALU.mult)
-            nc.vector.tensor_reduce(out=s2[:], in_=squares, axis=AX.X, op=ALU.add)
-            nc.vector.scalar_tensor_tensor(out=s2[:], in0=s2[:], scalar=1.0 / count, in1=s1[:],
+            nc.vector.tensor_reduce(out=s2[:], in_=sum_sq[:, q, first:first + width, :], axis=AX.X, op=ALU.add)
+            nc.vector.scalar_tensor_tensor(out=s2[:], in0=s2[:], scalar=1.0 / GATES, in1=s1[:],
                                            op0=ALU.mult, op1=ALU.subtract)
             nc.vector.tensor_scalar(out=s2[:], in0=s2[:], scalar1=0.0, scalar2=EPS, op0=ALU.max, op1=ALU.add)
             nc.gpsimd.tensor_tensor(out=rstd[:], in0=s2[:], in1=neg_half[:, 0:width], op=ALU.pow)
-            nc.gpsimd.tensor_tensor(out=shift[:], in0=negmean[:], in1=rstd[:], op=ALU.mult)
-            return negmean, rstd, shift
+            stats = {"negmean": negmean, "rstd": rstd}
+            if for_scalar:
+                shift = keep.tile([P, width], F32, name="shift" + label)
+                nc.gpsimd.tensor_tensor(out=shift[:], in0=negmean[:], in1=rstd[:], op=ALU.mult)
+                stats["shift"] = shift
+            return stats
 
-        def normalise(eng, q, m, d, st, col):
-            reg = gbuf[q][d][:, m, :]
-            nm = st[0][:, col:col + 1]
-            rs = st[1][:, col:col + 1]
-            if eng == 0:
-                nc.scalar.activation(out=reg, in_=reg, func=ACT.Identity, bias=st[2][:, col:col + 1], scale=rs)
-            elif eng == 1:
-                nc.vector.tensor_scalar(out=reg, in0=reg, scalar1=nm, scalar2=rs, op0=ALU.add, op1=ALU.mult)
+        def normalise(engine, q, m, j, stats, col):
+            patch = patches[q][j][:, m, :]
+            negmean = stats["negmean"][:, col:col + 1]
+            rstd = stats["rstd"][:, col:col + 1]
+            if engine == SCALAR:
+                nc.scalar.activation(out=patch, in_=patch, func=ACT.Identity, bias=stats["shift"][:, col:col + 1],
+                                     scale=rstd)
+            elif engine == VECTOR:
+                nc.vector.tensor_scalar(out=patch, in0=patch, scalar1=negmean, scalar2=rstd, op0=ALU.add, op1=ALU.mult)
             else:
-                nc.gpsimd.tensor_scalar(out=reg, in0=reg, scalar1=nm, scalar2=rs, op0=ALU.add, op1=ALU.mult)
+                nc.gpsimd.tensor_scalar(out=patch, in0=patch, scalar1=negmean, scalar2=rstd, op0=ALU.add, op1=ALU.mult)
 
         def turn(q, cb):
-            pt = psum.tile([P, BATCH], F32, name="ptn", tag="bank")
+            bank = psum.tile([P, BATCH], F32, name="ptn", tag="bank")
             k = cb % 4
             for m in range(MT):
-                nc.tensor.transpose(pt[:, P * m:P * (m + 1)], gbuf[q][cb // 4][:, m, P * k:P * (k + 1)], ident_f[:])
-            return pt
+                nc.tensor.transpose(bank[:, P * m:P * (m + 1)], patches[q][cb // 4][:, m, P * k:P * (k + 1)], ident_f[:])
+            return bank
 
-        def region(cb):
-            return turned[cb // 4][:, cb % 4, :]
+        def panel(cb):
+            return panel_tiles[cb // 4][:, cb % 4, :]
 
-        stats = [None, None]
-
-        def n_run(d, ks):
-            banks = [turn(0, 4 * d + k) for k in ks]
+        def turn_product0(j, ks):
+            banks = [turn(0, 4 * j + k) for k in ks]
             for i, k in enumerate(ks):
-                cb = 4 * d + k
-                nc.scalar.activation(out=region(cb), in_=banks[i][:], func=ACT.Identity,
-                                     bias=lbT[:, cb:cb + 1], scale=prmT[:, cb:cb + 1])
+                cb = 4 * j + k
+                nc.scalar.activation(out=panel(cb), in_=banks[i][:], func=ACT.Identity,
+                                     bias=shiftT[:, cb:cb + 1], scale=paramsT[:, cb:cb + 1])
 
-        bsm = keep.tile([P, 2, 32], BF16, name="bsm")
-        prm = keep.tile([P, P], BF16, name="prm")
-        bpart = keep.tile([P, 2], F32, name="bpart")
-        prmT = keep.tile([P, P], F32, name="prmT")
-        lbT = keep.tile([P, 32], F32, name="lbT")
-        wc = keep.tile([P, H], BF16, name="wc")
-        bc = keep.tile([P, H], BF16, name="bc")
-        tiles = 2 * CHUNKS * MT
-        stats_at = CHUNKS * MT + 2
+        bias_cols = keep.tile([P, 2, 32], BF16, name="bsm")
+        params = keep.tile([P, P], BF16, name="prm")
+        bias_part = keep.tile([P, 2], F32, name="bpart")
+        paramsT = keep.tile([P, P], F32, name="prmT")
+        shiftT = keep.tile([P, PANELS], F32, name="lbT")
+        cell_gain = keep.tile([P, H], BF16, name="wc")
+        cell_shift = keep.tile([P, H], BF16, name="bc")
+        stats0_step = CHUNKS * MT + 2
+        stats0 = []
+        early_pieces = 6 * MT
 
-        def norm_in_piece(i):
-            normalise(1 if 4 <= i < 24 else 2, 0, i % MT, i // MT, stats[0], i % MT)
+        def normalise_product0(i):
+            normalise(VECTOR if MT <= i < early_pieces else GPSIMD, 0, i % MT, i // MT, stats0[0], i % MT)
 
         nc.sync.dma_start(out=x_raw[:, 0, :], in_=x[0:P, :])
         load_raw(0)
         load_small(0)
         nc.sync.dma_start(out=z_first[0][:], in_=rows_view(zw[:, 0, :]))
         nc.sync.dma_start(out=z_first[1][:], in_=rows_view(zb[:, 0, :]))
-        nc.sync.dma_start(out=brow[0:CHUNKS, :], in_=b_ih.rearrange("(c n) -> c n", n=NT))
-        nc.sync.dma_start(out=brow[CHUNKS:2 * CHUNKS, :], in_=b_hh.rearrange("(c n) -> c n", n=NT))
+        nc.sync.dma_start(out=bias_rows[0:CHUNKS, :], in_=b_ih.rearrange("(c n) -> c n", n=NT))
+        nc.sync.dma_start(out=bias_rows[CHUNKS:2 * CHUNKS, :], in_=b_hh.rearrange("(c n) -> c n", n=NT))
         for b in range(1, 4):
             nc.sync.dma_start(out=x_raw[:, b, :], in_=x[P * b:P * (b + 1), :])
         load_raw(1)
@@ -316,38 +327,38 @@ def tile_adaptivelstmcell_pb_kernel(
         load_raw(2)
 
         x_words = x_raw.bitcast(F32)
-        x_stage = gbuf[1][0]
+        x_stage = patches[1][0]
 
-        def x_tile(m):
-            pt = psum.tile([P, PASSES, 2, P], F32, name="ptx", tag="bank")
+        def turn_x(m):
+            bank = psum.tile([P, PASSES, 2, P], F32, name="ptx", tag="bank")
             for g in range(PASSES):
                 for u in range(2):
-                    nc.tensor.transpose(pt[:, g, u, :], x_words[:, m, 256 * g + u:256 * (g + 1):2], ident_f[:])
+                    nc.tensor.transpose(bank[:, g, u, :], x_words[:, m, 256 * g + u:256 * (g + 1):2], ident_f[:])
             for g in range(PASSES):
-                copy_on(g, x_stage[:, 2 * g + m // 2, 256 * (m % 2):256 * (m % 2 + 1)].rearrange("p (c u) -> p c u", u=2),
-                        pt[:, g, :, :].rearrange("p u c -> p c u"))
+                copy_on((SCALAR, VECTOR)[g],
+                        x_stage[:, 2 * g + m // 2, 256 * (m % 2):256 * (m % 2 + 1)].rearrange("p (c u) -> p c u", u=2),
+                        bank[:, g, :, :].rearrange("p u c -> p c u"))
 
-        def x_quantise(m):
+        def quantise_x(m):
             for g in range(PASSES):
                 nc.vector.quantize_mx(
                     out=xcodes[0][:, g, P * m:P * (m + 1)].bitcast(FP8X4), scales=xscales[0][:, g, P * m:P * (m + 1)],
                     in_=x_stage[:].bitcast(BF16)[:, 2 * g + m // 2, NT * (m % 2):NT * (m % 2 + 1)])
 
-        def w_run_by_rows(c, halves):
+        def turn_weight_rows(c, duo):
             words = chunks[c]["raw"][:].bitcast(F32)
-            for half in halves:
-                banks = []
+            banks = []
+            for g in range(PASSES):
+                bank = psum.tile([P, 2, 256], F32, name="pt", tag="bank")
+                banks.append(bank)
+            for bb in range(2):
                 for g in range(PASSES):
-                    pt = psum.tile([P, 2, 256], F32, name="pt", tag="bank")
-                    banks.append(pt)
-                for bb in range(2):
-                    for g in range(PASSES):
-                        for u in range(2):
-                            nc.tensor.transpose(banks[g][:, u, P * bb:P * (bb + 1)],
-                                                words[:, 2 * half + bb, 256 * g + u:256 * (g + 1):2], ident_f[:])
-                for g in range(PASSES):
-                    gw = grouped[:, g, :].bitcast(F32).rearrange("p (c u) -> p c u", u=2)
-                    copy_on(g, gw[:, 256 * half:256 * (half + 1), :], banks[g][:].rearrange("p u c -> p c u"))
+                    for u in range(2):
+                        nc.tensor.transpose(banks[g][:, u, P * bb:P * (bb + 1)],
+                                            words[:, 2 * duo + bb, 256 * g + u:256 * (g + 1):2], ident_f[:])
+            for g in range(PASSES):
+                copy_on((SCALAR, VECTOR)[g], interleaved(g)[:, 256 * duo:256 * (duo + 1), :],
+                        banks[g][:].rearrange("p u c -> p c u"))
 
         warm_bank = psum.tile([P, P], F32, name="warmp", tag="bank")
 
@@ -356,249 +367,243 @@ def tile_adaptivelstmcell_pb_kernel(
                 nc.tensor.matmul(out=warm_bank[:], lhsT=ones_f[:], rhs=ones_f[:], start=True, stop=True)
 
         keep_warm(4)
-        x_tile(0)
-        x_quantise(0)
+        turn_x(0)
+        quantise_x(0)
         keep_warm(1)
-        w_run_by_rows(0, (0,))
+        turn_weight_rows(0, 0)
         keep_warm(1)
-        w_run_by_rows(0, (1,))
+        turn_weight_rows(0, 1)
         keep_warm(1)
-        chunks[0]["codes"] = wq.tile([P, PASSES, NT], U32, name="wcodes", tag="wcodes", align_bytes=64)
-        chunks[0]["scales"] = wq.tile([P, PASSES, NT], U8, name="wscales", tag="wscales", align_bytes=64)
+        new_codes(0)
         quantise_pass(chunks[0]["codes"], chunks[0]["scales"], 0)
         quantise_pass(chunks[0]["codes"], chunks[0]["scales"], 1)
-        ab_run(0)
+        turn_small(0)
         keep_warm(1)
-        z_run(0, (0, 0))
-        mm_alpha(0)
-        x_tile(1)
-        x_quantise(1)
+        turn_z(0)
+        alpha_of(0)
+        turn_x(1)
+        quantise_x(1)
         load_small(2)
         z_views = (rows_view(zw.rearrange("b s a -> b (s a)")), rows_view(zb.rearrange("b s a -> b (s a)")))
-        for raw, view in zip((zw_raw, zb_raw), z_views):
-            nc.sync.dma_start(out=raw[:, :, P:2 * P], in_=view[:, :, P:2 * P])
+
+        def load_z_slots(first, last):
+            for raw, view in zip((zw_raw, zb_raw), z_views):
+                nc.sync.dma_start(out=raw[:, :, P * first:P * last], in_=view[:, :, P * first:P * last])
+
+        load_z_slots(1, 2)
         load_bias(0)
         load_bias(2)
         load_raw(3)
 
-        for t in range(tiles + 1):
+        small_loads_step = 2 * MT
+        bias_sum_step = 15
+        for t in range(PATCHES + 1):
             c, m = divmod(t, MT)
-            d = c - CHUNKS
+            j1 = c - CHUNKS
             more = c + 1 < 2 * CHUNKS
-            live = t < tiles
+            live = t < PATCHES
             if live and m == 0 and c > 0:
                 if c + 2 < 2 * CHUNKS:
                     load_small(c + 2)
                     if c % 2 == 0:
                         load_bias(c + 2)
                 if c == 1:
-                    for raw, view in zip((zw_raw, zb_raw), z_views):
-                        nc.sync.dma_start(out=raw[:, :, 2 * P:4 * P], in_=view[:, :, 2 * P:4 * P])
+                    load_z_slots(2, 4)
                 if c + 3 < 2 * CHUNKS:
                     load_raw(c + 3)
             if t == 3 * MT:
-                for raw, view in zip((zw_raw, zb_raw), z_views):
-                    nc.sync.dma_start(out=raw[:, :, 4 * P:8 * P], in_=view[:, :, 4 * P:8 * P])
+                load_z_slots(4, 8)
             if t == 4 * MT:
                 nc.sync.dma_start(out=hx_raw, in_=rows_view(hx))
-            if t == 2 * MT:
-                nc.sync.dma_start(out=bsm[:, 0, :], in_=b_ih.rearrange("(p c) -> p c", c=32))
-                edge = PE_BIAS_CHUNKS * NT // 32
-                nc.sync.dma_start(out=bsm[0:edge, 1, :], in_=b_hh[GATES - 32 * edge:GATES].rearrange("(p c) -> p c", c=32))
-                nc.sync.dma_start(out=bsm[edge:P, 1, :], in_=b_hh[0:GATES - 32 * edge].rearrange("(p c) -> p c", c=32))
+            if t == small_loads_step:
+                edge = NT // 32
+                nc.sync.dma_start(out=bias_cols[:, 0, :], in_=b_ih.rearrange("(p c) -> p c", c=32))
+                nc.sync.dma_start(out=bias_cols[0:edge, 1, :],
+                                  in_=b_hh[GATES - 32 * edge:GATES].rearrange("(p c) -> p c", c=32))
+                nc.sync.dma_start(out=bias_cols[edge:P, 1, :],
+                                  in_=b_hh[0:GATES - 32 * edge].rearrange("(p c) -> p c", c=32))
                 for i, vec in enumerate((ln_i_w, ln_h_w, ln_i_b, ln_h_b)):
-                    nc.sync.dma_start(out=prm[32 * i:32 * (i + 1), :], in_=vec.rearrange("(c p) -> c p", p=P))
+                    nc.sync.dma_start(out=params[32 * i:32 * (i + 1), :], in_=vec.rearrange("(c p) -> c p", p=P))
             if live and c > 0 and m == 0 and more:
-                w_run(c + 1, 0)
-                w_run(c + 1, 1)
+                turn_weights(c + 1, 0)
+                turn_weights(c + 1, 1)
             if live and m == 2:
                 if more:
-                    ab_run(c + 1)
+                    turn_small(c + 1)
                 if 1 <= c <= 7:
-                    z_run(c)
-                if 2 <= d < CHUNKS - 1:
-                    n_run(d - 2, (0, 1))
-                    n_run(d - 2, (2, 3))
-            if t + 1 < tiles:
-                mm_alpha(t + 1)
+                    turn_z(c)
+                if 2 <= j1 < CHUNKS - 1:
+                    turn_product0(j1 - 2, (0, 1))
+                    turn_product0(j1 - 2, (2, 3))
+            if t + 1 < PATCHES:
+                alpha_of(t + 1)
             if live:
-                mm_rest(t)
+                product_of(t)
             if t >= 1:
-                mm_beta(t - 1)
-                add_beta_bias(t - 1)
+                beta_of(t - 1)
+                add_beta_and_bias(t - 1)
             if t < 2:
-                x_tile(t + 2)
-                x_quantise(t + 2)
+                turn_x(t + 2)
+                quantise_x(t + 2)
             if live and c == 0 and m < 2:
-                w_run_by_rows(c + 1, (m,))
+                turn_weight_rows(c + 1, m)
             if live and m == (2 if c == 0 else 1) and more:
-                w_quantise(c + 1)
-            if live and m == 3:
-                if c == 6:
-                    k_run(hx_raw.bitcast(F32), 0, (0, 1))
-                    k_run(hx_raw.bitcast(F32), 1, (0, 1))
-                    quantise(xcodes[1], xscales[1])
-            if t == 15:
-                nc.vector.tensor_reduce(out=bpart[:], in_=bsm[:], axis=AX.X, op=ALU.add)
-                nc.vector.memset(bpart[0:PE_BIAS_CHUNKS * NT // 32, :], 0.0)
-            if t == 17:
-                pb = psum.tile([P, 2], F32, name="pb", tag="bank")
-                nc.tensor.matmul(out=pb[:], lhsT=ones_f[:], rhs=bpart[:], start=True, stop=True)
-                pp = psum.tile([P, P], BF16, name="pp", tag="bank")
-                nc.tensor.transpose(pp[:], prm[:], ident_b[:])
-            if t == 18:
-                nc.vector.tensor_copy(out=bsum[:], in_=pb[:])
-                nc.vector.tensor_copy(out=prmT[:], in_=pp[:])
-                nc.vector.tensor_tensor(out=lbT[:], in0=prmT[:, 64:96], in1=prmT[:, 96:128], op=ALU.add)
+                quantise_weights(c + 1)
+            if t == 6 * MT + 3:
+                turn_pass(hx_raw.bitcast(F32), 0, (SCALAR, VECTOR))
+                turn_pass(hx_raw.bitcast(F32), 1, (SCALAR, VECTOR))
+                quantise(xcodes[1], xscales[1])
+            if t == bias_sum_step:
+                nc.vector.tensor_reduce(out=bias_part[:], in_=bias_cols[:], axis=AX.X, op=ALU.add)
+                nc.vector.memset(bias_part[0:NT // 32, :], 0.0)
+            if t == bias_sum_step + 2:
+                bias_bank = psum.tile([P, 2], F32, name="pb", tag="bank")
+                nc.tensor.matmul(out=bias_bank[:], lhsT=ones_f[:], rhs=bias_part[:], start=True, stop=True)
+                params_bank = psum.tile([P, P], BF16, name="pp", tag="bank")
+                nc.tensor.transpose(params_bank[:], params[:], ident_b[:])
+            if t == bias_sum_step + 3:
+                nc.vector.tensor_copy(out=bias_sum[:], in_=bias_bank[:])
+                nc.vector.tensor_copy(out=paramsT[:], in_=params_bank[:])
+                nc.vector.tensor_tensor(out=shiftT[:], in0=paramsT[:, 64:96], in1=paramsT[:, 96:128], op=ALU.add)
             if t >= 3:
                 square(t - 3)
-            if t == stats_at:
-                stats[0] = finish_stats(sum_u[:, 0, :, :], sum_sq[:, 0, :, :], bsum[:, 0:1], GATES, "i", MT, min(PE_BIAS))
-            if stats_at < t <= stats_at + 24:
-                norm_in_piece(t - stats_at - 1)
-            if tiles - 8 <= t < tiles:
-                norm_in_piece(24 + t - (tiles - 8))
-        cxt = rawp.tile([P, 4, K], BF16, name="raw", tag="raw")
-        nc.sync.dma_start(out=cxt[:], in_=rows_view(cx))
-        nc.sync.dma_start(out=wc[:], in_=ln_c_w.partition_broadcast(P))
-        nc.sync.dma_start(out=bc[:], in_=ln_c_b.partition_broadcast(P))
-        st_h = [finish_stats(sum_u[:, 1, 0:2, :], sum_sq[:, 1, 0:2, :], bsum[:, 1:2], GATES, "h0", 2)]
-        for t in range(tiles + 1, tiles + 3):
+            if t == stats0_step:
+                stats0.append(finish_stats(0, 0, MT, "i", False))
+            if stats0_step < t <= stats0_step + early_pieces:
+                normalise_product0(t - stats0_step - 1)
+            if PATCHES - 2 * MT <= t < PATCHES:
+                normalise_product0(early_pieces + t - (PATCHES - 2 * MT))
+        cx_raw = rawp.tile([P, 4, K], BF16, name="raw", tag="raw")
+        nc.sync.dma_start(out=cx_raw[:], in_=rows_view(cx))
+        nc.sync.dma_start(out=cell_gain[:], in_=ln_c_w.partition_broadcast(P))
+        nc.sync.dma_start(out=cell_shift[:], in_=ln_c_b.partition_broadcast(P))
+        stats1 = [finish_stats(1, 0, 2, "h0", True)]
+        for t in range(PATCHES + 1, PATCHES + 3):
             square(t - 3)
 
-        st_h.append(finish_stats(sum_u[:, 1, 2:4, :], sum_sq[:, 1, 2:4, :], bsum[:, 1:2], GATES, "h1", 2, min(PE_BIAS) - 2))
-        n_run(CHUNKS - 3, (0, 1))
-        n_run(CHUNKS - 3, (2, 3))
+        stats1.append(finish_stats(1, 2, 2, "h1", True))
+        turn_product0(CHUNKS - 3, (0, 1))
+        turn_product0(CHUNKS - 3, (2, 3))
 
-        def gates(cbs, funcs):
-            banks = []
-            for cb in cbs:
-                banks.append(turn(1, cb))
-            for i, cb in enumerate(cbs):
-                nc.vector.scalar_tensor_tensor(out=region(cb), in0=banks[i][:], scalar=prmT[:, 32 + cb:33 + cb],
-                                               in1=region(cb), op0=ALU.mult, op1=ALU.add)
-                if funcs:
-                    nc.scalar.activation(out=region(cb), in_=region(cb), func=funcs[i])
+        def normalise_product1(j, tiles_of_batch, engines):
+            for m in tiles_of_batch:
+                normalise(engines[m], 1, m, j, stats1[m // 2], m % 2)
 
-        def norm_piece(d, ms=(0, 1, 2, 3), engines=None):
-            for m in ms:
-                normalise((engines or (TAIL_NORM if d in (4, 0, 2) else TAIL_NORM_LATER))[m], 1, m, d, st_h[m // 2], m % 2)
+        def gate_panels(hb):
+            cbs = (16 + hb, hb, 8 + hb)
+            banks = [turn(1, cb) for cb in cbs]
+            for cb, bank, func in zip(cbs, banks, (ACT.Sigmoid, ACT.Sigmoid, ACT.Tanh)):
+                nc.vector.scalar_tensor_tensor(out=panel(cb), in0=bank[:], scalar=paramsT[:, 32 + cb:33 + cb],
+                                               in1=panel(cb), op0=ALU.mult, op1=ALU.add)
+                nc.scalar.activation(out=panel(cb), in_=panel(cb), func=func)
 
-        s_banks = {}
+        cx_banks = {}
 
-        def s_back_m(half, m, copy_eng):
-            sb = psum.tile([P, NT], F32, name="sb", tag="bank")
+        def turn_cx(hb):
+            bank = psum.tile([P, BATCH], BF16, name="cxT", tag="bank")
+            for m in range(MT):
+                nc.tensor.transpose(bank[:, P * m:P * (m + 1)], cx_raw[:, m, P * hb:P * (hb + 1)], ident_b[:])
+            cx_banks[hb] = bank
+
+        def cell_products(hb):
+            nc.vector.tensor_tensor(out=panel(16 + hb), in0=panel(16 + hb), in1=cx_banks[hb][:], op=ALU.mult)
+            nc.gpsimd.tensor_tensor(out=panel(hb), in0=panel(hb), in1=panel(8 + hb), op=ALU.mult)
+
+        held_banks = {}
+
+        def cell_sum_back(half, m):
+            bank = psum.tile([P, NT], F32, name="sb", tag="bank")
             for k in range(4):
                 for i, cb in enumerate((16 + 4 * half + k, 4 * half + k)):
-                    nc.tensor.matmul(out=sb[:, P * k:P * (k + 1)], lhsT=region(cb)[:, P * m:P * (m + 1)],
+                    nc.tensor.matmul(out=bank[:, P * k:P * (k + 1)], lhsT=panel(cb)[:, P * m:P * (m + 1)],
                                      rhs=ident_f[:], is_transpose=True, start=(i == 0), stop=(i == 1))
-            nc.vector.bn_stats(out=cbn[:, m, half, :], in_=sb[:])
+            nc.vector.bn_stats(out=cell_bn[:, m, half, :], in_=bank[:])
             if half == 0:
-                nc.scalar.copy(out=gbuf[1][half][:, m, :], in_=sb[:])
+                nc.scalar.copy(out=patches[1][half][:, m, :], in_=bank[:])
             else:
-                s_banks[m] = sb
+                held_banks[m] = bank
 
-        def stats_c(p):
-            pair = slice(2 * p, 2 * p + 2)
-            for m in (2 * p, 2 * p + 1):
-                nc.vector.bn_aggr(out=cmv[:, m, :], in_=cbn[:, m, :, :].rearrange("p a b -> p (a b)"))
-            nc.vector.tensor_scalar(out=cve[:, pair], in0=cmv[:, pair, 1], scalar1=1.0, scalar2=EPS, op0=ALU.mult,
+        def cell_stats(first):
+            cols = slice(first, first + 2)
+            for m in (first, first + 1):
+                nc.vector.bn_aggr(out=cell_mv[:, m, :], in_=cell_bn[:, m, :, :].rearrange("p a b -> p (a b)"))
+            nc.vector.tensor_scalar(out=cell_ve[:, cols], in0=cell_mv[:, cols, 1], scalar1=1.0, scalar2=EPS, op0=ALU.mult,
                                     op1=ALU.add)
-            nc.gpsimd.tensor_tensor(out=crs[:, pair], in0=cve[:, pair], in1=neg_half[:, 0:2], op=ALU.pow)
+            nc.gpsimd.tensor_tensor(out=cell_rstd[:, cols], in0=cell_ve[:, cols], in1=neg_half[:, 0:2], op=ALU.pow)
 
         def cy_centre(m, half):
             cols = slice(NT * half, NT * (half + 1))
-            nc.vector.scalar_tensor_tensor(out=gbuf[1][half][:, m, :],
-                                           in0=gbuf[1][half][:, m, :] if half == 0 else s_banks[m][:],
-                                           scalar=cmv[:, m, 0:1], in1=wc[:, cols], op0=ALU.subtract, op1=ALU.mult)
+            nc.vector.scalar_tensor_tensor(out=patches[1][half][:, m, :],
+                                           in0=patches[1][half][:, m, :] if half == 0 else held_banks[m][:],
+                                           scalar=cell_mv[:, m, 0:1], in1=cell_gain[:, cols], op0=ALU.subtract, op1=ALU.mult)
 
         def cy_finish(m):
             for half in range(2):
                 cols = slice(NT * half, NT * (half + 1))
-                cy_t = gbuf[1][2 + half][:, m, :]
-                nc.vector.scalar_tensor_tensor(out=cy_t, in0=gbuf[1][half][:, m, :], scalar=crs[:, m:m + 1],
-                                               in1=bc[:, cols], op0=ALU.mult, op1=ALU.add)
+                cy_t = patches[1][2 + half][:, m, :]
+                nc.vector.scalar_tensor_tensor(out=cy_t, in0=patches[1][half][:, m, :], scalar=cell_rstd[:, m:m + 1],
+                                               in1=cell_shift[:, cols], op0=ALU.mult, op1=ALU.add)
                 nc.sync.dma_start(out=out_1[P * m:P * (m + 1), cols], in_=cy_t)
-                nc.scalar.activation(out=gbuf[1][4 + half][:, m, :], in_=cy_t, func=ACT.Tanh)
+                nc.scalar.activation(out=patches[1][4 + half][:, m, :], in_=cy_t, func=ACT.Tanh)
 
-        o_h = (gbuf[0][CHUNKS - 1], gbuf[1][6])
-        o_sb = (gbuf[0][1], gbuf[0][2])
+        o_part1 = (patches[0][CHUNKS - 1], patches[1][6])
+        o_gate = (patches[0][1], patches[0][2])
 
-        def o_gate_h(group):
-            cbs = list(range(24 + 4 * group, 28 + 4 * group))
+        def o_panels_product1(half):
+            cbs = list(range(24 + 4 * half, 28 + 4 * half))
             banks = [turn(1, cb) for cb in cbs]
             for k, cb in enumerate(cbs):
-                nc.scalar.activation(out=o_h[group][:, k, :], in_=banks[k][:], func=ACT.Identity,
-                                     scale=prmT[:, 32 + cb:33 + cb])
+                nc.scalar.activation(out=o_part1[half][:, k, :], in_=banks[k][:], func=ACT.Identity,
+                                     scale=paramsT[:, 32 + cb:33 + cb])
 
         def o_back(m):
             for half in range(2):
-                ob = psum.tile([P, NT], F32, name="ob", tag="bank")
+                bank = psum.tile([P, NT], F32, name="ob", tag="bank")
                 for k in range(4):
-                    for i, part in enumerate((region(24 + 4 * half + k), o_h[half][:, k, :])):
-                        nc.tensor.matmul(out=ob[:, P * k:P * (k + 1)], lhsT=part[:, P * m:P * (m + 1)],
+                    for i, part in enumerate((panel(24 + 4 * half + k), o_part1[half][:, k, :])):
+                        nc.tensor.matmul(out=bank[:, P * k:P * (k + 1)], lhsT=part[:, P * m:P * (m + 1)],
                                          rhs=ident_f[:], is_transpose=True, start=(i == 0), stop=(i == 1))
-                nc.scalar.activation(out=o_sb[half][:, m, :], in_=ob[:], func=ACT.Sigmoid)
+                nc.scalar.activation(out=o_gate[half][:, m, :], in_=bank[:], func=ACT.Sigmoid)
 
-        def hy_part(m):
+        def hy_of(m):
             for half in range(2):
                 cols = slice(NT * half, NT * (half + 1))
-                hy_t = gbuf[1][half][:, m, :]
-                nc.vector.tensor_tensor(out=hy_t, in0=gbuf[1][4 + half][:, m, :], in1=o_sb[half][:, m, :], op=ALU.mult)
+                hy_t = patches[1][half][:, m, :]
+                nc.vector.tensor_tensor(out=hy_t, in0=patches[1][4 + half][:, m, :], in1=o_gate[half][:, m, :], op=ALU.mult)
                 nc.sync.dma_start(out=out_0[P * m:P * (m + 1), cols], in_=hy_t)
 
-        cx_banks = {}
-
-        def cell_gates(hb):
-            gates((16 + hb, hb, 8 + hb), (ACT.Sigmoid, ACT.Sigmoid, ACT.Tanh))
-
-        def cx_turn(hb):
-            cxT = psum.tile([P, BATCH], BF16, name="cxT", tag="bank")
-            for m in range(MT):
-                nc.tensor.transpose(cxT[:, P * m:P * (m + 1)], cxt[:, m, P * hb:P * (hb + 1)], ident_b[:])
-            cx_banks[hb] = cxT
-
-        def cell_sum(hb):
-            nc.vector.tensor_tensor(out=region(16 + hb), in0=region(16 + hb), in1=cx_banks[hb][:], op=ALU.mult)
-            nc.gpsimd.tensor_tensor(out=region(hb), in0=region(hb), in1=region(8 + hb), op=ALU.mult)
-
-        for d in (4, 0, 2):
-            norm_piece(d)
-        n_run(CHUNKS - 2, (0, 1))
-        n_run(CHUNKS - 2, (2, 3))
-        for d in (5, 1, 3):
-            norm_piece(d)
-        for hb in range(8):
-            cell_gates(hb)
+        for j in (4, 0, 2):
+            normalise_product1(j, range(MT), FIRST_NORM_ENGINES)
+        turn_product0(CHUNKS - 2, (0, 1))
+        turn_product0(CHUNKS - 2, (2, 3))
+        for j in (5, 1, 3):
+            normalise_product1(j, range(MT), LATER_NORM_ENGINES)
+        for hb in range(H // P):
+            gate_panels(hb)
             if hb >= 1:
-                cx_turn(hb - 1)
-                cell_sum(hb - 1)
+                turn_cx(hb - 1)
+                cell_products(hb - 1)
             if hb < 2:
-                norm_piece(6 + hb, (2, 3))
+                normalise_product1(6 + hb, (2, 3), LATER_NORM_ENGINES)
             if 2 <= hb < 6:
-                n_run(CHUNKS - 1, (hb - 2,))
-            if hb == 6:
-                s_back_m(0, 0, 1)
-                s_back_m(0, 1, 1)
-            if hb == 7:
-                s_back_m(0, 2, 1)
-                s_back_m(0, 3, 1)
-        cx_turn(7)
-        cell_sum(7)
-        s_back_m(1, 0, 1)
-        s_back_m(1, 1, 1)
-        s_back_m(1, 2, 1)
-        s_back_m(1, 3, 1)
-        norm_piece(6, (0, 1), (0, 0))
-        norm_piece(7, (0, 1), (0, 0))
-        o_gate_h(0)
-        o_gate_h(1)
-        stats_c(0)
+                turn_product0(CHUNKS - 1, (hb - 2,))
+            if hb >= 6:
+                cell_sum_back(0, 2 * (hb - 6))
+                cell_sum_back(0, 2 * (hb - 6) + 1)
+        turn_cx(H // P - 1)
+        cell_products(H // P - 1)
+        for m in range(MT):
+            cell_sum_back(1, m)
+        for j in (6, 7):
+            normalise_product1(j, (0, 1), (SCALAR, SCALAR))
+        o_panels_product1(0)
+        o_panels_product1(1)
+        cell_stats(0)
         o_back(0)
         cy_centre(0, 0)
         cy_centre(0, 1)
         cy_centre(1, 1)
-        stats_c(1)
+        cell_stats(2)
         cy_finish(0)
         o_back(1)
         cy_centre(1, 0)
@@ -609,9 +614,9 @@ def tile_adaptivelstmcell_pb_kernel(
         cy_centre(2, 0)
         cy_centre(3, 0)
         cy_finish(2)
-        hy_part(0)
+        hy_of(0)
         o_back(3)
         cy_finish(3)
-        hy_part(1)
-        hy_part(2)
-        hy_part(3)
+        hy_of(1)
+        hy_of(2)
+        hy_of(3)

from contextlib import ExitStack

import concourse.mybir as mybir
from concourse.masks import make_identity

F32 = mybir.dt.float32
BF16 = mybir.dt.bfloat16
U32 = mybir.dt.uint32
U8 = mybir.dt.uint8
FP8X4 = mybir.dt.float8_e5m2_x4
ALU = mybir.AluOpType
ACT = mybir.ActivationFunctionType
AX = mybir.AxisListType

P = 128
BATCH = 512
K = 1024
H = 1024
GATES = 4096
NT = 512
MT = BATCH // P
PASSES = K // 512
CHUNKS = GATES // NT
PATCHES = 2 * CHUNKS * MT
PANELS = GATES // P
EPS = 1e-5

SCALAR = 0
VECTOR = 1
GPSIMD = 2

WEIGHT_BANK_ENGINES = ((SCALAR, VECTOR), (VECTOR, SCALAR))
TENSOR_BIAS_TILE = 3
FIRST_NORM_ENGINES = (VECTOR, VECTOR, SCALAR, GPSIMD)
LATER_NORM_ENGINES = (VECTOR, VECTOR, GPSIMD, GPSIMD)

FLOPS = 2 * 2 * BATCH * GATES * K + 16 * 2 * BATCH * H * 128


def tile_adaptivelstmcell_pb_kernel(
    tc, x, hx, cx, zw, zb, w_ih, w_hh, b_ih, b_hh, norm_alpha_w, bias_beta_w,
    ln_i_w, ln_i_b, ln_h_w, ln_h_b, ln_c_w, ln_c_b, out_0, out_1,
):
    nc = tc.nc
    with ExitStack() as ctx:
        keep = ctx.enter_context(tc.tile_pool(name="keep", bufs=1))
        rawp = ctx.enter_context(tc.tile_pool(name="rawp", bufs=3))
        wq = ctx.enter_context(tc.tile_pool(name="wq", bufs=2))
        abp = ctx.enter_context(tc.tile_pool(name="abp", bufs=2))
        work = ctx.enter_context(tc.tile_pool(name="work", bufs=3))
        psum = ctx.enter_context(tc.psum_pool(name="psum", bufs=8))
        ctx.enter_context(tc.manual_schedule())

        ident_f = keep.tile([P, P], F32, name="ident_f")
        make_identity(nc, ident_f[:])
        ident_b = keep.tile([P, P], BF16, name="ident_b")
        make_identity(nc, ident_b[:])
        ones_f = keep.tile([P, P], F32, name="ones_f")
        nc.vector.memset(ones_f[:], 1.0)
        neg_half = keep.tile([P, MT], F32, name="neg_half")
        nc.vector.memset(neg_half[:], -0.5)
        bias_rows = keep.tile([P, NT], BF16, name="brow")
        nc.vector.memset(bias_rows[:], 0.0)
        warm = keep.tile([P, 1], F32, name="warm")
        nc.scalar.activation(out=warm[:], in_=neg_half[:, 0:1], func=ACT.Sigmoid)

        xcodes = [keep.tile([P, PASSES, BATCH], U32, name="xcodes%d" % q, align_bytes=64) for q in range(2)]
        xscales = [keep.tile([P, PASSES, BATCH], U8, name="xscales%d" % q, align_bytes=64) for q in range(2)]
        zT = [keep.tile([P, 8, BATCH], BF16, name="zT%d" % i) for i in range(2)]
        patches = [[keep.tile([P, MT, NT], F32, name="g%d_%d" % (q, j), align_bytes=64) for j in range(CHUNKS)]
                   for q in range(2)]
        spare = keep.tile([P, MT, NT], F32, name="spare")
        panel_tiles = [spare] + patches[0][0:CHUNKS - 1]
        grouped = keep.tile([P, PASSES, 4 * NT], BF16, name="grouped", align_bytes=64)
        sum_u = keep.tile([P, 2, MT, CHUNKS], F32, name="sum_u")
        sum_sq = keep.tile([P, 2, MT, CHUNKS], F32, name="sum_sq")
        cell_bn = keep.tile([P, MT, 2, 6], F32, name="cbn")
        cell_mv = keep.tile([P, MT, 2], F32, name="cmv")
        cell_ve = keep.tile([P, MT], F32, name="cve")
        cell_rstd = keep.tile([P, MT], F32, name="crs")
        bias_sum = keep.tile([P, 2], F32, name="bsum")

        def copy_on(engine, out, in_):
            if engine == SCALAR:
                nc.scalar.copy(out=out, in_=in_)
            else:
                nc.vector.tensor_copy(out=out, in_=in_)

        def interleaved(g):
            return grouped[:, g, :].bitcast(F32).rearrange("p (c u) -> p c u", u=2)

        def turn_pass(words, g, engines):
            banks = []
            for duo in range(2):
                bank = psum.tile([P, 2, 256], F32, name="pt", tag="bank")
                for bb in range(2):
                    for u in range(2):
                        nc.tensor.transpose(
                            bank[:, u, P * bb:P * (bb + 1)],
                            words[:, 2 * duo + bb, 256 * g + u:256 * (g + 1):2],
                            ident_f[:],
                        )
                banks.append(bank)
            for duo in range(2):
                copy_on(engines[duo], interleaved(g)[:, 256 * duo:256 * (duo + 1), :],
                        banks[duo][:].rearrange("p u c -> p c u"))

        def quantise(codes, scales):
            nc.vector.quantize_mx(out=codes[:].rearrange("p g c -> p (g c)").bitcast(FP8X4),
                                  scales=scales[:].rearrange("p g c -> p (g c)"),
                                  in_=grouped[:].rearrange("p g c -> p (g c)"))

        def quantise_pass(codes, scales, g):
            nc.vector.quantize_mx(out=codes[:, g, :].bitcast(FP8X4), scales=scales[:, g, :], in_=grouped[:, g, :])

        def rows_view(src2d):
            return src2d.rearrange("(b r) k -> r b k", r=P)

        x_raw, zw_raw, zb_raw, hx_raw = [patches[1][4 + i][:].bitcast(BF16) for i in range(4)]
        z_first = [keep.tile([P, MT, P], BF16, name="z_first%d" % i) for i in range(2)]
        chunks = {}
        alpha_copies = {}
        beta_banks = {}
        bias_tiles = {}

        def load_bias(c):
            q, j = divmod(c, CHUNKS)
            spread = abp.tile([P, 2, NT], BF16, name="bias", tag="bias", bufs=3)
            nc.sync.dma_start(out=spread[:].rearrange("p a n -> p (a n)"),
                              in_=(b_ih, b_hh)[q][NT * j:NT * (j + 2)].partition_broadcast(P))
            bias_tiles[c // 2] = spread

        def load_raw(c):
            q, j = divmod(c, CHUNKS)
            raw = rawp.tile([P, 4, K], BF16, name="raw", tag="raw")
            if c < 2:
                for b in range(4):
                    nc.sync.dma_start(out=raw[:, b, :], in_=w_ih[NT * c + P * b:NT * c + P * (b + 1), :])
            else:
                nc.sync.dma_start(out=raw[:], in_=rows_view((w_ih, w_hh)[q][NT * j:NT * (j + 1), :]))
            chunks[c] = {"raw": raw, "q": q}

        def load_small(c):
            q, j = divmod(c, CHUNKS)
            slot = 4 * q + j // 2
            h0 = NT * (j % 2)
            small = []
            for i, wsrc in enumerate((norm_alpha_w, bias_beta_w)):
                sraw = abp.tile([P, 4, P], BF16, name="sraw%d" % i, tag="sraw%d" % i)
                nc.sync.dma_start(out=sraw[:], in_=wsrc[slot, h0:h0 + NT, :].rearrange("(b r) a -> r b a", r=P))
                small.append(sraw)
            chunks[c]["small"] = small

        def turn_weights(c, g):
            ch = chunks[c]
            turn_pass(ch["raw"][:].bitcast(F32), g, WEIGHT_BANK_ENGINES[ch["q"]])

        def new_codes(c):
            chunks[c]["codes"] = wq.tile([P, PASSES, NT], U32, name="wcodes", tag="wcodes", align_bytes=64)
            chunks[c]["scales"] = wq.tile([P, PASSES, NT], U8, name="wscales", tag="wscales", align_bytes=64)

        def quantise_weights(c):
            new_codes(c)
            quantise(chunks[c]["codes"], chunks[c]["scales"])

        def turn_small(c):
            ch = chunks[c]
            banks = []
            for i in range(2):
                bank = psum.tile([P, NT], BF16, name="pta", tag="bank")
                for b in range(4):
                    nc.tensor.transpose(bank[:, P * b:P * (b + 1)], ch["small"][i][:, b, :], ident_b[:])
                banks.append(bank)
            ch["smallT"] = []
            for i in range(2):
                wT = abp.tile([P, NT], BF16, name="wT%d" % i, tag="wT%d" % i)
                nc.scalar.copy(out=wT[:], in_=banks[i][:])
                ch["smallT"].append(wT)

        def turn_z(slot):
            banks = []
            for raw, first in ((zw_raw, z_first[0]), (zb_raw, z_first[1])):
                bank = psum.tile([P, BATCH], BF16, name="ptz", tag="bank")
                for m in range(MT):
                    src = first[:, m, :] if slot == 0 else raw[:, m, P * slot:P * (slot + 1)]
                    nc.tensor.transpose(bank[:, P * m:P * (m + 1)], src, ident_b[:])
                banks.append(bank)
            for i in range(2):
                nc.scalar.copy(out=zT[i][:, slot, :], in_=banks[i][:])

        def where(t):
            c, m = divmod(t, MT)
            q, j = divmod(c, CHUNKS)
            return c, m, q, j, 4 * q + j // 2, slice(P * m, P * (m + 1))

        def bias_on_tensor(c, m):
            return m == TENSOR_BIAS_TILE or c == 0 or c == 2 * CHUNKS - 1

        def alpha_of(t):
            c, m, q, j, slot, rows = where(t)
            alpha = psum.tile([P, NT], F32, name="alpha", tag="bank")
            nc.tensor.matmul(out=alpha[:], lhsT=zT[0][:, slot, rows], rhs=chunks[c]["smallT"][0][:], start=True, stop=True)
            al = work.tile([P, NT], F32, name="al", tag="al")
            nc.scalar.copy(out=al[:], in_=alpha[:])
            alpha_copies[t] = al

        def product_of(t):
            c, m, q, j, slot, rows = where(t)
            ch = chunks[c]
            acc = psum.tile([P, NT], F32, name="xh", tag="bank")
            for g in range(PASSES):
                nc.tensor.matmul_mx(
                    out=acc[:],
                    lhsT=xcodes[q][:, g, rows].bitcast(FP8X4),
                    lhsT_scale=xscales[q][:, g, rows],
                    rhs=ch["codes"][:, g, :].bitcast(FP8X4),
                    rhs_scale=ch["scales"][:, g, :],
                    start=(g == 0),
                    stop=(g == PASSES - 1),
                )
            nc.vector.tensor_tensor(out=patches[q][j][:, m, :], in0=acc[:], in1=alpha_copies[t][:], op=ALU.mult)

        def beta_of(t):
            c, m, q, j, slot, rows = where(t)
            beta = psum.tile([P, NT], F32, name="beta", tag="bank")
            with_bias = bias_on_tensor(c, m)
            nc.tensor.matmul(out=beta[:], lhsT=zT[1][:, slot, rows], rhs=chunks[c]["smallT"][1][:], start=True,
                             stop=not with_bias)
            if with_bias:
                nc.tensor.matmul(out=beta[:], lhsT=ident_b[:, c:c + 1].to_broadcast([P, P]), rhs=bias_rows[:],
                                 start=False, stop=True)
            beta_banks[t] = beta

        def add_beta_and_bias(t):
            c, m, q, j, slot, rows = where(t)
            patch = patches[q][j][:, m, :]
            nc.vector.scalar_tensor_tensor(out=patch, in0=patch, scalar=1.0, in1=beta_banks[t][:], op0=ALU.mult,
                                           op1=ALU.add, accum_out=sum_u[:, q, m, j:j + 1])
            if not bias_on_tensor(c, m):
                nc.gpsimd.tensor_tensor(out=patch, in0=patch, in1=bias_tiles[c // 2][:, c % 2, :], op=ALU.add)

        def square(t):
            c, m, q, j, slot, rows = where(t)
            unread = work.tile([P, NT], BF16, name="junk", tag="junk")
            nc.scalar.activation(out=unread[:], in_=patches[q][j][:, m, :], func=ACT.Square,
                                 accum_out=sum_sq[:, q, m, j:j + 1])

        def finish_stats(q, first, width, label, for_scalar):
            s1 = keep.tile([P, width], F32, name="s1" + label)
            s2 = keep.tile([P, width], F32, name="s2" + label)
            negmean = keep.tile([P, width], F32, name="negmean" + label)
            rstd = keep.tile([P, width], F32, name="rstd" + label)
            nc.vector.tensor_reduce(out=s1[:], in_=sum_u[:, q, first:first + width, :], axis=AX.X, op=ALU.add)
            lacking = min(TENSOR_BIAS_TILE - first, width)
            nc.vector.tensor_scalar(out=negmean[:, 0:lacking], in0=s1[:, 0:lacking], scalar1=bias_sum[:, q:q + 1],
                                    scalar2=-1.0 / GATES, op0=ALU.add, op1=ALU.mult)
            if lacking < width:
                nc.vector.tensor_scalar(out=negmean[:, lacking:width], in0=s1[:, lacking:width], scalar1=0.0,
                                        scalar2=-1.0 / GATES, op0=ALU.add, op1=ALU.mult)
            nc.vector.tensor_tensor(out=s1[:], in0=negmean[:], in1=negmean[:], op=ALU.mult)
            nc.vector.tensor_reduce(out=s2[:], in_=sum_sq[:, q, first:first + width, :], axis=AX.X, op=ALU.add)
            nc.vector.scalar_tensor_tensor(out=s2[:], in0=s2[:], scalar=1.0 / GATES, in1=s1[:],
                                           op0=ALU.mult, op1=ALU.subtract)
            nc.vector.tensor_scalar(out=s2[:], in0=s2[:], scalar1=0.0, scalar2=EPS, op0=ALU.max, op1=ALU.add)
            nc.gpsimd.tensor_tensor(out=rstd[:], in0=s2[:], in1=neg_half[:, 0:width], op=ALU.pow)
            stats = {"negmean": negmean, "rstd": rstd}
            if for_scalar:
                shift = keep.tile([P, width], F32, name="shift" + label)
                nc.gpsimd.tensor_tensor(out=shift[:], in0=negmean[:], in1=rstd[:], op=ALU.mult)
                stats["shift"] = shift
            return stats

        def normalise(engine, q, m, j, stats, col):
            patch = patches[q][j][:, m, :]
            negmean = stats["negmean"][:, col:col + 1]
            rstd = stats["rstd"][:, col:col + 1]
            if engine == SCALAR:
                nc.scalar.activation(out=patch, in_=patch, func=ACT.Identity, bias=stats["shift"][:, col:col + 1],
                                     scale=rstd)
            elif engine == VECTOR:
                nc.vector.tensor_scalar(out=patch, in0=patch, scalar1=negmean, scalar2=rstd, op0=ALU.add, op1=ALU.mult)
            else:
                nc.gpsimd.tensor_scalar(out=patch, in0=patch, scalar1=negmean, scalar2=rstd, op0=ALU.add, op1=ALU.mult)

        def turn(q, cb):
            bank = psum.tile([P, BATCH], F32, name="ptn", tag="bank")
            k = cb % 4
            for m in range(MT):
                nc.tensor.transpose(bank[:, P * m:P * (m + 1)], patches[q][cb // 4][:, m, P * k:P * (k + 1)], ident_f[:])
            return bank

        def panel(cb):
            return panel_tiles[cb // 4][:, cb % 4, :]

        def turn_product0(j, ks):
            banks = [turn(0, 4 * j + k) for k in ks]
            for i, k in enumerate(ks):
                cb = 4 * j + k
                nc.scalar.activation(out=panel(cb), in_=banks[i][:], func=ACT.Identity,
                                     bias=shiftT[:, cb:cb + 1], scale=paramsT[:, cb:cb + 1])

        bias_cols = keep.tile([P, 2, 32], BF16, name="bsm")
        params = keep.tile([P, P], BF16, name="prm")
        bias_part = keep.tile([P, 2], F32, name="bpart")
        paramsT = keep.tile([P, P], F32, name="prmT")
        shiftT = keep.tile([P, PANELS], F32, name="lbT")
        cell_gain = keep.tile([P, H], BF16, name="wc")
        cell_shift = keep.tile([P, H], BF16, name="bc")
        stats0_step = CHUNKS * MT + 2
        stats0 = []
        early_pieces = 6 * MT

        def normalise_product0(i):
            normalise(VECTOR if MT <= i < early_pieces else GPSIMD, 0, i % MT, i // MT, stats0[0], i % MT)

        nc.sync.dma_start(out=x_raw[:, 0, :], in_=x[0:P, :])
        load_raw(0)
        load_small(0)
        nc.sync.dma_start(out=z_first[0][:], in_=rows_view(zw[:, 0, :]))
        nc.sync.dma_start(out=z_first[1][:], in_=rows_view(zb[:, 0, :]))
        nc.sync.dma_start(out=bias_rows[0:CHUNKS, :], in_=b_ih.rearrange("(c n) -> c n", n=NT))
        nc.sync.dma_start(out=bias_rows[CHUNKS:2 * CHUNKS, :], in_=b_hh.rearrange("(c n) -> c n", n=NT))
        for b in range(1, 4):
            nc.sync.dma_start(out=x_raw[:, b, :], in_=x[P * b:P * (b + 1), :])
        load_raw(1)
        load_small(1)
        load_raw(2)

        x_words = x_raw.bitcast(F32)
        x_stage = patches[1][0]

        def turn_x(m):
            bank = psum.tile([P, PASSES, 2, P], F32, name="ptx", tag="bank")
            for g in range(PASSES):
                for u in range(2):
                    nc.tensor.transpose(bank[:, g, u, :], x_words[:, m, 256 * g + u:256 * (g + 1):2], ident_f[:])
            for g in range(PASSES):
                copy_on((SCALAR, VECTOR)[g],
                        x_stage[:, 2 * g + m // 2, 256 * (m % 2):256 * (m % 2 + 1)].rearrange("p (c u) -> p c u", u=2),
                        bank[:, g, :, :].rearrange("p u c -> p c u"))

        def quantise_x(m):
            for g in range(PASSES):
                nc.vector.quantize_mx(
                    out=xcodes[0][:, g, P * m:P * (m + 1)].bitcast(FP8X4), scales=xscales[0][:, g, P * m:P * (m + 1)],
                    in_=x_stage[:].bitcast(BF16)[:, 2 * g + m // 2, NT * (m % 2):NT * (m % 2 + 1)])

        def turn_weight_rows(c, duo):
            words = chunks[c]["raw"][:].bitcast(F32)
            banks = []
            for g in range(PASSES):
                bank = psum.tile([P, 2, 256], F32, name="pt", tag="bank")
                banks.append(bank)
            for bb in range(2):
                for g in range(PASSES):
                    for u in range(2):
                        nc.tensor.transpose(banks[g][:, u, P * bb:P * (bb + 1)],
                                            words[:, 2 * duo + bb, 256 * g + u:256 * (g + 1):2], ident_f[:])
            for g in range(PASSES):
                copy_on((SCALAR, VECTOR)[g], interleaved(g)[:, 256 * duo:256 * (duo + 1), :],
                        banks[g][:].rearrange("p u c -> p c u"))

        warm_bank = psum.tile([P, P], F32, name="warmp", tag="bank")

        def keep_warm(n):
            for i in range(n):
                nc.tensor.matmul(out=warm_bank[:], lhsT=ones_f[:], rhs=ones_f[:], start=True, stop=True)

        keep_warm(4)
        turn_x(0)
        quantise_x(0)
        keep_warm(1)
        turn_weight_rows(0, 0)
        keep_warm(1)
        turn_weight_rows(0, 1)
        keep_warm(1)
        new_codes(0)
        quantise_pass(chunks[0]["codes"], chunks[0]["scales"], 0)
        quantise_pass(chunks[0]["codes"], chunks[0]["scales"], 1)
        turn_small(0)
        keep_warm(1)
        turn_z(0)
        alpha_of(0)
        turn_x(1)
        quantise_x(1)
        load_small(2)
        z_views = (rows_view(zw.rearrange("b s a -> b (s a)")), rows_view(zb.rearrange("b s a -> b (s a)")))

        def load_z_slots(first, last):
            for raw, view in zip((zw_raw, zb_raw), z_views):
                nc.sync.dma_start(out=raw[:, :, P * first:P * last], in_=view[:, :, P * first:P * last])

        load_z_slots(1, 2)
        load_bias(0)
        load_bias(2)
        load_raw(3)

        small_loads_step = 2 * MT
        bias_sum_step = 15
        for t in range(PATCHES + 1):
            c, m = divmod(t, MT)
            j1 = c - CHUNKS
            more = c + 1 < 2 * CHUNKS
            live = t < PATCHES
            if live and m == 0 and c > 0:
                if c + 2 < 2 * CHUNKS:
                    load_small(c + 2)
                    if c % 2 == 0:
                        load_bias(c + 2)
                if c == 1:
                    load_z_slots(2, 4)
                if c + 3 < 2 * CHUNKS:
                    load_raw(c + 3)
            if t == 3 * MT:
                load_z_slots(4, 8)
            if t == 4 * MT:
                nc.sync.dma_start(out=hx_raw, in_=rows_view(hx))
            if t == small_loads_step:
                edge = NT // 32
                nc.sync.dma_start(out=bias_cols[:, 0, :], in_=b_ih.rearrange("(p c) -> p c", c=32))
                nc.sync.dma_start(out=bias_cols[0:edge, 1, :],
                                  in_=b_hh[GATES - 32 * edge:GATES].rearrange("(p c) -> p c", c=32))
                nc.sync.dma_start(out=bias_cols[edge:P, 1, :],
                                  in_=b_hh[0:GATES - 32 * edge].rearrange("(p c) -> p c", c=32))
                for i, vec in enumerate((ln_i_w, ln_h_w, ln_i_b, ln_h_b)):
                    nc.sync.dma_start(out=params[32 * i:32 * (i + 1), :], in_=vec.rearrange("(c p) -> c p", p=P))
            if live and c > 0 and m == 0 and more:
                turn_weights(c + 1, 0)
                turn_weights(c + 1, 1)
            if live and m == 2:
                if more:
                    turn_small(c + 1)
                if 1 <= c <= 7:
                    turn_z(c)
                if 2 <= j1 < CHUNKS - 1:
                    turn_product0(j1 - 2, (0, 1))
                    turn_product0(j1 - 2, (2, 3))
            if t + 1 < PATCHES:
                alpha_of(t + 1)
            if live:
                product_of(t)
            if t >= 1:
                beta_of(t - 1)
                add_beta_and_bias(t - 1)
            if t < 2:
                turn_x(t + 2)
                quantise_x(t + 2)
            if live and c == 0 and m < 2:
                turn_weight_rows(c + 1, m)
            if live and m == (2 if c == 0 else 1) and more:
                quantise_weights(c + 1)
            if t == 6 * MT + 3:
                turn_pass(hx_raw.bitcast(F32), 0, (SCALAR, VECTOR))
                turn_pass(hx_raw.bitcast(F32), 1, (SCALAR, VECTOR))
                quantise(xcodes[1], xscales[1])
            if t == bias_sum_step:
                nc.vector.tensor_reduce(out=bias_part[:], in_=bias_cols[:], axis=AX.X, op=ALU.add)
                nc.vector.memset(bias_part[0:NT // 32, :], 0.0)
            if t == bias_sum_step + 2:
                bias_bank = psum.tile([P, 2], F32, name="pb", tag="bank")
                nc.tensor.matmul(out=bias_bank[:], lhsT=ones_f[:], rhs=bias_part[:], start=True, stop=True)
                params_bank = psum.tile([P, P], BF16, name="pp", tag="bank")
                nc.tensor.transpose(params_bank[:], params[:], ident_b[:])
            if t == bias_sum_step + 3:
                nc.vector.tensor_copy(out=bias_sum[:], in_=bias_bank[:])
                nc.vector.tensor_copy(out=paramsT[:], in_=params_bank[:])
                nc.vector.tensor_tensor(out=shiftT[:], in0=paramsT[:, 64:96], in1=paramsT[:, 96:128], op=ALU.add)
            if t >= 3:
                square(t - 3)
            if t == stats0_step:
                stats0.append(finish_stats(0, 0, MT, "i", False))
            if stats0_step < t <= stats0_step + early_pieces:
                normalise_product0(t - stats0_step - 1)
            if PATCHES - 2 * MT <= t < PATCHES:
                normalise_product0(early_pieces + t - (PATCHES - 2 * MT))
        cx_raw = rawp.tile([P, 4, K], BF16, name="raw", tag="raw")
        nc.sync.dma_start(out=cx_raw[:], in_=rows_view(cx))
        nc.sync.dma_start(out=cell_gain[:], in_=ln_c_w.partition_broadcast(P))
        nc.sync.dma_start(out=cell_shift[:], in_=ln_c_b.partition_broadcast(P))
        stats1 = [finish_stats(1, 0, 2, "h0", True)]
        for t in range(PATCHES + 1, PATCHES + 3):
            square(t - 3)

        stats1.append(finish_stats(1, 2, 2, "h1", True))
        turn_product0(CHUNKS - 3, (0, 1))
        turn_product0(CHUNKS - 3, (2, 3))

        def normalise_product1(j, tiles_of_batch, engines):
            for m in tiles_of_batch:
                normalise(engines[m], 1, m, j, stats1[m // 2], m % 2)

        def gate_panels(hb):
            cbs = (16 + hb, hb, 8 + hb)
            banks = [turn(1, cb) for cb in cbs]
            for cb, bank, func in zip(cbs, banks, (ACT.Sigmoid, ACT.Sigmoid, ACT.Tanh)):
                nc.vector.scalar_tensor_tensor(out=panel(cb), in0=bank[:], scalar=paramsT[:, 32 + cb:33 + cb],
                                               in1=panel(cb), op0=ALU.mult, op1=ALU.add)
                nc.scalar.activation(out=panel(cb), in_=panel(cb), func=func)

        cx_banks = {}

        def turn_cx(hb):
            bank = psum.tile([P, BATCH], BF16, name="cxT", tag="bank")
            for m in range(MT):
                nc.tensor.transpose(bank[:, P * m:P * (m + 1)], cx_raw[:, m, P * hb:P * (hb + 1)], ident_b[:])
            cx_banks[hb] = bank

        def cell_products(hb):
            nc.vector.tensor_tensor(out=panel(16 + hb), in0=panel(16 + hb), in1=cx_banks[hb][:], op=ALU.mult)
            nc.gpsimd.tensor_tensor(out=panel(hb), in0=panel(hb), in1=panel(8 + hb), op=ALU.mult)

        held_banks = {}

        def cell_sum_back(half, m):
            bank = psum.tile([P, NT], F32, name="sb", tag="bank")
            for k in range(4):
                for i, cb in enumerate((16 + 4 * half + k, 4 * half + k)):
                    nc.tensor.matmul(out=bank[:, P * k:P * (k + 1)], lhsT=panel(cb)[:, P * m:P * (m + 1)],
                                     rhs=ident_f[:], is_transpose=True, start=(i == 0), stop=(i == 1))
            nc.vector.bn_stats(out=cell_bn[:, m, half, :], in_=bank[:])
            if half == 0:
                nc.scalar.copy(out=patches[1][half][:, m, :], in_=bank[:])
            else:
                held_banks[m] = bank

        def cell_stats(first):
            cols = slice(first, first + 2)
            for m in (first, first + 1):
                nc.vector.bn_aggr(out=cell_mv[:, m, :], in_=cell_bn[:, m, :, :].rearrange("p a b -> p (a b)"))
            nc.vector.tensor_scalar(out=cell_ve[:, cols], in0=cell_mv[:, cols, 1], scalar1=1.0, scalar2=EPS, op0=ALU.mult,
                                    op1=ALU.add)
            nc.gpsimd.tensor_tensor(out=cell_rstd[:, cols], in0=cell_ve[:, cols], in1=neg_half[:, 0:2], op=ALU.pow)

        def cy_centre(m, half):
            cols = slice(NT * half, NT * (half + 1))
            nc.vector.scalar_tensor_tensor(out=patches[1][half][:, m, :],
                                           in0=patches[1][half][:, m, :] if half == 0 else held_banks[m][:],
                                           scalar=cell_mv[:, m, 0:1], in1=cell_gain[:, cols], op0=ALU.subtract, op1=ALU.mult)

        def cy_finish(m):
            for half in range(2):
                cols = slice(NT * half, NT * (half + 1))
                cy_t = patches[1][2 + half][:, m, :]
                nc.vector.scalar_tensor_tensor(out=cy_t, in0=patches[1][half][:, m, :], scalar=cell_rstd[:, m:m + 1],
                                               in1=cell_shift[:, cols], op0=ALU.mult, op1=ALU.add)
                nc.sync.dma_start(out=out_1[P * m:P * (m + 1), cols], in_=cy_t)
                nc.scalar.activation(out=patches[1][4 + half][:, m, :], in_=cy_t, func=ACT.Tanh)

        o_part1 = (patches[0][CHUNKS - 1], patches[1][6])
        o_gate = (patches[0][1], patches[0][2])

        def o_panels_product1(half):
            cbs = list(range(24 + 4 * half, 28 + 4 * half))
            banks = [turn(1, cb) for cb in cbs]
            for k, cb in enumerate(cbs):
                nc.scalar.activation(out=o_part1[half][:, k, :], in_=banks[k][:], func=ACT.Identity,
                                     scale=paramsT[:, 32 + cb:33 + cb])

        def o_back(m):
            for half in range(2):
                bank = psum.tile([P, NT], F32, name="ob", tag="bank")
                for k in range(4):
                    for i, part in enumerate((panel(24 + 4 * half + k), o_part1[half][:, k, :])):
                        nc.tensor.matmul(out=bank[:, P * k:P * (k + 1)], lhsT=part[:, P * m:P * (m + 1)],
                                         rhs=ident_f[:], is_transpose=True, start=(i == 0), stop=(i == 1))
                nc.scalar.activation(out=o_gate[half][:, m, :], in_=bank[:], func=ACT.Sigmoid)

        def hy_of(m):
            for half in range(2):
                cols = slice(NT * half, NT * (half + 1))
                hy_t = patches[1][half][:, m, :]
                nc.vector.tensor_tensor(out=hy_t, in0=patches[1][4 + half][:, m, :], in1=o_gate[half][:, m, :], op=ALU.mult)
                nc.sync.dma_start(out=out_0[P * m:P * (m + 1), cols], in_=hy_t)

        for j in (4, 0, 2):
            normalise_product1(j, range(MT), FIRST_NORM_ENGINES)
        turn_product0(CHUNKS - 2, (0, 1))
        turn_product0(CHUNKS - 2, (2, 3))
        for j in (5, 1, 3):
            normalise_product1(j, range(MT), LATER_NORM_ENGINES)
        for hb in range(H // P):
            gate_panels(hb)
            if hb >= 1:
                turn_cx(hb - 1)
                cell_products(hb - 1)
            if hb < 2:
                normalise_product1(6 + hb, (2, 3), LATER_NORM_ENGINES)
            if 2 <= hb < 6:
                turn_product0(CHUNKS - 1, (hb - 2,))
            if hb >= 6:
                cell_sum_back(0, 2 * (hb - 6))
                cell_sum_back(0, 2 * (hb - 6) + 1)
        turn_cx(H // P - 1)
        cell_products(H // P - 1)
        for m in range(MT):
            cell_sum_back(1, m)
        for j in (6, 7):
            normalise_product1(j, (0, 1), (SCALAR, SCALAR))
        o_panels_product1(0)
        o_panels_product1(1)
        cell_stats(0)
        o_back(0)
        cy_centre(0, 0)
        cy_centre(0, 1)
        cy_centre(1, 1)
        cell_stats(2)
        cy_finish(0)
        o_back(1)
        cy_centre(1, 0)
        cy_centre(2, 1)
        cy_centre(3, 1)
        cy_finish(1)
        o_back(2)
        cy_centre(2, 0)
        cy_centre(3, 0)
        cy_finish(2)
        hy_of(0)
        o_back(3)
        cy_finish(3)
        hy_of(1)
        hy_of(2)
        hy_of(3)
